import numpy as np
import ml_dtypes


def mxq(x, axis, fmt="e4m3"):
    dtype, down = {"e4m3": (ml_dtypes.float8_e4m3fn, 7), "e5m2": (ml_dtypes.float8_e5m2, 14)}[fmt]
    v = np.moveaxis(np.asarray(x, np.float32).astype(ml_dtypes.bfloat16).astype(np.float64), axis, -1)
    blocks = v.reshape(v.shape[:-1] + (-1, 32))
    amax = np.abs(blocks).max(-1, keepdims=True)
    byte = np.maximum(np.where(amax > 0, np.frexp(amax)[1] - 1 + 127, 0) - down, 1)
    scale = np.exp2(byte - 127.0)
    codes = (blocks / scale).astype(np.float32).astype(dtype).astype(np.float64)
    return np.moveaxis((codes * scale).reshape(v.shape), -1, axis)


WIDE = False


def mx_kscale(k):
    if not WIDE:
        return np.ones(k)
    levels = np.array([10, -10, 5, -5, 0])
    if k % 512:
        return np.exp2(np.random.permutation(np.resize(levels, k // 32))).repeat(32)
    a = np.empty((k // 512, 16))
    for p in range(k // 512):
        a[p, :8] = np.random.permutation(np.resize(levels, 8))
        for g in range(8):
            far = levels[np.abs(levels - a[p, g]) >= 10]
            a[p, g + 8] = far[np.random.randint(len(far))]
    return np.exp2(a.ravel()).repeat(32)


BF16 = ml_dtypes.bfloat16


def bf(x):
    return np.asarray(x, np.float32).astype(BF16)


def f64(x):
    return np.asarray(x).astype(np.float64)


E2M1 = np.array([0.0, 0.5, 1.0, 1.5, 2.0, 3.0, 4.0, 6.0, -0.0, -0.5, -1.0, -1.5, -2.0, -3.0, -4.0, -6.0])


def pack_weight(w, fmt):
    k, n = w.shape
    w = f64(bf(w)).reshape(k // 32, 32, n)
    amax = np.abs(w).max(1)
    if fmt == "e4m3":
        byte = np.frexp(amax)[1] - 1 + 127 - 7
    else:
        mant, ex = np.frexp(amax / 6.0)
        byte = np.where(mant > 0.5, ex, ex - 1) + 127
    byte = np.clip(np.where(amax > 0, byte, 1), 1, 254)
    scaled = (w * np.exp2(127.0 - byte)[:, None, :]).reshape(k, n).astype(np.float32)
    by_word = np.ascontiguousarray(scaled.reshape(k // 512, 128, 4, n).transpose(0, 1, 3, 2))
    if fmt == "e4m3":
        words = by_word.astype(ml_dtypes.float8_e4m3fn).view(np.uint8)
    else:
        c = by_word.astype(ml_dtypes.float4_e2m1fn).view(np.uint8) & 0xF
        words = c[..., 0::2] | (c[..., 1::2] << 4)
    return np.ascontiguousarray(words), np.ascontiguousarray(byte.astype(np.uint8).reshape(k // 512, 16, n))


def unpack_weight(words, scales, fmt):
    g, p, n, _ = words.shape
    if fmt == "e4m3":
        vals = np.ascontiguousarray(words).view(ml_dtypes.float8_e4m3fn).astype(np.float64)
    else:
        nib = np.empty((g, p, n, 4), np.uint8)
        nib[..., 0::2] = words & 0xF
        nib[..., 1::2] = words >> 4
        vals = E2M1[nib]
    vals = vals * np.repeat(np.exp2(scales.astype(np.float64) - 127.0), 8, axis=1)[..., None]
    return vals.transpose(0, 1, 3, 2).reshape(g * 512, n)


B, N_EP, S, D, IN_DIM, L, K = 6, 3, 512, 256, 255, 512, 10


def draw0():
    s, t = mx_kscale(S), mx_kscale(L)
    r = np.random.standard_normal
    g = r((B, S, S)) * 1.56
    a = np.exp(g - g.max(-1, keepdims=True))
    a = a / a.sum(-1, keepdims=True)
    v1 = bf(r((B, S, L)) * 4.0 / s[:, None] * t)
    Wq2_words, Wq2_scales = pack_weight(r((L, L)) * 4.0 / np.sqrt(L) / t[:, None], "e4m3")
    bq2 = bf(r(L) * 0.2)
    Wk2_words, Wk2_scales = pack_weight(r((L, L)) * 4.0 / np.sqrt(L) / t[:, None], "e4m3")
    bk2 = bf(r(L) * 0.2)
    Wv2_words, Wv2_scales = pack_weight(r((L, L)) * 3.2 / np.sqrt(L) / t[:, None], "e4m3")
    bv2 = bf(r(L) * 0.2)
    return {"attn1": bf(a * s), "v1": v1,
            "Wq2_words": Wq2_words, "Wq2_scales": Wq2_scales, "bq2": bq2,
            "Wk2_words": Wk2_words, "Wk2_scales": Wk2_scales, "bk2": bk2,
            "Wv2_words": Wv2_words, "Wv2_scales": Wv2_scales, "bv2": bv2}


def core(attn1, v1, Wq2_words, Wq2_scales, bq2, Wk2_words, Wk2_scales, bk2, Wv2_words, Wv2_scales, bv2):
    h = np.maximum(mxq(f64(attn1), 2, "e4m3") @ mxq(f64(v1), 1, "e4m3"), 0.0)
    hq = mxq(h, 2, "e4m3")
    q2 = (hq @ unpack_weight(Wq2_words, Wq2_scales, "e4m3")) + f64(bq2)
    k2 = (hq @ unpack_weight(Wk2_words, Wk2_scales, "e4m3")) + f64(bk2)
    v2 = (hq @ unpack_weight(Wv2_words, Wv2_scales, "e4m3")) + f64(bv2)
    return q2, k2, v2


def e4m3fn_bytes(y):
    return np.clip(np.asarray(y, np.float64), -448.0, 448.0).astype(np.float32).astype(ml_dtypes.float8_e4m3fn).view(np.uint8)


def e4m3fn_values(b):
    return np.asarray(b, np.uint8).view(ml_dtypes.float8_e4m3fn).astype(np.float64)


def setup_inputs():
    d = draw0()
    x0 = np.asarray(d['attn1']).astype(np.float64)
    s = (np.max(np.abs(x0), axis=(0, 1), keepdims=True) / 448.0).astype(np.float32)
    out = {}
    for k, v in d.items():
        if k == 'attn1':
            out['attn1_bytes'] = e4m3fn_bytes(x0 / s.astype(np.float64))
            out['attn1_scale'] = s
        else:
            out[k] = v
    return out


def reference(attn1_bytes, attn1_scale, v1, Wq2_words, Wq2_scales, bq2, Wk2_words, Wk2_scales, bk2, Wv2_words, Wv2_scales, bv2):
    return core(e4m3fn_values(attn1_bytes) * attn1_scale.astype(np.float64), v1, Wq2_words, Wq2_scales, bq2, Wk2_words, Wk2_scales, bk2, Wv2_words, Wv2_scales, bv2)

@@ -1,0 +1,330 @@
+from contextlib import ExitStack
+
+import concourse.mybir as mybir
+from concourse.masks import make_identity
+
+SETS, POINTS, FEATS = 6, 512, 512
+FLOPS = 2 * SETS * POINTS * FEATS * (POINTS + 3 * FEATS)
+
+F32 = mybir.dt.float32
+BF16 = mybir.dt.bfloat16
+U8 = mybir.dt.uint8
+I32 = mybir.dt.int32
+FP8 = mybir.dt.float8_e4m3fn
+FP8X4 = mybir.dt.float8_e4m3fn_x4
+ADD = mybir.AluOpType.add
+MULT = mybir.AluOpType.mult
+COPY = mybir.ActivationFunctionType.Copy
+RELU = mybir.ActivationFunctionType.Relu
+
+P = 128
+PAIRS = 2 * SETS
+EARLY = 3
+SHARED = {9: (1,), 10: (1,), 11: (1, 5)}
+
+
+def tile_perspectronencodernetwork_pa_w8_kernel(
+    tc, attn1_bytes, attn1_scale, v1,
+    wq_words, wq_scales, bq, wk_words, wk_scales, bk, wv_words, wv_scales, bv,
+    out_0, out_1, out_2,
+):
+    nc = tc.nc
+    outs = [out_0, out_1, out_2]
+    words_in = [wq_words, wk_words, wv_words]
+    wscales_in = [wq_scales, wk_scales, wv_scales]
+    biases_in = [bq, bk, bv]
+
+    with ExitStack() as ctx:
+        keep = ctx.enter_context(tc.tile_pool(name="keep", bufs=1))
+        work = ctx.enter_context(tc.tile_pool(name="work", bufs=4))
+        vwork = ctx.enter_context(tc.tile_pool(name="vwork", bufs=3))
+        stores = ctx.enter_context(tc.tile_pool(name="stores", bufs=5))
+        ps_out = ctx.enter_context(tc.psum_pool(name="ps_out", bufs=4))
+        ps_h = ctx.enter_context(tc.psum_pool(name="ps_h", bufs=2))
+        ps_x = ctx.enter_context(tc.psum_pool(name="ps_x", bufs=2))
+        ctx.enter_context(tc.manual_schedule())
+
+        ident = keep.tile([P, P], F32)
+        make_identity(nc, ident[:])
+        bias_rows = keep.tile([P, 3 * FEATS], BF16)
+        nc.vector.memset(bias_rows[:].bitcast(F32), 0.0)
+        wscale_sb = keep.tile([P, 3 * FEATS], U8, align_bytes=64)
+        nc.vector.memset(wscale_sb[:].bitcast(I32), 0)
+        warm = keep.tile([P, 1], F32)
+        nc.vector.memset(warm[:], 0.0)
+        ones = keep.tile([P, P], BF16)
+        nc.vector.memset(ones[:], 1.0)
+
+        for w in range(3):
+            nc.scalar.dma_start(out=bias_rows[0:1, FEATS * w : FEATS * (w + 1)], in_=biases_in[w].rearrange("(o n) -> o n", o=1))
+        warm_out = keep.tile([P, 1], F32)
+        nc.scalar.activation(out=warm_out[:], in_=warm[:], func=RELU)
+        scale_col = keep.tile([P, 4], F32)
+        nc.sync.dma_start(out=scale_col[:], in_=attn1_scale.rearrange("a b (p t) -> p (a b t)", t=4))
+        codes_in = keep.tile([P, SETS, 4, POINTS], U8, align_bytes=64)
+        vraw = keep.tile([P, SETS, 4, FEATS], BF16, align_bytes=64)
+        w_sb = keep.tile([P, 3, 4 * FEATS], U8, align_bytes=64)
+
+        def load_codes(b0, b1):
+            nc.sync.dma_start(out=codes_in[:, b0:b1], in_=attn1_bytes[b0:b1].rearrange("b (p r) s -> p b r s", r=4))
+
+        def load_v(b0, b1):
+            nc.sync.dma_start(out=vraw[:, b0:b1], in_=v1[b0:b1].rearrange("b (p j) f -> p b j f", j=4))
+
+        def load_words(w):
+            nc.sync.dma_start(out=w_sb[:, w, :], in_=words_in[w][0].rearrange("p n t -> p (n t)"))
+
+        def load_wscales(w):
+            for quad in range(4):
+                nc.sync.dma_start(
+                    out=wscale_sb[32 * quad : 32 * quad + 4, FEATS * w : FEATS * (w + 1)].bitcast(I32),
+                    in_=wscales_in[w][0, 4 * quad : 4 * quad + 4, :].bitcast(I32),
+                )
+
+        load_codes(0, 1)
+        load_v(0, 1)
+        load_v(1, 2)
+        load_codes(1, 2)
+        load_wscales(0)
+        load_words(0)
+        load_wscales(1)
+        load_words(1)
+        load_codes(2, 3)
+        load_words(2)
+        load_wscales(2)
+        load_v(2, 3)
+        load_codes(3, 6)
+        load_v(3, 6)
+
+        scale_ps = ps_x.tile([P, 4, P], F32, tag="x")
+        for t in range(4):
+            nc.tensor.transpose(scale_ps[:, t, :], scale_col[:, t : t + 1].to_broadcast([P, P]), ident[:])
+        scale_sb = keep.tile([P, POINTS], F32)
+        nc.scalar.copy(out=scale_sb[:].rearrange("q (p t) -> q p t", t=4), in_=scale_ps[:].rearrange("q t p -> q p t"))
+
+        bias_sb = keep.tile([P, 3, FEATS], BF16)
+
+        def spread_biases(w0, w1):
+            ps = ps_out.tile([P, 2, FEATS], BF16, tag="o", name="bias_ps")
+            for w in range(w0, w1):
+                nc.tensor.matmul(ps[:, w - w0, :], lhsT=ones[:], rhs=bias_rows[:, FEATS * w : FEATS * (w + 1)], start=True, stop=True)
+            (nc.vector.tensor_copy if w0 else nc.scalar.copy)(out=bias_sb[:, w0:w1, :], in_=ps[:, : w1 - w0, :])
+
+        cast, prod, xt, xg, xq, xs = {}, {}, {}, {}, {}, {}
+        vg, vq, vs = {}, {}, {}
+        hps, hg, hq, hs = {}, {}, {}, {}
+        bank, res, done = {}, {}, {}
+
+        def do_cast(i):
+            if i >= PAIRS:
+                return
+            c = work.tile([P, 2, POINTS], BF16, tag="cast", name="cast_t")
+            cast[i] = c
+            h = 2 * (i % 2)
+            nc.scalar.copy(out=c[:], in_=codes_in[:, i // 2, h : h + 2, :].bitcast(FP8))
+
+        def do_prod(i, k):
+            if i >= PAIRS:
+                return
+            if k == 0:
+                y = work.tile([P, 2, POINTS], BF16, tag="prod", name="prod_t", align_bytes=64)
+                prod[i] = y
+            if i < EARLY:
+                nc.vector.tensor_tensor(out=prod[i][:, k, :], in0=codes_in[:, i // 2, 2 * (i % 2) + k, :].bitcast(FP8), in1=scale_sb[:], op=MULT)
+            else:
+                nc.gpsimd.tensor_tensor(out=prod[i][:, k, :], in0=cast[i][:, k, :], in1=scale_sb[:], op=MULT)
+
+        def do_turn(i):
+            if i >= PAIRS:
+                return
+            x = ps_x.tile([P, 2, 2, P], F32, tag="x", name="xt_t")
+            xt[i] = x
+            pairs_of_k = prod[i][:].rearrange("p r s -> p (r s)").bitcast(F32)
+            for r in range(2):
+                for u in range(2):
+                    nc.tensor.transpose(x[:, r, u, :], pairs_of_k[:, 256 * r + u : 256 * (r + 1) : 2], ident[:])
+
+        def do_group(i):
+            if i >= PAIRS:
+                return
+            g = work.tile([P, 2 * P * 4], BF16, tag="xg", name="xg_t", align_bytes=64)
+            xg[i] = g
+            (nc.vector.tensor_copy if i == 1 else nc.scalar.copy)(out=g[:].bitcast(F32).rearrange("p (r q u) -> p r q u", r=2, u=2), in_=xt[i][:].rearrange("p r u q -> p r q u"))
+
+        def do_quant_x(i):
+            if i >= PAIRS:
+                return
+            q = work.tile([P, 4 * 2 * P], U8, tag="xq", name="xq_t", align_bytes=64)
+            s = work.tile([P, 2 * P], U8, tag="xs", name="xs_t", align_bytes=64)
+            xq[i], xs[i] = q, s
+            nc.vector.quantize_mx(out=q[:].bitcast(FP8X4), scales=s[:], in_=xg[i][:])
+
+        def do_group_v(j, k):
+            if j >= PAIRS:
+                return
+            b, quarter = j // 2, 2 * (j % 2) + k
+            if quarter == 0:
+                g = vwork.tile([P, 4, P, 4], BF16, tag="vg", name="vg_t", align_bytes=64)
+                vg[b] = g
+            m = slice(32 * quarter, 32 * (quarter + 1))
+            src = vraw[:, b].rearrange("p j (m t) -> p m t j", t=4)[:, m]
+            dst = vg[b][:].rearrange("p t m j -> p m t j")[:, m]
+            if b < 2 and quarter == 3:
+                nc.vector.tensor_copy(out=dst, in_=src)
+            else:
+                nc.scalar.copy(out=dst, in_=src)
+
+        def do_quant_v(j):
+            if j >= PAIRS:
+                return
+            b, half = j // 2, j % 2
+            if half == 0:
+                q = vwork.tile([P, 4 * FEATS], U8, tag="vq", name="vq_t", align_bytes=64)
+                s = vwork.tile([P, FEATS], U8, tag="vs", name="vs_t", align_bytes=64)
+                vq[b], vs[b] = q, s
+            nc.vector.quantize_mx(
+                out=vq[b][:, 1024 * half : 1024 * (half + 1)].bitcast(FP8X4),
+                scales=vs[b][:, 256 * half : 256 * (half + 1)],
+                in_=vg[b][:, 2 * half : 2 * half + 2].rearrange("p t m j -> p (t m j)"),
+            )
+
+        def do_mix(i, r):
+            if i >= PAIRS:
+                return
+            b = i // 2
+            h = ps_h.tile([P, 4, P], F32, tag="h", name="h_t")
+            hps[(i, r)] = h
+            for t in range(4):
+                nc.tensor.matmul_mx(
+                    out=h[:, t, :],
+                    lhsT=vq[b][:, 512 * t : 512 * (t + 1)].bitcast(FP8X4),
+                    lhsT_scale=vs[b][:, P * t : P * (t + 1)],
+                    rhs=xq[i][:, 512 * r : 512 * (r + 1)].bitcast(FP8X4),
+                    rhs_scale=xs[i][:, P * r : P * (r + 1)],
+                    start=True, stop=True,
+                )
+
+        def do_relu(i, r):
+            if i >= PAIRS:
+                return
+            if r == 0:
+                g = work.tile([P, 2, P, 4], BF16, tag="hg", name="hg_t", align_bytes=64)
+                hg[i] = g
+            nc.scalar.activation(out=hg[i][:, r], in_=hps[(i, r)][:].rearrange("p t q -> p q t"), func=RELU)
+
+        def do_quant_h(i):
+            if i >= PAIRS:
+                return
+            q = work.tile([P, 4 * 2 * P], U8, tag="hq", name="hq_t", align_bytes=64)
+            s = work.tile([P, 2 * P], U8, tag="hs", name="hs_t", align_bytes=64)
+            hq[i], hs[i] = q, s
+            nc.vector.quantize_mx(out=q[:].bitcast(FP8X4), scales=s[:], in_=hg[i][:].rearrange("p r q t -> p (r q t)"))
+
+        def do_project(i, k):
+            w, r = k // 2, k % 2
+            o = ps_out.tile([P, FEATS], F32, tag="o", name="o_t")
+            bank[(i, k)] = o
+            nc.tensor.matmul_mx(
+                out=o[:],
+                lhsT=hq[i][:, 512 * r : 512 * (r + 1)].bitcast(FP8X4),
+                lhsT_scale=hs[i][:, P * r : P * (r + 1)],
+                rhs=w_sb[:, w, :].bitcast(FP8X4),
+                rhs_scale=wscale_sb[:, FEATS * w : FEATS * (w + 1)],
+                start=True, stop=True,
+            )
+
+        def store(i, k):
+            w, r = k // 2, k % 2
+            h = 2 * (i % 2)
+            rows = outs[w][i // 2].rearrange("(p r) n -> p r n", r=4)
+            y = res[(i, w)]
+            if i == PAIRS - 1 and w == 2:
+                nc.sync.dma_start(out=rows[:, h + r, :], in_=y[:, r, :])
+            elif (i, w) in done:
+                nc.sync.dma_start(out=rows[:, h : h + 2, :], in_=y[:])
+            done[(i, w)] = True
+
+        def do_add(i, k):
+            w, r = k // 2, k % 2
+            if (i, w) not in res:
+                y = stores.tile([P, 2, FEATS], F32, tag="y%d" % w, name="y_t")
+                res[(i, w)] = y
+            if k in SHARED.get(i, ()):
+                z = work.tile([P, FEATS], F32, tag="z", name="z_t")
+                nc.scalar.copy(out=z[:], in_=bank[(i, k)][:])
+                bank[(i, k)] = z
+            else:
+                nc.vector.tensor_tensor(out=res[(i, w)][:, r, :], in0=bank[(i, k)][:], in1=bias_sb[:, w, :], op=ADD)
+                store(i, k)
+
+        def do_late_add(i, k):
+            if k in SHARED.get(i, ()):
+                w, r = k // 2, k % 2
+                nc.gpsimd.tensor_tensor(out=res[(i, w)][:, r, :], in0=bank[(i, k)][:], in1=bias_sb[:, w, :], op=ADD)
+                store(i, k)
+
+        do_prod(0, 0)
+        do_prod(0, 1)
+        do_group_v(0, 0)
+        do_group_v(0, 1)
+        do_turn(0)
+        do_prod(1, 0)
+        do_prod(1, 1)
+        do_group_v(1, 0)
+        do_group_v(1, 1)
+        do_quant_v(0)
+        do_group(0)
+        do_quant_x(0)
+        do_quant_v(1)
+        spread_biases(0, 2)
+        do_turn(1)
+        do_mix(0, 0)
+        do_mix(0, 1)
+        do_group_v(2, 0)
+        do_group(1)
+        do_relu(0, 0)
+        do_relu(0, 1)
+        do_prod(2, 0)
+        do_cast(3)
+        do_prod(2, 1)
+        do_quant_h(0)
+        do_group_v(3, 1)
+        spread_biases(2, 3)
+        do_quant_x(1)
+        do_group_v(2, 1)
+        do_group_v(3, 0)
+        do_prod(3, 0)
+        do_prod(3, 1)
+
+        for i in range(PAIRS):
+            do_project(i, 0)
+            do_project(i, 1)
+            do_mix(i + 1, 0)
+            do_project(i, 2)
+            do_add(i, 0)
+            do_mix(i + 1, 1)
+            do_add(i, 1)
+            do_late_add(i, 1)
+            do_project(i, 3)
+            do_add(i, 2)
+            do_add(i, 3)
+            do_relu(i + 1, 0)
+            do_relu(i + 1, 1)
+            do_turn(i + 2)
+            do_group(i + 2)
+            do_group_v(i + 4, 0)
+            do_project(i, 4)
+            do_quant_h(i + 1)
+            do_cast(i + 4)
+            if i % 2 == 0:
+                do_quant_v(i + 2)
+            do_project(i, 5)
+            do_quant_x(i + 2)
+            do_prod(i + 4, 0)
+            do_prod(i + 4, 1)
+            if i % 2 == 0:
+                do_quant_v(i + 3)
+            do_group_v(i + 4, 1)
+            do_add(i, 4)
+            do_add(i, 5)
+            do_late_add(i, 5)

@@ -19,8 +19,10 @@ RELU = mybir.ActivationFunctionType.Relu
 
 P = 128
 PAIRS = 2 * SETS
+BANKS = 6
 EARLY = 3
-SHARED = {9: (1,), 10: (1,), 11: (1, 5)}
+LATE = 2
+SHARED = {9: (0,), 10: (0,), 11: (0,)}
 
 
 def tile_perspectronencodernetwork_pa_w8_kernel(
@@ -36,40 +38,32 @@ def tile_perspectronencodernetwork_pa_w8_kernel(
 
     with ExitStack() as ctx:
         keep = ctx.enter_context(tc.tile_pool(name="keep", bufs=1))
-        work = ctx.enter_context(tc.tile_pool(name="work", bufs=4))
-        vwork = ctx.enter_context(tc.tile_pool(name="vwork", bufs=3))
-        stores = ctx.enter_context(tc.tile_pool(name="stores", bufs=5))
+        work = ctx.enter_context(tc.tile_pool(name="work", bufs=3))
+        stores = ctx.enter_context(tc.tile_pool(name="stores", bufs=8))
         ps_out = ctx.enter_context(tc.psum_pool(name="ps_out", bufs=4))
         ps_h = ctx.enter_context(tc.psum_pool(name="ps_h", bufs=2))
         ps_x = ctx.enter_context(tc.psum_pool(name="ps_x", bufs=2))
         ctx.enter_context(tc.manual_schedule())
 
-        ident = keep.tile([P, P], F32)
-        make_identity(nc, ident[:])
-        bias_rows = keep.tile([P, 3 * FEATS], BF16)
+        bias_rows = keep.tile([P, 3 * FEATS], BF16, name="bias_rows")
         nc.vector.memset(bias_rows[:].bitcast(F32), 0.0)
-        wscale_sb = keep.tile([P, 3 * FEATS], U8, align_bytes=64)
+        wscale_sb = keep.tile([P, 3 * FEATS], U8, align_bytes=64, name="wscale_sb")
         nc.vector.memset(wscale_sb[:].bitcast(I32), 0)
-        warm = keep.tile([P, 1], F32)
-        nc.vector.memset(warm[:], 0.0)
-        ones = keep.tile([P, P], BF16)
+        ones = keep.tile([P, P], BF16, name="ones")
         nc.vector.memset(ones[:], 1.0)
+        ident = keep.tile([P, P], F32, name="ident")
+        make_identity(nc, ident[:])
 
-        for w in range(3):
-            nc.scalar.dma_start(out=bias_rows[0:1, FEATS * w : FEATS * (w + 1)], in_=biases_in[w].rearrange("(o n) -> o n", o=1))
-        warm_out = keep.tile([P, 1], F32)
-        nc.scalar.activation(out=warm_out[:], in_=warm[:], func=RELU)
-        scale_col = keep.tile([P, 4], F32)
-        nc.sync.dma_start(out=scale_col[:], in_=attn1_scale.rearrange("a b (p t) -> p (a b t)", t=4))
-        codes_in = keep.tile([P, SETS, 4, POINTS], U8, align_bytes=64)
-        vraw = keep.tile([P, SETS, 4, FEATS], BF16, align_bytes=64)
-        w_sb = keep.tile([P, 3, 4 * FEATS], U8, align_bytes=64)
+        scale_col = keep.tile([P, 4], F32, name="scale_col")
+        codes_in = keep.tile([P, SETS, 4, POINTS], U8, align_bytes=64, name="codes_in")
+        vraw = keep.tile([P, SETS, 4, FEATS], BF16, align_bytes=64, name="vraw")
+        w_sb = keep.tile([P, 3, 4 * FEATS], U8, align_bytes=64, name="w_sb")
 
-        def load_codes(b0, b1):
-            nc.sync.dma_start(out=codes_in[:, b0:b1], in_=attn1_bytes[b0:b1].rearrange("b (p r) s -> p b r s", r=4))
+        def load_codes(b0, b1, r0=0, r1=4):
+            nc.sync.dma_start(out=codes_in[:, b0:b1, r0:r1], in_=attn1_bytes[b0:b1].rearrange("b (p r) s -> p b r s", r=4)[:, :, r0:r1])
 
-        def load_v(b0, b1):
-            nc.sync.dma_start(out=vraw[:, b0:b1], in_=v1[b0:b1].rearrange("b (p j) f -> p b j f", j=4))
+        def load_v(b0, b1, f0=0, f1=FEATS):
+            nc.sync.dma_start(out=vraw[:, b0:b1, :, f0:f1], in_=v1[b0:b1, :, f0:f1].rearrange("b (p j) f -> p b j f", j=4))
 
         def load_words(w):
             nc.sync.dma_start(out=w_sb[:, w, :], in_=words_in[w][0].rearrange("p n t -> p (n t)"))
@@ -81,107 +75,111 @@ def tile_perspectronencodernetwork_pa_w8_kernel(
                     in_=wscales_in[w][0, 4 * quad : 4 * quad + 4, :].bitcast(I32),
                 )
 
-        load_codes(0, 1)
-        load_v(0, 1)
-        load_v(1, 2)
+        def load_bias(w):
+            nc.scalar.dma_start(out=bias_rows[0:1, FEATS * w : FEATS * (w + 1)], in_=biases_in[w].rearrange("(o n) -> o n", o=1))
+
+        nc.sync.dma_start(out=scale_col[:], in_=attn1_scale.rearrange("a b (p t) -> p (a b t)", t=4))
+        load_v(0, 1, 0, FEATS // 2)
+        load_codes(0, 1, 0, 2)
+        load_v(0, 1, FEATS // 2, FEATS)
+        load_bias(0)
+        load_bias(1)
+        load_bias(2)
+        load_codes(0, 1, 2, 4)
         load_codes(1, 2)
         load_wscales(0)
         load_words(0)
+        load_v(1, 2)
         load_wscales(1)
         load_words(1)
-        load_codes(2, 3)
-        load_words(2)
         load_wscales(2)
+        load_words(2)
         load_v(2, 3)
+        load_codes(2, 3)
         load_codes(3, 6)
         load_v(3, 6)
 
-        scale_ps = ps_x.tile([P, 4, P], F32, tag="x")
-        for t in range(4):
-            nc.tensor.transpose(scale_ps[:, t, :], scale_col[:, t : t + 1].to_broadcast([P, P]), ident[:])
-        scale_sb = keep.tile([P, POINTS], F32)
-        nc.scalar.copy(out=scale_sb[:].rearrange("q (p t) -> q p t", t=4), in_=scale_ps[:].rearrange("q t p -> q p t"))
+        scale_sb = keep.tile([P, POINTS], F32, name="scale_sb")
+        bias_sb = keep.tile([P, 3, FEATS], BF16, name="bias_sb")
 
-        bias_sb = keep.tile([P, 3, FEATS], BF16)
+        def spread_scales():
+            scale_ps = ps_x.tile([P, 4, P], F32, tag="x", name="scale_ps")
+            for t in range(4):
+                nc.tensor.transpose(scale_ps[:, t, :], scale_col[:, t : t + 1].to_broadcast([P, P]), ident[:])
+            nc.scalar.activation(out=scale_sb[:].rearrange("q (p t) -> q p t", t=4), in_=scale_ps[:].rearrange("q t p -> q p t"), func=COPY)
+
+        bias_ps = {}
 
         def spread_biases(w0, w1):
             ps = ps_out.tile([P, 2, FEATS], BF16, tag="o", name="bias_ps")
+            bias_ps[w0] = ps
             for w in range(w0, w1):
                 nc.tensor.matmul(ps[:, w - w0, :], lhsT=ones[:], rhs=bias_rows[:, FEATS * w : FEATS * (w + 1)], start=True, stop=True)
-            (nc.vector.tensor_copy if w0 else nc.scalar.copy)(out=bias_sb[:, w0:w1, :], in_=ps[:, : w1 - w0, :])
 
-        cast, prod, xt, xg, xq, xs = {}, {}, {}, {}, {}, {}
+        def keep_biases(w0, w1):
+            nc.scalar.copy(out=bias_sb[:, w0:w1, :], in_=bias_ps[w0][:, : w1 - w0, :])
+
+        ring = [keep.tile([P, 2, POINTS], BF16, align_bytes=64, name="ring%d" % n) for n in range(3)]
+        first = [keep.tile([P, 2, POINTS], BF16, align_bytes=64, name="first%d" % n) for n in range(EARLY)]
+
+        def prod(i):
+            return first[i] if i < EARLY else ring[(2 * i - 1) % 3]
+
+        def xg(i):
+            return ring[(2 * i) % 3]
+
+        cast, xt, xq, xs = {}, {}, {}, {}
         vg, vq, vs = {}, {}, {}
         hps, hg, hq, hs = {}, {}, {}, {}
         bank, res, done = {}, {}, {}
 
         def do_cast(i):
-            if i >= PAIRS:
-                return
             c = work.tile([P, 2, POINTS], BF16, tag="cast", name="cast_t")
             cast[i] = c
             h = 2 * (i % 2)
             nc.scalar.copy(out=c[:], in_=codes_in[:, i // 2, h : h + 2, :].bitcast(FP8))
 
-        def do_prod(i, k):
-            if i >= PAIRS:
-                return
-            if k == 0:
-                y = work.tile([P, 2, POINTS], BF16, tag="prod", name="prod_t", align_bytes=64)
-                prod[i] = y
-            if i < EARLY:
-                nc.vector.tensor_tensor(out=prod[i][:, k, :], in0=codes_in[:, i // 2, 2 * (i % 2) + k, :].bitcast(FP8), in1=scale_sb[:], op=MULT)
-            else:
-                nc.gpsimd.tensor_tensor(out=prod[i][:, k, :], in0=cast[i][:, k, :], in1=scale_sb[:], op=MULT)
+        def do_prod_early(i, r):
+            nc.vector.tensor_tensor(out=prod(i)[:, r, :], in0=codes_in[:, i // 2, 2 * (i % 2) + r, :].bitcast(FP8), in1=scale_sb[:], op=MULT)
 
-        def do_turn(i):
-            if i >= PAIRS:
-                return
+        def do_prod(i):
+            nc.gpsimd.tensor_tensor(out=prod(i)[:], in0=cast[i][:], in1=scale_sb[:].unsqueeze(1).to_broadcast([P, 2, POINTS]), op=MULT)
+
+        def do_turn(i, tiles=(0, 1)):
             x = ps_x.tile([P, 2, 2, P], F32, tag="x", name="xt_t")
             xt[i] = x
-            pairs_of_k = prod[i][:].rearrange("p r s -> p (r s)").bitcast(F32)
-            for r in range(2):
+            for r in tiles:
+                pairs_of_k = prod(i)[:, r, :].bitcast(F32)
                 for u in range(2):
-                    nc.tensor.transpose(x[:, r, u, :], pairs_of_k[:, 256 * r + u : 256 * (r + 1) : 2], ident[:])
+                    nc.tensor.transpose(x[:, r, u, :], pairs_of_k[:, u : 256 : 2], ident[:])
 
-        def do_group(i):
-            if i >= PAIRS:
-                return
-            g = work.tile([P, 2 * P * 4], BF16, tag="xg", name="xg_t", align_bytes=64)
-            xg[i] = g
-            (nc.vector.tensor_copy if i == 1 else nc.scalar.copy)(out=g[:].bitcast(F32).rearrange("p (r q u) -> p r q u", r=2, u=2), in_=xt[i][:].rearrange("p r u q -> p r q u"))
+        def do_group(i, r0=0, r1=2, engine=None):
+            (engine or nc.scalar.copy)(
+                out=xg(i)[:, r0:r1, :].bitcast(F32).rearrange("p r (q u) -> p r q u", u=2),
+                in_=xt[i][:, r0:r1].rearrange("p r u q -> p r q u"),
+            )
 
-        def do_quant_x(i):
-            if i >= PAIRS:
-                return
-            q = work.tile([P, 4 * 2 * P], U8, tag="xq", name="xq_t", align_bytes=64)
-            s = work.tile([P, 2 * P], U8, tag="xs", name="xs_t", align_bytes=64)
-            xq[i], xs[i] = q, s
-            nc.vector.quantize_mx(out=q[:].bitcast(FP8X4), scales=s[:], in_=xg[i][:])
+        def do_quant_x(i, r0=0, r1=2):
+            if r0 == 0:
+                xq[i] = work.tile([P, 4 * 2 * P], U8, tag="xq", name="xq_t", align_bytes=64)
+                xs[i] = work.tile([P, 2 * P], U8, tag="xs", name="xs_t", align_bytes=64)
+            nc.vector.quantize_mx(
+                out=xq[i][:, 512 * r0 : 512 * r1].bitcast(FP8X4), scales=xs[i][:, P * r0 : P * r1],
+                in_=xg(i)[:, r0:r1, :].rearrange("p r s -> p (r s)"),
+            )
 
-        def do_group_v(j, k):
-            if j >= PAIRS:
-                return
-            b, quarter = j // 2, 2 * (j % 2) + k
-            if quarter == 0:
-                g = vwork.tile([P, 4, P, 4], BF16, tag="vg", name="vg_t", align_bytes=64)
-                vg[b] = g
-            m = slice(32 * quarter, 32 * (quarter + 1))
+        def do_group_v(b, quarter, quarters=1, engine=None):
+            if b not in vg:
+                vg[b] = work.tile([P, 4, P, 4], BF16, tag="vg", name="vg_t", align_bytes=64)
+            m = slice(32 * quarter, 32 * (quarter + quarters))
             src = vraw[:, b].rearrange("p j (m t) -> p m t j", t=4)[:, m]
             dst = vg[b][:].rearrange("p t m j -> p m t j")[:, m]
-            if b < 2 and quarter == 3:
-                nc.vector.tensor_copy(out=dst, in_=src)
-            else:
-                nc.scalar.copy(out=dst, in_=src)
+            (engine or nc.scalar.copy)(out=dst, in_=src)
 
-        def do_quant_v(j):
-            if j >= PAIRS:
-                return
-            b, half = j // 2, j % 2
+        def do_quant_v(b, half):
             if half == 0:
-                q = vwork.tile([P, 4 * FEATS], U8, tag="vq", name="vq_t", align_bytes=64)
-                s = vwork.tile([P, FEATS], U8, tag="vs", name="vs_t", align_bytes=64)
-                vq[b], vs[b] = q, s
+                vq[b] = work.tile([P, 4 * FEATS], U8, tag="vq", name="vq_t", align_bytes=64)
+                vs[b] = work.tile([P, FEATS], U8, tag="vs", name="vs_t", align_bytes=64)
             nc.vector.quantize_mx(
                 out=vq[b][:, 1024 * half : 1024 * (half + 1)].bitcast(FP8X4),
                 scales=vs[b][:, 256 * half : 256 * (half + 1)],
@@ -189,8 +187,6 @@ def tile_perspectronencodernetwork_pa_w8_kernel(
             )
 
         def do_mix(i, r):
-            if i >= PAIRS:
-                return
             b = i // 2
             h = ps_h.tile([P, 4, P], F32, tag="h", name="h_t")
             hps[(i, r)] = h
@@ -205,20 +201,18 @@ def tile_perspectronencodernetwork_pa_w8_kernel(
                 )
 
         def do_relu(i, r):
-            if i >= PAIRS:
-                return
             if r == 0:
-                g = work.tile([P, 2, P, 4], BF16, tag="hg", name="hg_t", align_bytes=64)
-                hg[i] = g
+                hg[i] = work.tile([P, 2, P, 4], BF16, tag="hg", name="hg_t", align_bytes=64)
             nc.scalar.activation(out=hg[i][:, r], in_=hps[(i, r)][:].rearrange("p t q -> p q t"), func=RELU)
 
-        def do_quant_h(i):
-            if i >= PAIRS:
-                return
-            q = work.tile([P, 4 * 2 * P], U8, tag="hq", name="hq_t", align_bytes=64)
-            s = work.tile([P, 2 * P], U8, tag="hs", name="hs_t", align_bytes=64)
-            hq[i], hs[i] = q, s
-            nc.vector.quantize_mx(out=q[:].bitcast(FP8X4), scales=s[:], in_=hg[i][:].rearrange("p r q t -> p (r q t)"))
+        def do_quant_h(i, r0=0, r1=2):
+            if r0 == 0:
+                hq[i] = work.tile([P, 4 * 2 * P], U8, tag="hq", name="hq_t", align_bytes=64)
+                hs[i] = work.tile([P, 2 * P], U8, tag="hs", name="hs_t", align_bytes=64)
+            nc.vector.quantize_mx(
+                out=hq[i][:, 512 * r0 : 512 * r1].bitcast(FP8X4), scales=hs[i][:, P * r0 : P * r1],
+                in_=hg[i][:, r0:r1].rearrange("p r q t -> p (r q t)"),
+            )
 
         def do_project(i, k):
             w, r = k // 2, k % 2
@@ -238,93 +232,131 @@ def tile_perspectronencodernetwork_pa_w8_kernel(
             h = 2 * (i % 2)
             rows = outs[w][i // 2].rearrange("(p r) n -> p r n", r=4)
             y = res[(i, w)]
-            if i == PAIRS - 1 and w == 2:
+            if i == PAIRS - 1 or any(s // 2 == w for s in SHARED.get(i, ())):
                 nc.sync.dma_start(out=rows[:, h + r, :], in_=y[:, r, :])
             elif (i, w) in done:
                 nc.sync.dma_start(out=rows[:, h : h + 2, :], in_=y[:])
             done[(i, w)] = True
 
-        def do_add(i, k):
+        def do_empty(i, k):
             w, r = k // 2, k % 2
             if (i, w) not in res:
-                y = stores.tile([P, 2, FEATS], F32, tag="y%d" % w, name="y_t")
-                res[(i, w)] = y
+                res[(i, w)] = stores.tile([P, 2, FEATS], F32, tag="y%d" % w, name="y_t")
             if k in SHARED.get(i, ()):
-                z = work.tile([P, FEATS], F32, tag="z", name="z_t")
-                nc.scalar.copy(out=z[:], in_=bank[(i, k)][:])
-                bank[(i, k)] = z
+                nc.scalar.copy(out=res[(i, w)][:, r, :], in_=bank[(i, k)][:])
             else:
                 nc.vector.tensor_tensor(out=res[(i, w)][:, r, :], in0=bank[(i, k)][:], in1=bias_sb[:, w, :], op=ADD)
-                store(i, k)
 
-        def do_late_add(i, k):
-            if k in SHARED.get(i, ()):
-                w, r = k // 2, k % 2
-                nc.gpsimd.tensor_tensor(out=res[(i, w)][:, r, :], in0=bank[(i, k)][:], in1=bias_sb[:, w, :], op=ADD)
-                store(i, k)
+        def do_late_add(i):
+            ks = SHARED.get(i, ())
+            if ks:
+                w, r0, r1 = ks[0] // 2, ks[0] % 2, ks[-1] % 2 + 1
+                y = res[(i, w)][:, r0:r1, :]
+                nc.gpsimd.tensor_tensor(out=y, in0=y, in1=bias_sb[:, w : w + 1, :].to_broadcast([P, r1 - r0, FEATS]), op=ADD)
 
-        do_prod(0, 0)
-        do_prod(0, 1)
-        do_group_v(0, 0)
-        do_group_v(0, 1)
-        do_turn(0)
-        do_prod(1, 0)
-        do_prod(1, 1)
-        do_group_v(1, 0)
-        do_group_v(1, 1)
-        do_quant_v(0)
-        do_group(0)
-        do_quant_x(0)
-        do_quant_v(1)
+        def order(i):
+            return [0, 2, 4, 1, 3, 5] if i == 0 else list(range(BANKS))
+
+        spread_scales()
         spread_biases(0, 2)
-        do_turn(1)
-        do_mix(0, 0)
-        do_mix(0, 1)
-        do_group_v(2, 0)
-        do_group(1)
-        do_relu(0, 0)
-        do_relu(0, 1)
-        do_prod(2, 0)
-        do_cast(3)
-        do_prod(2, 1)
-        do_quant_h(0)
-        do_group_v(3, 1)
         spread_biases(2, 3)
+        do_group_v(0, 0, 2, nc.vector.tensor_copy)
+        do_prod_early(0, 0)
+        do_turn(0, (0,))
+        do_group_v(0, 2)
+        do_group_v(0, 3, 1, nc.vector.tensor_copy)
+        keep_biases(0, 2)
+        keep_biases(2, 3)
+        do_group(0, 0, 1)
+        do_prod_early(0, 1)
+        do_turn(0, (1,))
+        do_group(0, 1, 2)
+        do_quant_v(0, 0)
+        do_quant_v(0, 1)
+        do_quant_x(0, 0, 1)
+        do_mix(0, 0)
+        do_prod_early(1, 0)
+        do_quant_x(0, 1, 2)
+        do_prod_early(1, 1)
+        do_cast(3)
+        do_relu(0, 0)
+        do_mix(0, 1)
+        do_turn(1)
+        do_prod_early(2, 0)
+        do_group_v(1, 3, 1, nc.vector.tensor_copy)
+        do_relu(0, 1)
+        do_quant_h(0, 0, 1)
+        do_project(0, 0)
+        do_group(1)
+        do_project(0, 2)
+        do_prod_early(2, 1)
+        do_project(0, 4)
+        do_quant_h(0, 1, 2)
+        do_project(0, 1)
+        do_turn(2)
+        do_empty(0, 0)
         do_quant_x(1)
-        do_group_v(2, 1)
-        do_group_v(3, 0)
-        do_prod(3, 0)
-        do_prod(3, 1)
+        do_prod(3)
+        do_group_v(1, 0, 2)
+        do_mix(1, 0)
+        do_mix(1, 1)
+        do_project(0, 3)
+        do_relu(1, 0)
+        do_relu(1, 1)
+        do_group_v(1, 2)
+        store(0, 0)
+        for k in order(0)[1 : BANKS - LATE]:
+            do_empty(0, k)
+            if k == 2:
+                do_project(0, 5)
+            store(0, k)
+        do_group(2, 0, 2, nc.vector.tensor_copy)
+        do_cast(4)
 
-        for i in range(PAIRS):
-            do_project(i, 0)
-            do_project(i, 1)
-            do_mix(i + 1, 0)
-            do_project(i, 2)
-            do_add(i, 0)
-            do_mix(i + 1, 1)
-            do_add(i, 1)
-            do_late_add(i, 1)
-            do_project(i, 3)
-            do_add(i, 2)
-            do_add(i, 3)
-            do_relu(i + 1, 0)
-            do_relu(i + 1, 1)
-            do_turn(i + 2)
-            do_group(i + 2)
-            do_group_v(i + 4, 0)
-            do_project(i, 4)
-            do_quant_h(i + 1)
-            do_cast(i + 4)
-            if i % 2 == 0:
-                do_quant_v(i + 2)
-            do_project(i, 5)
-            do_quant_x(i + 2)
-            do_prod(i + 4, 0)
-            do_prod(i + 4, 1)
-            if i % 2 == 0:
-                do_quant_v(i + 3)
-            do_group_v(i + 4, 1)
-            do_add(i, 4)
-            do_add(i, 5)
-            do_late_add(i, 5)
+        for c in range(1, PAIRS + 1):
+            if c + 2 < PAIRS:
+                do_turn(c + 2)
+                do_group(c + 2)
+            if c < PAIRS:
+                do_quant_h(c)
+            if c % 2 == 1 and c + 1 < PAIRS:
+                do_quant_v((c + 1) // 2, 0)
+                do_quant_v((c + 1) // 2, 1)
+            if c + 1 < PAIRS:
+                do_quant_x(c + 1)
+            if c + 3 < PAIRS:
+                do_prod(c + 3)
+            early = order(c)[: BANKS - LATE] if c < PAIRS else []
+            shared = SHARED.get(c, ())
+            vb, vh = (c + 3) // 2, (c + 1) % 2
+            if vb < SETS:
+                do_group_v(vb, 2 * vh, 2)
+            for k in early[:2]:
+                do_project(c, k)
+            for k in shared:
+                do_empty(c, k)
+            do_late_add(c)
+            if c + 1 < PAIRS:
+                do_mix(c + 1, 0)
+            if c + 1 < PAIRS:
+                do_mix(c + 1, 1)
+            for k in order(c - 1)[BANKS - LATE :]:
+                do_empty(c - 1, k)
+                store(c - 1, k)
+            for k in early[2:4]:
+                do_project(c, k)
+            if c + 1 < PAIRS:
+                do_relu(c + 1, 0)
+                do_relu(c + 1, 1)
+            if c + 4 < PAIRS:
+                do_cast(c + 4)
+            for n, k in enumerate(early):
+                if k not in shared:
+                    do_empty(c, k)
+                if n < 2:
+                    do_project(c, order(c)[4 + n])
+                if k not in shared:
+                    store(c, k)
+                if n == 3:
+                    for k in shared:
+                        store(c, k)

@@ -22,6 +22,10 @@ PAIRS = 2 * SETS
 BANKS = 6
 EARLY = 3
 LATE = 2
+LATE0 = 2
+OUT_BANKS = 4
+TURN_FIRST = False
+POOL_SHARE = 8
 SHARED = {9: (0,), 10: (0,), 11: (0,)}
 
 
@@ -116,8 +120,8 @@ def tile_perspectronencodernetwork_pa_w8_kernel(
             for w in range(w0, w1):
                 nc.tensor.matmul(ps[:, w - w0, :], lhsT=ones[:], rhs=bias_rows[:, FEATS * w : FEATS * (w + 1)], start=True, stop=True)
 
-        def keep_biases(w0, w1):
-            nc.scalar.copy(out=bias_sb[:, w0:w1, :], in_=bias_ps[w0][:, : w1 - w0, :])
+        def keep_biases(w0, w1, engine):
+            engine(out=bias_sb[:, w0:w1, :], in_=bias_ps[w0][:, : w1 - w0, :])
 
         ring = [keep.tile([P, 2, POINTS], BF16, align_bytes=64, name="ring%d" % n) for n in range(3)]
         first = [keep.tile([P, 2, POINTS], BF16, align_bytes=64, name="first%d" % n) for n in range(EARLY)]
@@ -168,23 +172,21 @@ def tile_perspectronencodernetwork_pa_w8_kernel(
                 in_=xg(i)[:, r0:r1, :].rearrange("p r s -> p (r s)"),
             )
 
-        def do_group_v(b, quarter, quarters=1, engine=None):
+        def do_group_v(b, n0, n1, engine=None):
             if b not in vg:
                 vg[b] = work.tile([P, 4, P, 4], BF16, tag="vg", name="vg_t", align_bytes=64)
-            m = slice(32 * quarter, 32 * (quarter + quarters))
-            src = vraw[:, b].rearrange("p j (m t) -> p m t j", t=4)[:, m]
-            dst = vg[b][:].rearrange("p t m j -> p m t j")[:, m]
+            src = vraw[:, b].rearrange("p j (n m t) -> p n t m j", m=2, t=4)[:, n0:n1]
+            dst = vg[b][:].rearrange("p t (n m) j -> p n t m j", m=2)[:, n0:n1]
             (engine or nc.scalar.copy)(out=dst, in_=src)
 
-        def do_quant_v(b, half):
-            if half == 0:
-                vq[b] = work.tile([P, 4 * FEATS], U8, tag="vq", name="vq_t", align_bytes=64)
-                vs[b] = work.tile([P, FEATS], U8, tag="vs", name="vs_t", align_bytes=64)
-            nc.vector.quantize_mx(
-                out=vq[b][:, 1024 * half : 1024 * (half + 1)].bitcast(FP8X4),
-                scales=vs[b][:, 256 * half : 256 * (half + 1)],
-                in_=vg[b][:, 2 * half : 2 * half + 2].rearrange("p t m j -> p (t m j)"),
-            )
+        def do_group_v_pool(b, n0, n1):
+            src = vraw[:, b].rearrange("p j (m t) -> p t m j", t=4)[:, :, 2 * n0 : 2 * n1]
+            nc.gpsimd.tensor_scalar(out=vg[b][:, :, 2 * n0 : 2 * n1], in0=src, scalar1=1.0, scalar2=0.0, op0=MULT, op1=ADD)
+
+        def do_quant_v(b):
+            vq[b] = work.tile([P, 4 * FEATS], U8, tag="vq", name="vq_t", align_bytes=64)
+            vs[b] = work.tile([P, FEATS], U8, tag="vs", name="vs_t", align_bytes=64)
+            nc.vector.quantize_mx(out=vq[b][:].bitcast(FP8X4), scales=vs[b][:], in_=vg[b][:].rearrange("p t m j -> p (t m j)"))
 
         def do_mix(i, r):
             b = i // 2
@@ -232,7 +234,7 @@ def tile_perspectronencodernetwork_pa_w8_kernel(
             h = 2 * (i % 2)
             rows = outs[w][i // 2].rearrange("(p r) n -> p r n", r=4)
             y = res[(i, w)]
-            if i == PAIRS - 1 or any(s // 2 == w for s in SHARED.get(i, ())):
+            if i >= PAIRS - 3 or any(s // 2 == w for s in SHARED.get(i, ())):
                 nc.sync.dma_start(out=rows[:, h + r, :], in_=y[:, r, :])
             elif (i, w) in done:
                 nc.sync.dma_start(out=rows[:, h : h + 2, :], in_=y[:])
@@ -257,22 +259,21 @@ def tile_perspectronencodernetwork_pa_w8_kernel(
         def order(i):
             return [0, 2, 4, 1, 3, 5] if i == 0 else list(range(BANKS))
 
+        def late(i):
+            return LATE0 if i == 0 else LATE
+
         spread_scales()
-        spread_biases(0, 2)
-        spread_biases(2, 3)
-        do_group_v(0, 0, 2, nc.vector.tensor_copy)
+        do_group_v(0, 0, 32, nc.vector.tensor_copy)
         do_prod_early(0, 0)
         do_turn(0, (0,))
-        do_group_v(0, 2)
-        do_group_v(0, 3, 1, nc.vector.tensor_copy)
-        keep_biases(0, 2)
-        keep_biases(2, 3)
+        do_group_v(0, 32, 48)
+        do_group_v(0, 48, 64, nc.vector.tensor_copy)
         do_group(0, 0, 1)
         do_prod_early(0, 1)
         do_turn(0, (1,))
+        spread_biases(0, 2)
         do_group(0, 1, 2)
-        do_quant_v(0, 0)
-        do_quant_v(0, 1)
+        do_quant_v(0)
         do_quant_x(0, 0, 1)
         do_mix(0, 0)
         do_prod_early(1, 0)
@@ -281,82 +282,93 @@ def tile_perspectronencodernetwork_pa_w8_kernel(
         do_cast(3)
         do_relu(0, 0)
         do_mix(0, 1)
+        spread_biases(2, 3)
         do_turn(1)
+        keep_biases(0, 2, nc.vector.tensor_copy)
         do_prod_early(2, 0)
-        do_group_v(1, 3, 1, nc.vector.tensor_copy)
         do_relu(0, 1)
         do_quant_h(0, 0, 1)
         do_project(0, 0)
         do_group(1)
+        keep_biases(2, 3, nc.scalar.copy)
         do_project(0, 2)
         do_prod_early(2, 1)
         do_project(0, 4)
         do_quant_h(0, 1, 2)
         do_project(0, 1)
-        do_turn(2)
         do_empty(0, 0)
+        do_group_v(1, 48, 64, nc.vector.tensor_copy)
         do_quant_x(1)
         do_prod(3)
-        do_group_v(1, 0, 2)
+        do_group_v(1, 0, 32)
         do_mix(1, 0)
         do_mix(1, 1)
         do_project(0, 3)
+        do_turn(2)
         do_relu(1, 0)
         do_relu(1, 1)
-        do_group_v(1, 2)
+        do_group_v(1, 32, 48)
         store(0, 0)
-        for k in order(0)[1 : BANKS - LATE]:
+        for k in order(0)[1 : BANKS - LATE0]:
             do_empty(0, k)
             if k == 2:
                 do_project(0, 5)
             store(0, k)
         do_group(2, 0, 2, nc.vector.tensor_copy)
         do_cast(4)
+        do_turn(3)
 
         for c in range(1, PAIRS + 1):
-            if c + 2 < PAIRS:
-                do_turn(c + 2)
-                do_group(c + 2)
-            if c < PAIRS:
+            new_set = c % 2 == 1 and c + 1 < PAIRS
+            if new_set:
                 do_quant_h(c)
-            if c % 2 == 1 and c + 1 < PAIRS:
-                do_quant_v((c + 1) // 2, 0)
-                do_quant_v((c + 1) // 2, 1)
             if c + 1 < PAIRS:
                 do_quant_x(c + 1)
+            if new_set:
+                do_quant_v((c + 1) // 2)
+            elif c < PAIRS:
+                do_quant_h(c)
             if c + 3 < PAIRS:
                 do_prod(c + 3)
-            early = order(c)[: BANKS - LATE] if c < PAIRS else []
+            left = [(c - 1, k) for k in order(c - 1)[BANKS - late(c - 1) :]]
+            fresh = [(c, k) for k in order(c)] if c < PAIRS else []
+            free = OUT_BANKS - len(left)
             shared = SHARED.get(c, ())
+            if c + 2 < PAIRS:
+                do_group(c + 2)
             vb, vh = (c + 3) // 2, (c + 1) % 2
             if vb < SETS:
-                do_group_v(vb, 2 * vh, 2)
-            for k in early[:2]:
-                do_project(c, k)
+                do_group_v(vb, 32 * vh, 32 * (vh + 1) - POOL_SHARE)
+                do_group_v_pool(vb, 32 * (vh + 1) - POOL_SHARE, 32 * (vh + 1))
+            if c + 1 < PAIRS and not new_set:
+                do_mix(c + 1, 0)
+            for i, k in fresh[:free]:
+                do_project(i, k)
             for k in shared:
                 do_empty(c, k)
             do_late_add(c)
             if c + 1 < PAIRS:
-                do_mix(c + 1, 0)
-            if c + 1 < PAIRS:
+                if new_set:
+                    do_mix(c + 1, 0)
                 do_mix(c + 1, 1)
-            for k in order(c - 1)[BANKS - LATE :]:
-                do_empty(c - 1, k)
-                store(c - 1, k)
-            for k in early[2:4]:
-                do_project(c, k)
-            if c + 1 < PAIRS:
                 do_relu(c + 1, 0)
                 do_relu(c + 1, 1)
             if c + 4 < PAIRS:
                 do_cast(c + 4)
-            for n, k in enumerate(early):
-                if k not in shared:
-                    do_empty(c, k)
-                if n < 2:
-                    do_project(c, order(c)[4 + n])
-                if k not in shared:
-                    store(c, k)
-                if n == 3:
+            waiting = fresh[free:]
+            todo = left + fresh[: BANKS - late(c)]
+            for n, (i, k) in enumerate(todo):
+                mine = not (i == c and k in shared)
+                if mine:
+                    do_empty(i, k)
+                if len(waiting) == 1 and c + 3 < PAIRS and TURN_FIRST:
+                    do_turn(c + 3)
+                if waiting:
+                    do_project(*waiting.pop(0))
+                if mine:
+                    store(i, k)
+                if n == len(todo) - 2:
                     for k in shared:
                         store(c, k)
+            if c + 3 < PAIRS and not TURN_FIRST:
+                do_turn(c + 3)

@@ -21,12 +21,7 @@ P = 128
 PAIRS = 2 * SETS
 BANKS = 6
 EARLY = 3
-LATE = 2
-LATE0 = 2
-OUT_BANKS = 4
-TURN_FIRST = False
-POOL_SHARE = 8
-SHARED = {9: (0,), 10: (0,), 11: (0,)}
+SHARED = {9: (0,), 10: (0,)}
 
 
 def tile_perspectronencodernetwork_pa_w8_kernel(
@@ -43,31 +38,28 @@ def tile_perspectronencodernetwork_pa_w8_kernel(
     with ExitStack() as ctx:
         keep = ctx.enter_context(tc.tile_pool(name="keep", bufs=1))
         work = ctx.enter_context(tc.tile_pool(name="work", bufs=3))
-        stores = ctx.enter_context(tc.tile_pool(name="stores", bufs=8))
-        ps_out = ctx.enter_context(tc.psum_pool(name="ps_out", bufs=4))
+        stores = ctx.enter_context(tc.tile_pool(name="stores", bufs=SETS))
+        ps_out = ctx.enter_context(tc.psum_pool(name="ps_out", bufs=1))
         ps_h = ctx.enter_context(tc.psum_pool(name="ps_h", bufs=2))
         ps_x = ctx.enter_context(tc.psum_pool(name="ps_x", bufs=2))
         ctx.enter_context(tc.manual_schedule())
 
-        bias_rows = keep.tile([P, 3 * FEATS], BF16, name="bias_rows")
-        nc.vector.memset(bias_rows[:].bitcast(F32), 0.0)
         wscale_sb = keep.tile([P, 3 * FEATS], U8, align_bytes=64, name="wscale_sb")
         nc.vector.memset(wscale_sb[:].bitcast(I32), 0)
-        ones = keep.tile([P, P], BF16, name="ones")
-        nc.vector.memset(ones[:], 1.0)
         ident = keep.tile([P, P], F32, name="ident")
         make_identity(nc, ident[:])
 
         scale_col = keep.tile([P, 4], F32, name="scale_col")
+        bias_col = keep.tile([P, 3, 16], BF16, name="bias_col")
         codes_in = keep.tile([P, SETS, 4, POINTS], U8, align_bytes=64, name="codes_in")
-        vraw = keep.tile([P, SETS, 4, FEATS], BF16, align_bytes=64, name="vraw")
+        vraw = [stores.tile([P, 2, 4, FEATS], BF16, tag="y%d" % n, name="vraw") for n in range(3)]
         w_sb = keep.tile([P, 3, 4 * FEATS], U8, align_bytes=64, name="w_sb")
 
         def load_codes(b0, b1, r0=0, r1=4):
             nc.sync.dma_start(out=codes_in[:, b0:b1, r0:r1], in_=attn1_bytes[b0:b1].rearrange("b (p r) s -> p b r s", r=4)[:, :, r0:r1])
 
-        def load_v(b0, b1, f0=0, f1=FEATS):
-            nc.sync.dma_start(out=vraw[:, b0:b1, :, f0:f1], in_=v1[b0:b1, :, f0:f1].rearrange("b (p j) f -> p b j f", j=4))
+        def load_v(b0, b1):
+            nc.sync.dma_start(out=vraw[b0 // 2][:, b0 % 2 : b0 % 2 + b1 - b0], in_=v1[b0:b1].rearrange("b (p j) f -> p b j f", j=4))
 
         def load_words(w):
             nc.sync.dma_start(out=w_sb[:, w, :], in_=words_in[w][0].rearrange("p n t -> p (n t)"))
@@ -80,28 +72,26 @@ def tile_perspectronencodernetwork_pa_w8_kernel(
                 )
 
         def load_bias(w):
-            nc.scalar.dma_start(out=bias_rows[0:1, FEATS * w : FEATS * (w + 1)], in_=biases_in[w].rearrange("(o n) -> o n", o=1))
+            nc.scalar.dma_start(out=bias_col[:, w, 0:4], in_=biases_in[w].rearrange("(p t) -> p t", t=4))
 
         nc.sync.dma_start(out=scale_col[:], in_=attn1_scale.rearrange("a b (p t) -> p (a b t)", t=4))
-        load_v(0, 1, 0, FEATS // 2)
-        load_codes(0, 1, 0, 2)
-        load_v(0, 1, FEATS // 2, FEATS)
+        load_v(0, 1)
+        load_codes(0, 1)
         load_bias(0)
         load_bias(1)
         load_bias(2)
-        load_codes(0, 1, 2, 4)
         load_codes(1, 2)
+        load_v(1, 2)
         load_wscales(0)
         load_words(0)
-        load_v(1, 2)
         load_wscales(1)
         load_words(1)
         load_wscales(2)
         load_words(2)
-        load_v(2, 3)
         load_codes(2, 3)
+        load_v(2, 4)
         load_codes(3, 6)
-        load_v(3, 6)
+        load_v(4, 6)
 
         scale_sb = keep.tile([P, POINTS], F32, name="scale_sb")
         bias_sb = keep.tile([P, 3, FEATS], BF16, name="bias_sb")
@@ -115,13 +105,18 @@ def tile_perspectronencodernetwork_pa_w8_kernel(
         bias_ps = {}
 
         def spread_biases(w0, w1):
-            ps = ps_out.tile([P, 2, FEATS], BF16, tag="o", name="bias_ps")
+            ps = ps_out.tile([P, 2, 2, P], F32, tag="o%d" % w1, name="bias_ps")
             bias_ps[w0] = ps
             for w in range(w0, w1):
-                nc.tensor.matmul(ps[:, w - w0, :], lhsT=ones[:], rhs=bias_rows[:, FEATS * w : FEATS * (w + 1)], start=True, stop=True)
+                words = bias_col[:, w, :].bitcast(F32)
+                for u in range(2):
+                    nc.tensor.transpose(ps[:, w - w0, u, :], words[:, u : u + 1].to_broadcast([P, P]), ident[:])
 
         def keep_biases(w0, w1, engine):
-            engine(out=bias_sb[:, w0:w1, :], in_=bias_ps[w0][:, : w1 - w0, :])
+            engine(
+                out=bias_sb[:, w0:w1, :].bitcast(F32).rearrange("q w (p u) -> q w p u", u=2),
+                in_=bias_ps[w0][:, : w1 - w0].rearrange("q w u p -> q w p u"),
+            )
 
         ring = [keep.tile([P, 2, POINTS], BF16, align_bytes=64, name="ring%d" % n) for n in range(3)]
         first = [keep.tile([P, 2, POINTS], BF16, align_bytes=64, name="first%d" % n) for n in range(EARLY)]
@@ -151,7 +146,8 @@ def tile_perspectronencodernetwork_pa_w8_kernel(
 
         def do_turn(i, tiles=(0, 1)):
             x = ps_x.tile([P, 2, 2, P], F32, tag="x", name="xt_t")
-            xt[i] = x
+            for r in tiles:
+                xt[(i, r)] = x
             for r in tiles:
                 pairs_of_k = prod(i)[:, r, :].bitcast(F32)
                 for u in range(2):
@@ -160,7 +156,7 @@ def tile_perspectronencodernetwork_pa_w8_kernel(
         def do_group(i, r0=0, r1=2, engine=None):
             (engine or nc.scalar.copy)(
                 out=xg(i)[:, r0:r1, :].bitcast(F32).rearrange("p r (q u) -> p r q u", u=2),
-                in_=xt[i][:, r0:r1].rearrange("p r u q -> p r q u"),
+                in_=xt[(i, r0)][:, r0:r1].rearrange("p r u q -> p r q u"),
             )
 
         def do_quant_x(i, r0=0, r1=2):
@@ -175,13 +171,10 @@ def tile_perspectronencodernetwork_pa_w8_kernel(
         def do_group_v(b, n0, n1, engine=None):
             if b not in vg:
                 vg[b] = work.tile([P, 4, P, 4], BF16, tag="vg", name="vg_t", align_bytes=64)
-            src = vraw[:, b].rearrange("p j (n m t) -> p n t m j", m=2, t=4)[:, n0:n1]
+            src = vraw[b // 2][:, b % 2].rearrange("p j (n m t) -> p n t m j", m=2, t=4)[:, n0:n1]
             dst = vg[b][:].rearrange("p t (n m) j -> p n t m j", m=2)[:, n0:n1]
             (engine or nc.scalar.copy)(out=dst, in_=src)
 
-        def do_group_v_pool(b, n0, n1):
-            src = vraw[:, b].rearrange("p j (m t) -> p t m j", t=4)[:, :, 2 * n0 : 2 * n1]
-            nc.gpsimd.tensor_scalar(out=vg[b][:, :, 2 * n0 : 2 * n1], in0=src, scalar1=1.0, scalar2=0.0, op0=MULT, op1=ADD)
 
         def do_quant_v(b):
             vq[b] = work.tile([P, 4 * FEATS], U8, tag="vq", name="vq_t", align_bytes=64)
@@ -218,7 +211,8 @@ def tile_perspectronencodernetwork_pa_w8_kernel(
 
         def do_project(i, k):
             w, r = k // 2, k % 2
-            o = ps_out.tile([P, FEATS], F32, tag="o", name="o_t")
+            n = len(bank)
+            o = ps_out.tile([P, FEATS], F32, tag="o%d" % (2 * (n // 2 % 2) + (n + n // 4) % 2), name="o_t")
             bank[(i, k)] = o
             nc.tensor.matmul_mx(
                 out=o[:],
@@ -229,146 +223,148 @@ def tile_perspectronencodernetwork_pa_w8_kernel(
                 start=True, stop=True,
             )
 
+        def tiles_per_store(i, w):
+            if (i == PAIRS - 1 and w == 2) or (i in SHARED and w == 0):
+                return 1
+            return 2
+
         def store(i, k):
-            w, r = k // 2, k % 2
-            h = 2 * (i % 2)
+            w, r = k // 2, 2 * (i % 2) + k % 2
             rows = outs[w][i // 2].rearrange("(p r) n -> p r n", r=4)
-            y = res[(i, w)]
-            if i >= PAIRS - 3 or any(s // 2 == w for s in SHARED.get(i, ())):
-                nc.sync.dma_start(out=rows[:, h + r, :], in_=y[:, r, :])
-            elif (i, w) in done:
-                nc.sync.dma_start(out=rows[:, h : h + 2, :], in_=y[:])
-            done[(i, w)] = True
+            n = tiles_per_store(i, w)
+            r0 = r // n * n
+            done[(i // 2, w, r0)] = done.get((i // 2, w, r0), 0) + 1
+            if done[(i // 2, w, r0)] == n:
+                nc.sync.dma_start(out=rows[:, r0 : r0 + n, :], in_=res[(i // 2, w)][:, r0 : r0 + n, :])
 
         def do_empty(i, k):
-            w, r = k // 2, k % 2
-            if (i, w) not in res:
-                res[(i, w)] = stores.tile([P, 2, FEATS], F32, tag="y%d" % w, name="y_t")
+            b, w, r = i // 2, k // 2, 2 * (i % 2) + k % 2
+            if (b, w) not in res:
+                res[(b, w)] = stores.tile([P, 4, FEATS], F32, tag="y%d" % w, name="y_t")
             if k in SHARED.get(i, ()):
-                nc.scalar.copy(out=res[(i, w)][:, r, :], in_=bank[(i, k)][:])
+                nc.scalar.copy(out=res[(b, w)][:, r, :], in_=bank[(i, k)][:])
             else:
-                nc.vector.tensor_tensor(out=res[(i, w)][:, r, :], in0=bank[(i, k)][:], in1=bias_sb[:, w, :], op=ADD)
+                nc.vector.tensor_tensor(out=res[(b, w)][:, r, :], in0=bank[(i, k)][:], in1=bias_sb[:, w, :], op=ADD)
 
         def do_late_add(i):
-            ks = SHARED.get(i, ())
-            if ks:
-                w, r0, r1 = ks[0] // 2, ks[0] % 2, ks[-1] % 2 + 1
-                y = res[(i, w)][:, r0:r1, :]
-                nc.gpsimd.tensor_tensor(out=y, in0=y, in1=bias_sb[:, w : w + 1, :].to_broadcast([P, r1 - r0, FEATS]), op=ADD)
+            for k in SHARED.get(i, ()):
+                b, w, r = i // 2, k // 2, 2 * (i % 2) + k % 2
+                y = res[(b, w)][:, r, :]
+                nc.gpsimd.tensor_tensor(out=y, in0=y, in1=bias_sb[:, w, :], op=ADD)
 
         def order(i):
             return [0, 2, 4, 1, 3, 5] if i == 0 else list(range(BANKS))
 
-        def late(i):
-            return LATE0 if i == 0 else LATE
+        def project_two(i, n):
+            two = order(i)[2 * n : 2 * n + 2]
+            for k in two:
+                do_project(i, k)
+            for k in two:
+                if k in SHARED.get(i, ()):
+                    do_empty(i, k)
+                    do_late_add(i)
+
+        def empty_two(i, n):
+            for k in reversed(order(i)[2 * n : 2 * n + 2]):
+                if k not in SHARED.get(i, ()):
+                    do_empty(i, k)
+
+        def store_two(i, n):
+            for k in reversed(order(i)[2 * n : 2 * n + 2]):
+                if k not in SHARED.get(i, ()):
+                    store(i, k)
 
         spread_scales()
+        spread_biases(0, 2)
+        spread_biases(2, 3)
         do_group_v(0, 0, 32, nc.vector.tensor_copy)
+        do_group_v(0, 32, 64)
         do_prod_early(0, 0)
         do_turn(0, (0,))
-        do_group_v(0, 32, 48)
-        do_group_v(0, 48, 64, nc.vector.tensor_copy)
-        do_group(0, 0, 1)
         do_prod_early(0, 1)
         do_turn(0, (1,))
-        spread_biases(0, 2)
-        do_group(0, 1, 2)
+        keep_biases(2, 3, nc.scalar.copy)
         do_quant_v(0)
+        do_group(0, 0, 1)
         do_quant_x(0, 0, 1)
         do_mix(0, 0)
+        do_group(0, 1, 2)
+        keep_biases(0, 2, nc.scalar.copy)
         do_prod_early(1, 0)
         do_quant_x(0, 1, 2)
-        do_prod_early(1, 1)
-        do_cast(3)
-        do_relu(0, 0)
         do_mix(0, 1)
-        spread_biases(2, 3)
+        do_prod_early(1, 1)
         do_turn(1)
-        keep_biases(0, 2, nc.vector.tensor_copy)
+        do_relu(0, 0)
         do_prod_early(2, 0)
         do_relu(0, 1)
+        do_group_v(1, 0, 8)
         do_quant_h(0, 0, 1)
         do_project(0, 0)
-        do_group(1)
-        keep_biases(2, 3, nc.scalar.copy)
         do_project(0, 2)
+        do_group(1)
+        do_cast(3)
         do_prod_early(2, 1)
         do_project(0, 4)
         do_quant_h(0, 1, 2)
         do_project(0, 1)
+        do_turn(2)
         do_empty(0, 0)
-        do_group_v(1, 48, 64, nc.vector.tensor_copy)
+        do_group_v(1, 40, 64, nc.vector.tensor_copy)
         do_quant_x(1)
         do_prod(3)
-        do_group_v(1, 0, 32)
+        do_group_v(1, 8, 24)
         do_mix(1, 0)
         do_mix(1, 1)
         do_project(0, 3)
-        do_turn(2)
         do_relu(1, 0)
         do_relu(1, 1)
-        do_group_v(1, 32, 48)
+        do_group_v(1, 24, 40)
         store(0, 0)
-        for k in order(0)[1 : BANKS - LATE0]:
-            do_empty(0, k)
-            if k == 2:
-                do_project(0, 5)
-            store(0, k)
+        do_empty(0, 2)
+        store(0, 2)
+        do_project(0, 5)
+        empty_two(0, 1)
+        store_two(0, 1)
         do_group(2, 0, 2, nc.vector.tensor_copy)
         do_cast(4)
         do_turn(3)
 
         for c in range(1, PAIRS + 1):
-            new_set = c % 2 == 1 and c + 1 < PAIRS
-            if new_set:
+            if c < PAIRS:
                 do_quant_h(c)
             if c + 1 < PAIRS:
                 do_quant_x(c + 1)
-            if new_set:
+            if c % 2 == 1 and c + 1 < PAIRS:
                 do_quant_v((c + 1) // 2)
-            elif c < PAIRS:
-                do_quant_h(c)
             if c + 3 < PAIRS:
                 do_prod(c + 3)
-            left = [(c - 1, k) for k in order(c - 1)[BANKS - late(c - 1) :]]
-            fresh = [(c, k) for k in order(c)] if c < PAIRS else []
-            free = OUT_BANKS - len(left)
-            shared = SHARED.get(c, ())
             if c + 2 < PAIRS:
                 do_group(c + 2)
             vb, vh = (c + 3) // 2, (c + 1) % 2
             if vb < SETS:
-                do_group_v(vb, 32 * vh, 32 * (vh + 1) - POOL_SHARE)
-                do_group_v_pool(vb, 32 * (vh + 1) - POOL_SHARE, 32 * (vh + 1))
-            if c + 1 < PAIRS and not new_set:
-                do_mix(c + 1, 0)
-            for i, k in fresh[:free]:
-                do_project(i, k)
-            for k in shared:
-                do_empty(c, k)
-            do_late_add(c)
+                do_group_v(vb, 32 * vh, 32 * (vh + 1))
+            if c < PAIRS:
+                project_two(c, 0)
             if c + 1 < PAIRS:
-                if new_set:
-                    do_mix(c + 1, 0)
+                do_mix(c + 1, 0)
                 do_mix(c + 1, 1)
+            empty_two(c - 1, 2)
+            store_two(c - 1, 2)
+            if c < PAIRS:
+                project_two(c, 1)
+            if c + 1 < PAIRS:
                 do_relu(c + 1, 0)
                 do_relu(c + 1, 1)
             if c + 4 < PAIRS:
                 do_cast(c + 4)
-            waiting = fresh[free:]
-            todo = left + fresh[: BANKS - late(c)]
-            for n, (i, k) in enumerate(todo):
-                mine = not (i == c and k in shared)
-                if mine:
-                    do_empty(i, k)
-                if len(waiting) == 1 and c + 3 < PAIRS and TURN_FIRST:
-                    do_turn(c + 3)
-                if waiting:
-                    do_project(*waiting.pop(0))
-                if mine:
-                    store(i, k)
-                if n == len(todo) - 2:
-                    for k in shared:
-                        store(c, k)
-            if c + 3 < PAIRS and not TURN_FIRST:
+            if c < PAIRS:
+                empty_two(c, 0)
+                project_two(c, 2)
+                store_two(c, 0)
+                empty_two(c, 1)
+                for k in SHARED.get(c, ()):
+                    store(c, k)
+                store_two(c, 1)
+            if c + 3 < PAIRS:
                 do_turn(c + 3)

@@ -18,10 +18,12 @@ COPY = mybir.ActivationFunctionType.Copy
 RELU = mybir.ActivationFunctionType.Relu
 
 P = 128
+HALF = 256
+FIRST = 2
 PAIRS = 2 * SETS
 BANKS = 6
 EARLY = 3
-SHARED = {9: (0,), 10: (0,)}
+SHARED = {c: HALF if c < 9 else FEATS for c in range(FIRST, 11)}
 
 
 def tile_perspectronencodernetwork_pa_w8_kernel(
@@ -224,7 +226,7 @@ def tile_perspectronencodernetwork_pa_w8_kernel(
             )
 
         def tiles_per_store(i, w):
-            if (i == PAIRS - 1 and w == 2) or (i in SHARED and w == 0):
+            if (i == PAIRS - 1 and w == 2) or (SHARED.get(i) == FEATS and w == 0):
                 return 1
             return 2
 
@@ -237,42 +239,41 @@ def tile_perspectronencodernetwork_pa_w8_kernel(
             if done[(i // 2, w, r0)] == n:
                 nc.sync.dma_start(out=rows[:, r0 : r0 + n, :], in_=res[(i // 2, w)][:, r0 : r0 + n, :])
 
-        def do_empty(i, k):
+        def shared_columns(i, k):
+            return slice(FEATS - SHARED.get(i, 0) if k == 0 else FEATS, FEATS)
+
+        def result(i, k):
             b, w, r = i // 2, k // 2, 2 * (i % 2) + k % 2
             if (b, w) not in res:
                 res[(b, w)] = stores.tile([P, 4, FEATS], F32, tag="y%d" % w, name="y_t")
-            if k in SHARED.get(i, ()):
-                nc.scalar.copy(out=res[(b, w)][:, r, :], in_=bank[(i, k)][:])
-            else:
-                nc.vector.tensor_tensor(out=res[(b, w)][:, r, :], in0=bank[(i, k)][:], in1=bias_sb[:, w, :], op=ADD)
+            return res[(b, w)][:, r, :]
 
-        def do_late_add(i):
-            for k in SHARED.get(i, ()):
-                b, w, r = i // 2, k // 2, 2 * (i % 2) + k % 2
-                y = res[(b, w)][:, r, :]
-                nc.gpsimd.tensor_tensor(out=y, in0=y, in1=bias_sb[:, w, :], op=ADD)
+        def do_empty(i, k):
+            own = slice(0, shared_columns(i, k).start)
+            if own.stop:
+                nc.vector.tensor_tensor(out=result(i, k)[:, own], in0=bank[(i, k)][:, own], in1=bias_sb[:, k // 2, own], op=ADD)
+
+        def do_share(i):
+            if i in SHARED:
+                cols = shared_columns(i, 0)
+                y = result(i, 0)[:, cols]
+                nc.scalar.copy(out=y, in_=bank[(i, 0)][:, cols])
+                nc.gpsimd.tensor_tensor(out=y, in0=y, in1=bias_sb[:, 0, cols], op=ADD)
 
         def order(i):
             return [0, 2, 4, 1, 3, 5] if i == 0 else list(range(BANKS))
 
         def project_two(i, n):
-            two = order(i)[2 * n : 2 * n + 2]
-            for k in two:
+            for k in order(i)[2 * n : 2 * n + 2]:
                 do_project(i, k)
-            for k in two:
-                if k in SHARED.get(i, ()):
-                    do_empty(i, k)
-                    do_late_add(i)
 
         def empty_two(i, n):
             for k in reversed(order(i)[2 * n : 2 * n + 2]):
-                if k not in SHARED.get(i, ()):
-                    do_empty(i, k)
+                do_empty(i, k)
 
         def store_two(i, n):
             for k in reversed(order(i)[2 * n : 2 * n + 2]):
-                if k not in SHARED.get(i, ()):
-                    store(i, k)
+                store(i, k)
 
         spread_scales()
         spread_biases(0, 2)
@@ -339,13 +340,12 @@ def tile_perspectronencodernetwork_pa_w8_kernel(
                 do_quant_v((c + 1) // 2)
             if c + 3 < PAIRS:
                 do_prod(c + 3)
-            if c + 2 < PAIRS:
-                do_group(c + 2)
             vb, vh = (c + 3) // 2, (c + 1) % 2
             if vb < SETS:
                 do_group_v(vb, 32 * vh, 32 * (vh + 1))
             if c < PAIRS:
                 project_two(c, 0)
+                do_share(c)
             if c + 1 < PAIRS:
                 do_mix(c + 1, 0)
                 do_mix(c + 1, 1)
@@ -356,15 +356,20 @@ def tile_perspectronencodernetwork_pa_w8_kernel(
             if c + 1 < PAIRS:
                 do_relu(c + 1, 0)
                 do_relu(c + 1, 1)
+            if c + 2 < PAIRS:
+                do_group(c + 2)
             if c + 4 < PAIRS:
                 do_cast(c + 4)
             if c < PAIRS:
                 empty_two(c, 0)
                 project_two(c, 2)
-                store_two(c, 0)
+                if c in SHARED:
+                    store(c, 1)
+                else:
+                    store_two(c, 0)
                 empty_two(c, 1)
-                for k in SHARED.get(c, ()):
-                    store(c, k)
                 store_two(c, 1)
+                if c in SHARED:
+                    store(c, 0)
             if c + 3 < PAIRS:
                 do_turn(c + 3)

@@ -18,12 +18,10 @@ COPY = mybir.ActivationFunctionType.Copy
 RELU = mybir.ActivationFunctionType.Relu
 
 P = 128
-HALF = 256
-FIRST = 2
 PAIRS = 2 * SETS
 BANKS = 6
 EARLY = 3
-SHARED = {c: HALF if c < 9 else FEATS for c in range(FIRST, 11)}
+SHARED = {c: 192 if c < 9 else 384 for c in range(2, 11)}
 
 
 def tile_perspectronencodernetwork_pa_w8_kernel(
@@ -86,12 +84,13 @@ def tile_perspectronencodernetwork_pa_w8_kernel(
         load_v(1, 2)
         load_wscales(0)
         load_words(0)
-        load_wscales(1)
         load_words(1)
-        load_wscales(2)
-        load_words(2)
         load_codes(2, 3)
-        load_v(2, 4)
+        load_wscales(1)
+        load_words(2)
+        load_v(2, 3)
+        load_wscales(2)
+        load_v(3, 4)
         load_codes(3, 6)
         load_v(4, 6)
 
@@ -211,10 +210,14 @@ def tile_perspectronencodernetwork_pa_w8_kernel(
                 in_=hg[i][:, r0:r1].rearrange("p r q t -> p (r q t)"),
             )
 
+        places = [0, 1, 2, 3]
+
         def do_project(i, k):
             w, r = k // 2, k % 2
-            n = len(bank)
-            o = ps_out.tile([P, FEATS], F32, tag="o%d" % (2 * (n // 2 % 2) + (n + n // 4) % 2), name="o_t")
+            n = len(places)
+            swap = i == 0 or k < 4
+            places.append(places[n - 4 + (1 - 2 * (n % 2) if swap else 0)])
+            o = ps_out.tile([P, FEATS], F32, tag="o%d" % places[n], name="o_t")
             bank[(i, k)] = o
             nc.tensor.matmul_mx(
                 out=o[:],
@@ -225,19 +228,12 @@ def tile_perspectronencodernetwork_pa_w8_kernel(
                 start=True, stop=True,
             )
 
-        def tiles_per_store(i, w):
-            if (i == PAIRS - 1 and w == 2) or (SHARED.get(i) == FEATS and w == 0):
-                return 1
-            return 2
-
         def store(i, k):
-            w, r = k // 2, 2 * (i % 2) + k % 2
-            rows = outs[w][i // 2].rearrange("(p r) n -> p r n", r=4)
-            n = tiles_per_store(i, w)
-            r0 = r // n * n
-            done[(i // 2, w, r0)] = done.get((i // 2, w, r0), 0) + 1
-            if done[(i // 2, w, r0)] == n:
-                nc.sync.dma_start(out=rows[:, r0 : r0 + n, :], in_=res[(i // 2, w)][:, r0 : r0 + n, :])
+            w, h = k // 2, 2 * (i % 2)
+            done[(i, w)] = done.get((i, w), 0) + 1
+            if done[(i, w)] == 2:
+                rows = outs[w][i // 2].rearrange("(p r) n -> p r n", r=4)
+                nc.sync.dma_start(out=rows[:, h : h + 2, :], in_=res[(i // 2, w)][:, h : h + 2, :])
 
         def shared_columns(i, k):
             return slice(FEATS - SHARED.get(i, 0) if k == 0 else FEATS, FEATS)
@@ -309,14 +305,14 @@ def tile_perspectronencodernetwork_pa_w8_kernel(
         do_project(0, 4)
         do_quant_h(0, 1, 2)
         do_project(0, 1)
-        do_turn(2)
-        do_empty(0, 0)
         do_group_v(1, 40, 64, nc.vector.tensor_copy)
         do_quant_x(1)
         do_prod(3)
         do_group_v(1, 8, 24)
         do_mix(1, 0)
         do_mix(1, 1)
+        do_empty(0, 0)
+        do_turn(2)
         do_project(0, 3)
         do_relu(1, 0)
         do_relu(1, 1)
@@ -368,8 +364,8 @@ def tile_perspectronencodernetwork_pa_w8_kernel(
                 else:
                     store_two(c, 0)
                 empty_two(c, 1)
-                store_two(c, 1)
                 if c in SHARED:
                     store(c, 0)
+                store_two(c, 1)
             if c + 3 < PAIRS:
                 do_turn(c + 3)

@@ -21,7 +21,7 @@ P = 128
 PAIRS = 2 * SETS
 BANKS = 6
 EARLY = 3
-SHARED = {c: 192 if c < 9 else 384 for c in range(2, 11)}
+SHARED = {c: 192 if c < 9 else 384 for c in range(1, 11)}
 
 
 def tile_perspectronencodernetwork_pa_w8_kernel(
@@ -44,13 +44,16 @@ def tile_perspectronencodernetwork_pa_w8_kernel(
         ps_x = ctx.enter_context(tc.psum_pool(name="ps_x", bufs=2))
         ctx.enter_context(tc.manual_schedule())
 
+        bias_rows = keep.tile([P, 3 * FEATS], BF16, name="bias_rows")
+        nc.vector.memset(bias_rows[:].bitcast(F32), 0.0)
+        ones = keep.tile([P, P], BF16, name="ones")
+        nc.vector.memset(ones[:], 1.0)
         wscale_sb = keep.tile([P, 3 * FEATS], U8, align_bytes=64, name="wscale_sb")
         nc.vector.memset(wscale_sb[:].bitcast(I32), 0)
         ident = keep.tile([P, P], F32, name="ident")
         make_identity(nc, ident[:])
 
         scale_col = keep.tile([P, 4], F32, name="scale_col")
-        bias_col = keep.tile([P, 3, 16], BF16, name="bias_col")
         codes_in = keep.tile([P, SETS, 4, POINTS], U8, align_bytes=64, name="codes_in")
         vraw = [stores.tile([P, 2, 4, FEATS], BF16, tag="y%d" % n, name="vraw") for n in range(3)]
         w_sb = keep.tile([P, 3, 4 * FEATS], U8, align_bytes=64, name="w_sb")
@@ -72,14 +75,14 @@ def tile_perspectronencodernetwork_pa_w8_kernel(
                 )
 
         def load_bias(w):
-            nc.scalar.dma_start(out=bias_col[:, w, 0:4], in_=biases_in[w].rearrange("(p t) -> p t", t=4))
+            nc.sync.dma_start(out=bias_rows[0:1, FEATS * w : FEATS * (w + 1)], in_=biases_in[w].rearrange("(o n) -> o n", o=1))
 
         nc.sync.dma_start(out=scale_col[:], in_=attn1_scale.rearrange("a b (p t) -> p (a b t)", t=4))
         load_v(0, 1)
-        load_codes(0, 1)
         load_bias(0)
         load_bias(1)
         load_bias(2)
+        load_codes(0, 1)
         load_codes(1, 2)
         load_v(1, 2)
         load_wscales(0)
@@ -106,18 +109,13 @@ def tile_perspectronencodernetwork_pa_w8_kernel(
         bias_ps = {}
 
         def spread_biases(w0, w1):
-            ps = ps_out.tile([P, 2, 2, P], F32, tag="o%d" % w1, name="bias_ps")
+            ps = ps_out.tile([P, 2, FEATS], BF16, tag="o%d" % w1, name="bias_ps")
             bias_ps[w0] = ps
             for w in range(w0, w1):
-                words = bias_col[:, w, :].bitcast(F32)
-                for u in range(2):
-                    nc.tensor.transpose(ps[:, w - w0, u, :], words[:, u : u + 1].to_broadcast([P, P]), ident[:])
+                nc.tensor.matmul(ps[:, w - w0, :], lhsT=ones[:], rhs=bias_rows[:, FEATS * w : FEATS * (w + 1)], start=True, stop=True)
 
         def keep_biases(w0, w1, engine):
-            engine(
-                out=bias_sb[:, w0:w1, :].bitcast(F32).rearrange("q w (p u) -> q w p u", u=2),
-                in_=bias_ps[w0][:, : w1 - w0].rearrange("q w u p -> q w p u"),
-            )
+            engine(out=bias_sb[:, w0:w1, :], in_=bias_ps[w0][:, : w1 - w0, :])
 
         ring = [keep.tile([P, 2, POINTS], BF16, align_bytes=64, name="ring%d" % n) for n in range(3)]
         first = [keep.tile([P, 2, POINTS], BF16, align_bytes=64, name="first%d" % n) for n in range(EARLY)]
@@ -257,7 +255,7 @@ def tile_perspectronencodernetwork_pa_w8_kernel(
                 nc.gpsimd.tensor_tensor(out=y, in0=y, in1=bias_sb[:, 0, cols], op=ADD)
 
         def order(i):
-            return [0, 2, 4, 1, 3, 5] if i == 0 else list(range(BANKS))
+            return [0, 2, 1, 3, 4, 5] if i == 0 else list(range(BANKS))
 
         def project_two(i, n):
             for k in order(i)[2 * n : 2 * n + 2]:
@@ -273,20 +271,20 @@ def tile_perspectronencodernetwork_pa_w8_kernel(
 
         spread_scales()
         spread_biases(0, 2)
-        spread_biases(2, 3)
         do_group_v(0, 0, 32, nc.vector.tensor_copy)
         do_group_v(0, 32, 64)
         do_prod_early(0, 0)
         do_turn(0, (0,))
         do_prod_early(0, 1)
         do_turn(0, (1,))
-        keep_biases(2, 3, nc.scalar.copy)
+        spread_biases(2, 3)
         do_quant_v(0)
         do_group(0, 0, 1)
         do_quant_x(0, 0, 1)
         do_mix(0, 0)
         do_group(0, 1, 2)
         keep_biases(0, 2, nc.scalar.copy)
+        keep_biases(2, 3, nc.scalar.copy)
         do_prod_early(1, 0)
         do_quant_x(0, 1, 2)
         do_mix(0, 1)
@@ -302,10 +300,10 @@ def tile_perspectronencodernetwork_pa_w8_kernel(
         do_group(1)
         do_cast(3)
         do_prod_early(2, 1)
-        do_project(0, 4)
         do_quant_h(0, 1, 2)
         do_project(0, 1)
-        do_group_v(1, 40, 64, nc.vector.tensor_copy)
+        do_project(0, 3)
+        do_group_v(1, 32, 64, nc.vector.tensor_copy)
         do_quant_x(1)
         do_prod(3)
         do_group_v(1, 8, 24)
@@ -313,16 +311,18 @@ def tile_perspectronencodernetwork_pa_w8_kernel(
         do_mix(1, 1)
         do_empty(0, 0)
         do_turn(2)
-        do_project(0, 3)
+        do_project(0, 4)
         do_relu(1, 0)
         do_relu(1, 1)
-        do_group_v(1, 24, 40)
+        do_group_v(1, 24, 32)
         store(0, 0)
         do_empty(0, 2)
         store(0, 2)
         do_project(0, 5)
-        empty_two(0, 1)
-        store_two(0, 1)
+        do_empty(0, 1)
+        store(0, 1)
+        do_empty(0, 3)
+        store(0, 3)
         do_group(2, 0, 2, nc.vector.tensor_copy)
         do_cast(4)
         do_turn(3)

@@ -21,7 +21,7 @@ P = 128
 PAIRS = 2 * SETS
 BANKS = 6
 EARLY = 3
-SHARED = {c: 192 if c < 9 else 384 for c in range(1, 11)}
+SHARED = {c: 224 if c < 9 else 384 for c in range(1, 11)}
 
 
 def tile_perspectronencodernetwork_pa_w8_kernel(
@@ -120,15 +120,24 @@ def tile_perspectronencodernetwork_pa_w8_kernel(
         ring = [keep.tile([P, 2, POINTS], BF16, align_bytes=64, name="ring%d" % n) for n in range(3)]
         first = [keep.tile([P, 2, POINTS], BF16, align_bytes=64, name="first%d" % n) for n in range(EARLY)]
 
+        relu_ring = [keep.tile([P, 2, P, 4], BF16, align_bytes=64, name="relu_ring%d" % n) for n in range(3)]
+
+        def hg(i):
+            return relu_ring[i % 3][:]
+
         def prod(i):
-            return first[i] if i < EARLY else ring[(2 * i - 1) % 3]
+            if i < EARLY:
+                return first[i][:]
+            if i % 2 == 1 and i > EARLY:
+                return hg(i - 3).rearrange("p r q t -> p r (q t)")
+            return ring[(2 * i - 1) % 3][:]
 
         def xg(i):
             return ring[(2 * i) % 3]
 
         cast, xt, xq, xs = {}, {}, {}, {}
         vg, vq, vs = {}, {}, {}
-        hps, hg, hq, hs = {}, {}, {}, {}
+        hps, hq, hs = {}, {}, {}
         bank, res, done = {}, {}, {}
 
         def do_cast(i):
@@ -141,7 +150,7 @@ def tile_perspectronencodernetwork_pa_w8_kernel(
             nc.vector.tensor_tensor(out=prod(i)[:, r, :], in0=codes_in[:, i // 2, 2 * (i % 2) + r, :].bitcast(FP8), in1=scale_sb[:], op=MULT)
 
         def do_prod(i):
-            nc.gpsimd.tensor_tensor(out=prod(i)[:], in0=cast[i][:], in1=scale_sb[:].unsqueeze(1).to_broadcast([P, 2, POINTS]), op=MULT)
+            nc.gpsimd.tensor_tensor(out=prod(i), in0=cast[i][:], in1=scale_sb[:].unsqueeze(1).to_broadcast([P, 2, POINTS]), op=MULT)
 
         def do_turn(i, tiles=(0, 1)):
             x = ps_x.tile([P, 2, 2, P], F32, tag="x", name="xt_t")
@@ -195,9 +204,7 @@ def tile_perspectronencodernetwork_pa_w8_kernel(
                 )
 
         def do_relu(i, r):
-            if r == 0:
-                hg[i] = work.tile([P, 2, P, 4], BF16, tag="hg", name="hg_t", align_bytes=64)
-            nc.scalar.activation(out=hg[i][:, r], in_=hps[(i, r)][:].rearrange("p t q -> p q t"), func=RELU)
+            nc.scalar.activation(out=hg(i)[:, r], in_=hps[(i, r)][:].rearrange("p t q -> p q t"), func=RELU)
 
         def do_quant_h(i, r0=0, r1=2):
             if r0 == 0:
@@ -205,7 +212,7 @@ def tile_perspectronencodernetwork_pa_w8_kernel(
                 hs[i] = work.tile([P, 2 * P], U8, tag="hs", name="hs_t", align_bytes=64)
             nc.vector.quantize_mx(
                 out=hq[i][:, 512 * r0 : 512 * r1].bitcast(FP8X4), scales=hs[i][:, P * r0 : P * r1],
-                in_=hg[i][:, r0:r1].rearrange("p r q t -> p (r q t)"),
+                in_=hg(i)[:, r0:r1].rearrange("p r q t -> p (r q t)"),
             )
 
         places = [0, 1, 2, 3]
@@ -280,30 +287,30 @@ def tile_perspectronencodernetwork_pa_w8_kernel(
         spread_biases(2, 3)
         do_quant_v(0)
         do_group(0, 0, 1)
+        do_prod_early(1, 0)
         do_quant_x(0, 0, 1)
         do_mix(0, 0)
         do_group(0, 1, 2)
         keep_biases(0, 2, nc.scalar.copy)
         keep_biases(2, 3, nc.scalar.copy)
-        do_prod_early(1, 0)
+        do_prod_early(1, 1)
         do_quant_x(0, 1, 2)
         do_mix(0, 1)
-        do_prod_early(1, 1)
         do_turn(1)
+        do_group_v(1, 0, 8)
         do_relu(0, 0)
         do_prod_early(2, 0)
+        do_prod_early(2, 1)
         do_relu(0, 1)
-        do_group_v(1, 0, 8)
         do_quant_h(0, 0, 1)
         do_project(0, 0)
         do_project(0, 2)
         do_group(1)
         do_cast(3)
-        do_prod_early(2, 1)
+        do_group_v(1, 32, 64, nc.vector.tensor_copy)
         do_quant_h(0, 1, 2)
         do_project(0, 1)
         do_project(0, 3)
-        do_group_v(1, 32, 64, nc.vector.tensor_copy)
         do_quant_x(1)
         do_prod(3)
         do_group_v(1, 8, 24)

@@ -13,6 +13,7 @@ I32 = mybir.dt.int32
 FP8 = mybir.dt.float8_e4m3fn
 FP8X4 = mybir.dt.float8_e4m3fn_x4
 ADD = mybir.AluOpType.add
+MAX = mybir.AluOpType.max
 MULT = mybir.AluOpType.mult
 COPY = mybir.ActivationFunctionType.Copy
 RELU = mybir.ActivationFunctionType.Relu
@@ -21,7 +22,15 @@ P = 128
 PAIRS = 2 * SETS
 BANKS = 6
 EARLY = 3
-SHARED = {c: 224 if c < 9 else 384 for c in range(1, 11)}
+LEAD = 4
+BUSY = PAIRS - LEAD
+SHARE = 224
+SHARED = {
+    **{(c, 2): SHARE for c in range(1, BUSY)},
+    **{(c, 2): FEATS for c in range(BUSY, PAIRS - 1)},
+    (BUSY, 5): 256,
+    (PAIRS - 1, 2): 384,
+}
 
 
 def tile_perspectronencodernetwork_pa_w8_kernel(
@@ -77,13 +86,13 @@ def tile_perspectronencodernetwork_pa_w8_kernel(
         def load_bias(w):
             nc.sync.dma_start(out=bias_rows[0:1, FEATS * w : FEATS * (w + 1)], in_=biases_in[w].rearrange("(o n) -> o n", o=1))
 
-        nc.sync.dma_start(out=scale_col[:], in_=attn1_scale.rearrange("a b (p t) -> p (a b t)", t=4))
         load_v(0, 1)
+        load_codes(0, 1)
+        nc.sync.dma_start(out=scale_col[:], in_=attn1_scale.rearrange("a b (p t) -> p (a b t)", t=4))
+        load_codes(1, 2)
         load_bias(0)
         load_bias(1)
         load_bias(2)
-        load_codes(0, 1)
-        load_codes(1, 2)
         load_v(1, 2)
         load_wscales(0)
         load_words(0)
@@ -93,23 +102,25 @@ def tile_perspectronencodernetwork_pa_w8_kernel(
         load_words(2)
         load_v(2, 3)
         load_wscales(2)
-        load_v(3, 4)
         load_codes(3, 6)
+        load_v(3, 4)
         load_v(4, 6)
 
         scale_sb = keep.tile([P, POINTS], F32, name="scale_sb")
+        scale_ps = ps_out.tile([P, 4, P], F32, tag="o0", name="scale_ps")
         bias_sb = keep.tile([P, 3, FEATS], BF16, name="bias_sb")
 
         def spread_scales():
-            scale_ps = ps_x.tile([P, 4, P], F32, tag="x", name="scale_ps")
             for t in range(4):
                 nc.tensor.transpose(scale_ps[:, t, :], scale_col[:, t : t + 1].to_broadcast([P, P]), ident[:])
+
+        def keep_scales():
             nc.scalar.activation(out=scale_sb[:].rearrange("q (p t) -> q p t", t=4), in_=scale_ps[:].rearrange("q t p -> q p t"), func=COPY)
 
         bias_ps = {}
 
         def spread_biases(w0, w1):
-            ps = ps_out.tile([P, 2, FEATS], BF16, tag="o%d" % w1, name="bias_ps")
+            ps = ps_out.tile([P, 2, FEATS], BF16, tag="o%d" % (2 + w0), name="bias_ps")
             bias_ps[w0] = ps
             for w in range(w0, w1):
                 nc.tensor.matmul(ps[:, w - w0, :], lhsT=ones[:], rhs=bias_rows[:, FEATS * w : FEATS * (w + 1)], start=True, stop=True)
@@ -117,8 +128,7 @@ def tile_perspectronencodernetwork_pa_w8_kernel(
         def keep_biases(w0, w1, engine):
             engine(out=bias_sb[:, w0:w1, :], in_=bias_ps[w0][:, : w1 - w0, :])
 
-        ring = [keep.tile([P, 2, POINTS], BF16, align_bytes=64, name="ring%d" % n) for n in range(3)]
-        first = [keep.tile([P, 2, POINTS], BF16, align_bytes=64, name="first%d" % n) for n in range(EARLY)]
+        ring = [keep.tile([P, 2, POINTS], BF16, align_bytes=64, name="ring%d" % n) for n in range(4)]
 
         relu_ring = [keep.tile([P, 2, P, 4], BF16, align_bytes=64, name="relu_ring%d" % n) for n in range(3)]
 
@@ -127,33 +137,43 @@ def tile_perspectronencodernetwork_pa_w8_kernel(
 
         def prod(i):
             if i < EARLY:
-                return first[i][:]
-            if i % 2 == 1 and i > EARLY:
-                return hg(i - 3).rearrange("p r q t -> p r (q t)")
-            return ring[(2 * i - 1) % 3][:]
+                return cast[i][:]
+            if i == EARLY:
+                return xg(0)[:]
+            if i % 2 == 0 and i > LEAD:
+                return hg(i - LEAD).rearrange("p r q t -> p r (q t)")
+            return xg(i - LEAD + 1)[:]
 
         def xg(i):
-            return ring[(2 * i) % 3]
+            return ring[i % 3] if i != EARLY else ring[3]
 
         cast, xt, xq, xs = {}, {}, {}, {}
         vg, vq, vs = {}, {}, {}
         hps, hq, hs = {}, {}, {}
         bank, res, done = {}, {}, {}
 
-        def do_cast(i):
-            c = work.tile([P, 2, POINTS], BF16, tag="cast", name="cast_t")
-            cast[i] = c
+        def do_cast(i, r0=0, r1=2):
+            if r0 == 0:
+                cast[i] = work.tile([P, 2, POINTS], BF16, tag="cast", name="cast_t")
             h = 2 * (i % 2)
-            nc.scalar.copy(out=c[:], in_=codes_in[:, i // 2, h : h + 2, :].bitcast(FP8))
+            nc.scalar.copy(out=cast[i][:, r0:r1, :], in_=codes_in[:, i // 2, h + r0 : h + r1, :].bitcast(FP8))
 
-        def do_prod_early(i, r):
-            nc.vector.tensor_tensor(out=prod(i)[:, r, :], in0=codes_in[:, i // 2, 2 * (i % 2) + r, :].bitcast(FP8), in1=scale_sb[:], op=MULT)
+        def do_scale_out(i, r):
+            nc.vector.tensor_tensor(
+                out=xg(i)[:, r, :].rearrange("p (q u e) -> p q u e", u=2, e=2),
+                in0=xt[(i, r)][:, r].bitcast(BF16).rearrange("p u (q e) -> p q u e", e=2),
+                in1=scale_col[:].rearrange("p (u e) -> p u e", e=2).unsqueeze(1).to_broadcast([P, P, 2, 2]),
+                op=MULT,
+            )
 
         def do_prod(i):
             nc.gpsimd.tensor_tensor(out=prod(i), in0=cast[i][:], in1=scale_sb[:].unsqueeze(1).to_broadcast([P, 2, POINTS]), op=MULT)
 
-        def do_turn(i, tiles=(0, 1)):
-            x = ps_x.tile([P, 2, 2, P], F32, tag="x", name="xt_t")
+        def do_turn(i, tiles=(0, 1), spare=False):
+            if spare:
+                x = ps_out.tile([P, 2, 2, P], F32, tag="o1", name="xt_t")
+            else:
+                x = ps_x.tile([P, 2, 2, P], F32, tag="x", name="xt_t")
             for r in tiles:
                 xt[(i, r)] = x
             for r in tiles:
@@ -206,6 +226,9 @@ def tile_perspectronencodernetwork_pa_w8_kernel(
         def do_relu(i, r):
             nc.scalar.activation(out=hg(i)[:, r], in_=hps[(i, r)][:].rearrange("p t q -> p q t"), func=RELU)
 
+        def do_relu_vector(i, r):
+            nc.vector.tensor_scalar(out=hg(i)[:, r], in0=hps[(i, r)][:].rearrange("p t q -> p q t"), scalar1=0.0, scalar2=None, op0=MAX)
+
         def do_quant_h(i, r0=0, r1=2):
             if r0 == 0:
                 hq[i] = work.tile([P, 4 * 2 * P], U8, tag="hq", name="hq_t", align_bytes=64)
@@ -215,14 +238,14 @@ def tile_perspectronencodernetwork_pa_w8_kernel(
                 in_=hg(i)[:, r0:r1].rearrange("p r q t -> p (r q t)"),
             )
 
-        places = [0, 1, 2, 3]
+        free_banks = [1, 0, 3, 2]
+        place = {}
 
         def do_project(i, k):
             w, r = k // 2, k % 2
-            n = len(places)
-            swap = i == 0 or k < 4
-            places.append(places[n - 4 + (1 - 2 * (n % 2) if swap else 0)])
-            o = ps_out.tile([P, FEATS], F32, tag="o%d" % places[n], name="o_t")
+            place[(i, k)] = free_banks[0]
+            free_banks.remove(place[(i, k)])
+            o = ps_out.tile([P, FEATS], F32, tag="o%d" % place[(i, k)], name="o_t")
             bank[(i, k)] = o
             nc.tensor.matmul_mx(
                 out=o[:],
@@ -241,7 +264,7 @@ def tile_perspectronencodernetwork_pa_w8_kernel(
                 nc.sync.dma_start(out=rows[:, h : h + 2, :], in_=res[(i // 2, w)][:, h : h + 2, :])
 
         def shared_columns(i, k):
-            return slice(FEATS - SHARED.get(i, 0) if k == 0 else FEATS, FEATS)
+            return slice(FEATS - SHARED.get((i, k), 0), FEATS)
 
         def result(i, k):
             b, w, r = i // 2, k // 2, 2 * (i % 2) + k % 2
@@ -253,85 +276,73 @@ def tile_perspectronencodernetwork_pa_w8_kernel(
             own = slice(0, shared_columns(i, k).start)
             if own.stop:
                 nc.vector.tensor_tensor(out=result(i, k)[:, own], in0=bank[(i, k)][:, own], in1=bias_sb[:, k // 2, own], op=ADD)
+            free_banks.append(place[(i, k)])
 
-        def do_share(i):
-            if i in SHARED:
-                cols = shared_columns(i, 0)
-                y = result(i, 0)[:, cols]
-                nc.scalar.copy(out=y, in_=bank[(i, 0)][:, cols])
-                nc.gpsimd.tensor_tensor(out=y, in0=y, in1=bias_sb[:, 0, cols], op=ADD)
+        def do_share(i, k):
+            if SHARED.get((i, k), 0):
+                cols = shared_columns(i, k)
+                y = result(i, k)[:, cols]
+                nc.scalar.copy(out=y, in_=bank[(i, k)][:, cols])
+                nc.gpsimd.tensor_tensor(out=y, in0=y, in1=bias_sb[:, k // 2, cols], op=ADD)
 
-        def order(i):
-            return [0, 2, 1, 3, 4, 5] if i == 0 else list(range(BANKS))
-
-        def project_two(i, n):
-            for k in order(i)[2 * n : 2 * n + 2]:
-                do_project(i, k)
-
-        def empty_two(i, n):
-            for k in reversed(order(i)[2 * n : 2 * n + 2]):
-                do_empty(i, k)
-
-        def store_two(i, n):
-            for k in reversed(order(i)[2 * n : 2 * n + 2]):
-                store(i, k)
-
-        spread_scales()
-        spread_biases(0, 2)
-        do_group_v(0, 0, 32, nc.vector.tensor_copy)
-        do_group_v(0, 32, 64)
-        do_prod_early(0, 0)
+        do_group_v(0, 16, 64, nc.vector.tensor_copy)
+        do_group_v(0, 0, 16)
+        do_cast(0, 0, 1)
         do_turn(0, (0,))
-        do_prod_early(0, 1)
+        do_cast(0, 1, 2)
         do_turn(0, (1,))
-        spread_biases(2, 3)
+        spread_scales()
+        do_cast(1)
+        do_turn(1, (0, 1), True)
         do_quant_v(0)
-        do_group(0, 0, 1)
-        do_prod_early(1, 0)
-        do_quant_x(0, 0, 1)
-        do_mix(0, 0)
-        do_group(0, 1, 2)
-        keep_biases(0, 2, nc.scalar.copy)
-        keep_biases(2, 3, nc.scalar.copy)
-        do_prod_early(1, 1)
-        do_quant_x(0, 1, 2)
-        do_mix(0, 1)
-        do_turn(1)
-        do_group_v(1, 0, 8)
-        do_relu(0, 0)
-        do_prod_early(2, 0)
-        do_prod_early(2, 1)
-        do_relu(0, 1)
-        do_quant_h(0, 0, 1)
-        do_project(0, 0)
-        do_project(0, 2)
-        do_group(1)
-        do_cast(3)
-        do_group_v(1, 32, 64, nc.vector.tensor_copy)
-        do_quant_h(0, 1, 2)
-        do_project(0, 1)
-        do_project(0, 3)
-        do_quant_x(1)
-        do_prod(3)
-        do_group_v(1, 8, 24)
-        do_mix(1, 0)
-        do_mix(1, 1)
-        do_empty(0, 0)
+        do_scale_out(0, 0)
+        do_scale_out(0, 1)
+        do_cast(2)
         do_turn(2)
-        do_project(0, 4)
+        do_cast(3)
+        keep_scales()
+        do_quant_x(0, 0, 1)
+        do_quant_x(0, 1, 2)
+        do_prod(3)
+        do_mix(0, 0)
+        do_mix(0, 1)
+        spread_biases(0, 1)
+        spread_biases(1, 3)
+        do_group_v(1, 0, 16)
+        do_scale_out(1, 0)
+        do_scale_out(1, 1)
+        do_scale_out(2, 0)
+        do_scale_out(2, 1)
+        keep_biases(0, 1, nc.vector.tensor_copy)
+        do_relu(0, 0)
+        do_relu(0, 1)
+        do_cast(4)
+        do_quant_h(0)
+        do_quant_x(1)
+        do_group_v(1, 48, 64, nc.vector.tensor_copy)
+        do_prod(4)
+        keep_biases(1, 3, nc.scalar.copy)
+        do_project(0, 0)
+        do_project(0, 1)
+        do_mix(1, 0)
+        do_project(0, 2)
+        do_mix(1, 1)
+        do_project(0, 3)
+        do_group_v(1, 16, 40)
+        do_empty(0, 0)
         do_relu(1, 0)
         do_relu(1, 1)
-        do_group_v(1, 24, 32)
         store(0, 0)
+        do_empty(0, 1)
+        store(0, 1)
+        do_project(0, 4)
         do_empty(0, 2)
         store(0, 2)
         do_project(0, 5)
-        do_empty(0, 1)
-        store(0, 1)
         do_empty(0, 3)
         store(0, 3)
-        do_group(2, 0, 2, nc.vector.tensor_copy)
-        do_cast(4)
+        do_group_v(1, 40, 48)
+        do_cast(5)
         do_turn(3)
 
         for c in range(1, PAIRS + 1):
@@ -341,38 +352,42 @@ def tile_perspectronencodernetwork_pa_w8_kernel(
                 do_quant_x(c + 1)
             if c % 2 == 1 and c + 1 < PAIRS:
                 do_quant_v((c + 1) // 2)
-            if c + 3 < PAIRS:
-                do_prod(c + 3)
+            if c + LEAD < PAIRS:
+                do_prod(c + LEAD)
+            do_share(c - 1, 5)
             vb, vh = (c + 3) // 2, (c + 1) % 2
             if vb < SETS:
                 do_group_v(vb, 32 * vh, 32 * (vh + 1))
+            first, second = (2, 0) if (c, 2) in SHARED else (0, 1)
+            third = 3 - first - second
             if c < PAIRS:
-                project_two(c, 0)
-                do_share(c)
+                do_project(c, first)
+                do_project(c, second)
+                do_share(c, 2)
             if c + 1 < PAIRS:
                 do_mix(c + 1, 0)
                 do_mix(c + 1, 1)
-            empty_two(c - 1, 2)
-            store_two(c - 1, 2)
+            for k in (5, 4):
+                do_empty(c - 1, k)
+                store(c - 1, k)
             if c < PAIRS:
-                project_two(c, 1)
+                do_project(c, third)
+                do_project(c, 3)
             if c + 1 < PAIRS:
                 do_relu(c + 1, 0)
                 do_relu(c + 1, 1)
-            if c + 2 < PAIRS:
+            if EARLY <= c + 2 < PAIRS:
                 do_group(c + 2)
-            if c + 4 < PAIRS:
-                do_cast(c + 4)
+            if c + LEAD + 1 < PAIRS:
+                do_cast(c + LEAD + 1)
             if c < PAIRS:
-                empty_two(c, 0)
-                project_two(c, 2)
-                if c in SHARED:
-                    store(c, 1)
-                else:
-                    store_two(c, 0)
-                empty_two(c, 1)
-                if c in SHARED:
-                    store(c, 0)
-                store_two(c, 1)
+                for k in (0, 1):
+                    do_empty(c, k)
+                    store(c, k)
+                do_project(c, 4)
+                do_project(c, 5)
+                for k in (2, 3):
+                    do_empty(c, k)
+                    store(c, k)
             if c + 3 < PAIRS:
                 do_turn(c + 3)

@@ -199,8 +199,8 @@ def tile_perspectronencodernetwork_pa_w8_kernel(
         def do_group_v(b, n0, n1, engine=None):
             if b not in vg:
                 vg[b] = work.tile([P, 4, P, 4], BF16, tag="vg", name="vg_t", align_bytes=64)
-            src = vraw[b // 2][:, b % 2].rearrange("p j (n m t) -> p n t m j", m=2, t=4)[:, n0:n1]
-            dst = vg[b][:].rearrange("p t (n m) j -> p n t m j", m=2)[:, n0:n1]
+            src = vraw[b // 2][:, b % 2].rearrange("p j (n m t) -> p n j m t", m=2, t=4)[:, n0:n1]
+            dst = vg[b][:].rearrange("p t (n m) j -> p n j m t", m=2)[:, n0:n1]
             (engine or nc.scalar.copy)(out=dst, in_=src)
 
 

@@ -13,7 +13,6 @@ I32 = mybir.dt.int32
 FP8 = mybir.dt.float8_e4m3fn
 FP8X4 = mybir.dt.float8_e4m3fn_x4
 ADD = mybir.AluOpType.add
-MAX = mybir.AluOpType.max
 MULT = mybir.AluOpType.mult
 COPY = mybir.ActivationFunctionType.Copy
 RELU = mybir.ActivationFunctionType.Relu
@@ -55,7 +54,7 @@ def tile_perspectronencodernetwork_pa_w8_kernel(
 
         bias_rows = keep.tile([P, 3 * FEATS], BF16, name="bias_rows")
         nc.vector.memset(bias_rows[:].bitcast(F32), 0.0)
-        ones = keep.tile([P, P], BF16, name="ones")
+        ones = keep.tile([P, FEATS], BF16, name="ones")
         nc.vector.memset(ones[:], 1.0)
         wscale_sb = keep.tile([P, 3 * FEATS], U8, align_bytes=64, name="wscale_sb")
         nc.vector.memset(wscale_sb[:].bitcast(I32), 0)
@@ -87,12 +86,12 @@ def tile_perspectronencodernetwork_pa_w8_kernel(
             nc.sync.dma_start(out=bias_rows[0:1, FEATS * w : FEATS * (w + 1)], in_=biases_in[w].rearrange("(o n) -> o n", o=1))
 
         load_v(0, 1)
-        load_codes(0, 1)
-        nc.sync.dma_start(out=scale_col[:], in_=attn1_scale.rearrange("a b (p t) -> p (a b t)", t=4))
-        load_codes(1, 2)
         load_bias(0)
         load_bias(1)
         load_bias(2)
+        load_codes(0, 1)
+        nc.sync.dma_start(out=scale_col[:], in_=attn1_scale.rearrange("a b (p t) -> p (a b t)", t=4))
+        load_codes(1, 2)
         load_v(1, 2)
         load_wscales(0)
         load_words(0)
@@ -120,10 +119,15 @@ def tile_perspectronencodernetwork_pa_w8_kernel(
         bias_ps = {}
 
         def spread_biases(w0, w1):
-            ps = ps_out.tile([P, 2, FEATS], BF16, tag="o%d" % (2 + w0), name="bias_ps")
+            ps = ps_out.tile([P, 2, FEATS], BF16, tag="o%d" % (2 + w0 // 2), name="bias_ps")
             bias_ps[w0] = ps
             for w in range(w0, w1):
-                nc.tensor.matmul(ps[:, w - w0, :], lhsT=ones[:], rhs=bias_rows[:, FEATS * w : FEATS * (w + 1)], start=True, stop=True)
+                nc.tensor.matmul(ps[:, w - w0, :], lhsT=ones[:, :P], rhs=bias_rows[:, FEATS * w : FEATS * (w + 1)], start=True, stop=True)
+
+        def warm_up(pool, tag, count, moving):
+            idle = pool.tile([P, FEATS], F32, tag=tag, name="idle")
+            for n in range(count):
+                nc.tensor.matmul(idle[:], lhsT=ones[:, :P], rhs=moving, start=True, stop=True)
 
         def keep_biases(w0, w1, engine):
             engine(out=bias_sb[:, w0:w1, :], in_=bias_ps[w0][:, : w1 - w0, :])
@@ -226,9 +230,6 @@ def tile_perspectronencodernetwork_pa_w8_kernel(
         def do_relu(i, r):
             nc.scalar.activation(out=hg(i)[:, r], in_=hps[(i, r)][:].rearrange("p t q -> p q t"), func=RELU)
 
-        def do_relu_vector(i, r):
-            nc.vector.tensor_scalar(out=hg(i)[:, r], in0=hps[(i, r)][:].rearrange("p t q -> p q t"), scalar1=0.0, scalar2=None, op0=MAX)
-
         def do_quant_h(i, r0=0, r1=2):
             if r0 == 0:
                 hq[i] = work.tile([P, 4 * 2 * P], U8, tag="hq", name="hq_t", align_bytes=64)
@@ -285,12 +286,16 @@ def tile_perspectronencodernetwork_pa_w8_kernel(
                 nc.scalar.copy(out=y, in_=bank[(i, k)][:, cols])
                 nc.gpsimd.tensor_tensor(out=y, in0=y, in1=bias_sb[:, k // 2, cols], op=ADD)
 
+        warm_up(ps_h, "h", 2, ones[:])
         do_group_v(0, 16, 64, nc.vector.tensor_copy)
         do_group_v(0, 0, 16)
+        spread_biases(0, 2)
         do_cast(0, 0, 1)
         do_turn(0, (0,))
         do_cast(0, 1, 2)
         do_turn(0, (1,))
+        spread_biases(2, 3)
+        warm_up(ps_h, "h", 1, bias_rows[:, :FEATS])
         spread_scales()
         do_cast(1)
         do_turn(1, (0, 1), True)
@@ -298,6 +303,7 @@ def tile_perspectronencodernetwork_pa_w8_kernel(
         do_scale_out(0, 0)
         do_scale_out(0, 1)
         do_cast(2)
+        warm_up(ps_h, "h", 1, bias_rows[:, :FEATS])
         do_turn(2)
         do_cast(3)
         keep_scales()
@@ -306,29 +312,28 @@ def tile_perspectronencodernetwork_pa_w8_kernel(
         do_prod(3)
         do_mix(0, 0)
         do_mix(0, 1)
-        spread_biases(0, 1)
-        spread_biases(1, 3)
-        do_group_v(1, 0, 16)
+        do_group_v(1, 0, 8)
         do_scale_out(1, 0)
         do_scale_out(1, 1)
         do_scale_out(2, 0)
         do_scale_out(2, 1)
-        keep_biases(0, 1, nc.vector.tensor_copy)
+        keep_biases(2, 3, nc.vector.tensor_copy)
+        keep_biases(0, 2, nc.scalar.copy)
         do_relu(0, 0)
+        warm_up(ps_x, "x", 2, hg(0)[:, 0].rearrange("p q t -> p (q t)"))
         do_relu(0, 1)
         do_cast(4)
         do_quant_h(0)
         do_quant_x(1)
         do_group_v(1, 48, 64, nc.vector.tensor_copy)
         do_prod(4)
-        keep_biases(1, 3, nc.scalar.copy)
         do_project(0, 0)
         do_project(0, 1)
         do_mix(1, 0)
         do_project(0, 2)
         do_mix(1, 1)
         do_project(0, 3)
-        do_group_v(1, 16, 40)
+        do_group_v(1, 8, 40)
         do_empty(0, 0)
         do_relu(1, 0)
         do_relu(1, 1)

@@ -23,10 +23,11 @@ BANKS = 6
 EARLY = 3
 LEAD = 4
 BUSY = PAIRS - LEAD
-SHARE = 224
+SHARE = 256
+LAST_CUT = 48
 SHARED = {
-    **{(c, 2): SHARE for c in range(1, BUSY)},
-    **{(c, 2): FEATS for c in range(BUSY, PAIRS - 1)},
+    **{(c, 2): SHARE for c in range(1, BUSY - 1)},
+    **{(c, 2): FEATS for c in range(BUSY - 1, PAIRS - 1)},
     (BUSY, 5): 256,
     (PAIRS - 1, 2): 384,
 }
@@ -132,24 +133,22 @@ def tile_perspectronencodernetwork_pa_w8_kernel(
         def keep_biases(w0, w1, engine):
             engine(out=bias_sb[:, w0:w1, :], in_=bias_ps[w0][:, : w1 - w0, :])
 
-        ring = [keep.tile([P, 2, POINTS], BF16, align_bytes=64, name="ring%d" % n) for n in range(4)]
-
-        relu_ring = [keep.tile([P, 2, P, 4], BF16, align_bytes=64, name="relu_ring%d" % n) for n in range(3)]
+        ring = [keep.tile([P, 2, 2, POINTS], BF16, align_bytes=64, name="ring%d" % n) for n in range(3)]
 
         def hg(i):
-            return relu_ring[i % 3][:]
+            return ring[i % 3][:, 0].rearrange("p r (q t) -> p r q t", t=4)
+
+        def xg(i):
+            return ring[(i - 1) % 3][:, 1]
 
         def prod(i):
             if i < EARLY:
                 return cast[i][:]
             if i == EARLY:
-                return xg(0)[:]
+                return xg(0)
             if i % 2 == 0 and i > LEAD:
-                return hg(i - LEAD).rearrange("p r q t -> p r (q t)")
-            return xg(i - LEAD + 1)[:]
-
-        def xg(i):
-            return ring[i % 3] if i != EARLY else ring[3]
+                return ring[(i - LEAD) % 3][:, 0]
+            return xg(i - LEAD + 1)
 
         cast, xt, xq, xs = {}, {}, {}, {}
         vg, vq, vs = {}, {}, {}
@@ -173,6 +172,12 @@ def tile_perspectronencodernetwork_pa_w8_kernel(
         def do_prod(i):
             nc.gpsimd.tensor_tensor(out=prod(i), in0=cast[i][:], in1=scale_sb[:].unsqueeze(1).to_broadcast([P, 2, POINTS]), op=MULT)
 
+        last = {}
+
+        def do_prod_last(r, into):
+            last[r] = into
+            nc.gpsimd.tensor_tensor(out=into, in0=cast[PAIRS - 1][:, r, :], in1=scale_sb[:], op=MULT)
+
         def do_turn(i, tiles=(0, 1), spare=False):
             if spare:
                 x = ps_out.tile([P, 2, 2, P], F32, tag="o1", name="xt_t")
@@ -181,7 +186,7 @@ def tile_perspectronencodernetwork_pa_w8_kernel(
             for r in tiles:
                 xt[(i, r)] = x
             for r in tiles:
-                pairs_of_k = prod(i)[:, r, :].bitcast(F32)
+                pairs_of_k = (last[r] if i == PAIRS - 1 else prod(i)[:, r, :]).bitcast(F32)
                 for u in range(2):
                     nc.tensor.transpose(x[:, r, u, :], pairs_of_k[:, u : 256 : 2], ident[:])
 
@@ -191,10 +196,24 @@ def tile_perspectronencodernetwork_pa_w8_kernel(
                 in_=xt[(i, r0)][:, r0:r1].rearrange("p r u q -> p r q u"),
             )
 
+        codes, planes = {}, {}
+
+        def new_codes(c):
+            if c not in codes:
+                codes[c] = work.tile([P, 2, 4 * 2 * P], U8, tag="codes", name="codes_t", align_bytes=64)
+                planes[c] = work.tile([P, 2, 2 * P], U8, tag="planes", name="planes_t", align_bytes=64)
+                hq[c], hs[c] = codes[c][:, 0], planes[c][:, 0]
+                xq[c + 1], xs[c + 1] = codes[c][:, 1], planes[c][:, 1]
+
+        def do_quant_hx(c):
+            new_codes(c)
+            nc.vector.quantize_mx(
+                out=codes[c][:].rearrange("p a w -> p (a w)").bitcast(FP8X4), scales=planes[c][:].rearrange("p a w -> p (a w)"),
+                in_=ring[c % 3][:].rearrange("p a r s -> p (a r s)"),
+            )
+
         def do_quant_x(i, r0=0, r1=2):
-            if r0 == 0:
-                xq[i] = work.tile([P, 4 * 2 * P], U8, tag="xq", name="xq_t", align_bytes=64)
-                xs[i] = work.tile([P, 2 * P], U8, tag="xs", name="xs_t", align_bytes=64)
+            new_codes(i - 1)
             nc.vector.quantize_mx(
                 out=xq[i][:, 512 * r0 : 512 * r1].bitcast(FP8X4), scales=xs[i][:, P * r0 : P * r1],
                 in_=xg(i)[:, r0:r1, :].rearrange("p r s -> p (r s)"),
@@ -231,9 +250,7 @@ def tile_perspectronencodernetwork_pa_w8_kernel(
             nc.scalar.activation(out=hg(i)[:, r], in_=hps[(i, r)][:].rearrange("p t q -> p q t"), func=RELU)
 
         def do_quant_h(i, r0=0, r1=2):
-            if r0 == 0:
-                hq[i] = work.tile([P, 4 * 2 * P], U8, tag="hq", name="hq_t", align_bytes=64)
-                hs[i] = work.tile([P, 2 * P], U8, tag="hs", name="hs_t", align_bytes=64)
+            new_codes(i)
             nc.vector.quantize_mx(
                 out=hq[i][:, 512 * r0 : 512 * r1].bitcast(FP8X4), scales=hs[i][:, P * r0 : P * r1],
                 in_=hg(i)[:, r0:r1].rearrange("p r q t -> p (r q t)"),
@@ -351,18 +368,24 @@ def tile_perspectronencodernetwork_pa_w8_kernel(
         do_turn(3)
 
         for c in range(1, PAIRS + 1):
-            if c < PAIRS:
-                do_quant_h(c)
-            if c + 1 < PAIRS:
-                do_quant_x(c + 1)
             if c % 2 == 1 and c + 1 < PAIRS:
+                do_quant_hx(c)
                 do_quant_v((c + 1) // 2)
-            if c + LEAD < PAIRS:
+            else:
+                if c < PAIRS:
+                    do_quant_h(c)
+                if c + 1 < PAIRS:
+                    do_quant_x(c + 1)
+            if c + LEAD < PAIRS - 1:
                 do_prod(c + LEAD)
+            elif c == BUSY - 1:
+                do_prod_last(0, xg(c + 1)[:, 0, :])
+            elif c == BUSY:
+                do_prod_last(1, ring[c % 3][:, 0, 0, :])
             do_share(c - 1, 5)
             vb, vh = (c + 3) // 2, (c + 1) % 2
             if vb < SETS:
-                do_group_v(vb, 32 * vh, 32 * (vh + 1))
+                do_group_v(vb, 32 * vh, 32 * (vh + 1) if c < BUSY else LAST_CUT)
             first, second = (2, 0) if (c, 2) in SHARED else (0, 1)
             third = 3 - first - second
             if c < PAIRS:
@@ -381,8 +404,15 @@ def tile_perspectronencodernetwork_pa_w8_kernel(
             if c + 1 < PAIRS:
                 do_relu(c + 1, 0)
                 do_relu(c + 1, 1)
-            if EARLY <= c + 2 < PAIRS:
+            if c < BUSY:
                 do_group(c + 2)
+            if c == BUSY - 1:
+                do_turn(c + 3)
+                do_group(c + 3)
+            if c == BUSY:
+                do_group_v(vb, LAST_CUT, 64)
+                do_turn(c + 3)
+                do_group(c + 3)
             if c + LEAD + 1 < PAIRS:
                 do_cast(c + LEAD + 1)
             if c < PAIRS:
@@ -394,5 +424,5 @@ def tile_perspectronencodernetwork_pa_w8_kernel(
                 for k in (2, 3):
                     do_empty(c, k)
                     store(c, k)
-            if c + 3 < PAIRS:
+            if c < BUSY - 1:
                 do_turn(c + 3)

@@ -19,18 +19,12 @@ RELU = mybir.ActivationFunctionType.Relu
 
 P = 128
 PAIRS = 2 * SETS
-BANKS = 6
-EARLY = 3
-LEAD = 4
+EARLY = 2
+LEAD = 3
 BUSY = PAIRS - LEAD
+STRIP = 128
+PE_STRIPS = 1
 SHARE = 256
-LAST_CUT = 48
-SHARED = {
-    **{(c, 2): SHARE for c in range(1, BUSY - 1)},
-    **{(c, 2): FEATS for c in range(BUSY - 1, PAIRS - 1)},
-    (BUSY, 5): 256,
-    (PAIRS - 1, 2): 384,
-}
 
 
 def tile_perspectronencodernetwork_pa_w8_kernel(
@@ -47,10 +41,10 @@ def tile_perspectronencodernetwork_pa_w8_kernel(
     with ExitStack() as ctx:
         keep = ctx.enter_context(tc.tile_pool(name="keep", bufs=1))
         work = ctx.enter_context(tc.tile_pool(name="work", bufs=3))
-        stores = ctx.enter_context(tc.tile_pool(name="stores", bufs=SETS))
+        stores = ctx.enter_context(tc.tile_pool(name="stores", bufs=PAIRS - 1))
         ps_out = ctx.enter_context(tc.psum_pool(name="ps_out", bufs=1))
         ps_h = ctx.enter_context(tc.psum_pool(name="ps_h", bufs=2))
-        ps_x = ctx.enter_context(tc.psum_pool(name="ps_x", bufs=2))
+        ps_x = ctx.enter_context(tc.psum_pool(name="ps_x", bufs=1))
         ctx.enter_context(tc.manual_schedule())
 
         bias_rows = keep.tile([P, 3 * FEATS], BF16, name="bias_rows")
@@ -61,17 +55,19 @@ def tile_perspectronencodernetwork_pa_w8_kernel(
         nc.vector.memset(wscale_sb[:].bitcast(I32), 0)
         ident = keep.tile([P, P], F32, name="ident")
         make_identity(nc, ident[:])
+        ident_bf = keep.tile([P, P], BF16, name="ident_bf")
+        nc.vector.tensor_copy(out=ident_bf[:], in_=ident[:])
 
         scale_col = keep.tile([P, 4], F32, name="scale_col")
         codes_in = keep.tile([P, SETS, 4, POINTS], U8, align_bytes=64, name="codes_in")
-        vraw = [stores.tile([P, 2, 4, FEATS], BF16, tag="y%d" % n, name="vraw") for n in range(3)]
+        vraw = [keep.tile([P, 4, FEATS], BF16, name="vraw%d" % b) for b in range(SETS)]
         w_sb = keep.tile([P, 3, 4 * FEATS], U8, align_bytes=64, name="w_sb")
 
-        def load_codes(b0, b1, r0=0, r1=4):
-            nc.sync.dma_start(out=codes_in[:, b0:b1, r0:r1], in_=attn1_bytes[b0:b1].rearrange("b (p r) s -> p b r s", r=4)[:, :, r0:r1])
+        def load_codes(b0, b1):
+            nc.sync.dma_start(out=codes_in[:, b0:b1], in_=attn1_bytes[b0:b1].rearrange("b (p r) s -> p b r s", r=4))
 
-        def load_v(b0, b1):
-            nc.sync.dma_start(out=vraw[b0 // 2][:, b0 % 2 : b0 % 2 + b1 - b0], in_=v1[b0:b1].rearrange("b (p j) f -> p b j f", j=4))
+        def load_v(b):
+            nc.sync.dma_start(out=vraw[b][:], in_=v1[b].rearrange("(p j) f -> p j f", j=4))
 
         def load_words(w):
             nc.sync.dma_start(out=w_sb[:, w, :], in_=words_in[w][0].rearrange("p n t -> p (n t)"))
@@ -86,80 +82,77 @@ def tile_perspectronencodernetwork_pa_w8_kernel(
         def load_bias(w):
             nc.sync.dma_start(out=bias_rows[0:1, FEATS * w : FEATS * (w + 1)], in_=biases_in[w].rearrange("(o n) -> o n", o=1))
 
-        load_v(0, 1)
+        def load_scale():
+            nc.sync.dma_start(out=scale_col[:], in_=attn1_scale.rearrange("a b (p t) -> p (a b t)", t=4))
+
+        load_v(0)
+        load_codes(0, 1)
+        load_scale()
         load_bias(0)
         load_bias(1)
-        load_bias(2)
-        load_codes(0, 1)
-        nc.sync.dma_start(out=scale_col[:], in_=attn1_scale.rearrange("a b (p t) -> p (a b t)", t=4))
         load_codes(1, 2)
-        load_v(1, 2)
+        load_bias(2)
+        load_v(1)
         load_wscales(0)
         load_words(0)
         load_words(1)
-        load_codes(2, 3)
         load_wscales(1)
         load_words(2)
-        load_v(2, 3)
         load_wscales(2)
+        load_codes(2, 3)
+        load_v(2)
         load_codes(3, 6)
-        load_v(3, 4)
-        load_v(4, 6)
+        load_v(3)
+        load_v(4)
+        load_v(5)
 
         scale_sb = keep.tile([P, POINTS], F32, name="scale_sb")
-        scale_ps = ps_out.tile([P, 4, P], F32, tag="o0", name="scale_ps")
         bias_sb = keep.tile([P, 3, FEATS], BF16, name="bias_sb")
+        spread = {}
 
-        def spread_scales():
+        def spread_scales(tag):
+            spread["scale"] = ps_out.tile([P, 4, P], F32, tag=tag, name="scale_ps")
             for t in range(4):
-                nc.tensor.transpose(scale_ps[:, t, :], scale_col[:, t : t + 1].to_broadcast([P, P]), ident[:])
+                nc.tensor.transpose(spread["scale"][:, t, :], scale_col[:, t : t + 1].to_broadcast([P, P]), ident[:])
 
         def keep_scales():
-            nc.scalar.activation(out=scale_sb[:].rearrange("q (p t) -> q p t", t=4), in_=scale_ps[:].rearrange("q t p -> q p t"), func=COPY)
+            nc.scalar.activation(out=scale_sb[:].rearrange("q (p t) -> q p t", t=4), in_=spread["scale"][:].rearrange("q t p -> q p t"), func=COPY)
 
-        bias_ps = {}
-
-        def spread_biases(w0, w1):
-            ps = ps_out.tile([P, 2, FEATS], BF16, tag="o%d" % (2 + w0 // 2), name="bias_ps")
-            bias_ps[w0] = ps
+        def spread_biases(w0, w1, tag):
+            rows = ps_out.tile([P, 2, FEATS], BF16, tag=tag, name="bias_ps")
             for w in range(w0, w1):
-                nc.tensor.matmul(ps[:, w - w0, :], lhsT=ones[:, :P], rhs=bias_rows[:, FEATS * w : FEATS * (w + 1)], start=True, stop=True)
+                spread[w] = rows[:, w - w0 :, :]
+                nc.tensor.matmul(rows[:, w - w0, :], lhsT=ones[:, :P], rhs=bias_rows[:, FEATS * w : FEATS * (w + 1)], start=True, stop=True)
+
+        def keep_biases(w0, w1, engine):
+            engine(out=bias_sb[:, w0:w1, :], in_=spread[w0][:, : w1 - w0, :])
 
         def warm_up(pool, tag, count, moving):
             idle = pool.tile([P, FEATS], F32, tag=tag, name="idle")
             for n in range(count):
                 nc.tensor.matmul(idle[:], lhsT=ones[:, :P], rhs=moving, start=True, stop=True)
 
-        def keep_biases(w0, w1, engine):
-            engine(out=bias_sb[:, w0:w1, :], in_=bias_ps[w0][:, : w1 - w0, :])
-
-        ring = [keep.tile([P, 2, 2, POINTS], BF16, align_bytes=64, name="ring%d" % n) for n in range(3)]
+        ring = [keep.tile([P, 2, 2, POINTS], BF16, align_bytes=64, name="ring%d" % n) for n in range(2)]
 
         def hg(i):
-            return ring[i % 3][:, 0].rearrange("p r (q t) -> p r q t", t=4)
+            return ring[i % 2][:, 0].rearrange("p r (q t) -> p r q t", t=4)
 
         def xg(i):
-            return ring[(i - 1) % 3][:, 1]
-
-        def prod(i):
-            if i < EARLY:
-                return cast[i][:]
-            if i == EARLY:
-                return xg(0)
-            if i % 2 == 0 and i > LEAD:
-                return ring[(i - LEAD) % 3][:, 0]
-            return xg(i - LEAD + 1)
+            return ring[(i - 1) % 2][:, 1]
 
         cast, xt, xq, xs = {}, {}, {}, {}
-        vg, vq, vs = {}, {}, {}
+        vg, vq, vs, vb = {}, {}, {}, {}
         hps, hq, hs = {}, {}, {}
         bank, res, done = {}, {}, {}
+        source = {}
 
         def do_cast(i, r0=0, r1=2):
-            if r0 == 0:
+            if i not in cast:
                 cast[i] = work.tile([P, 2, POINTS], BF16, tag="cast", name="cast_t")
             h = 2 * (i % 2)
             nc.scalar.copy(out=cast[i][:, r0:r1, :], in_=codes_in[:, i // 2, h + r0 : h + r1, :].bitcast(FP8))
+            for r in range(r0, r1):
+                source[(i, r)] = cast[i][:, r, :]
 
         def do_scale_out(i, r):
             nc.vector.tensor_tensor(
@@ -169,31 +162,24 @@ def tile_perspectronencodernetwork_pa_w8_kernel(
                 op=MULT,
             )
 
-        def do_prod(i):
-            nc.gpsimd.tensor_tensor(out=prod(i), in0=cast[i][:], in1=scale_sb[:].unsqueeze(1).to_broadcast([P, 2, POINTS]), op=MULT)
+        def do_prod(i, r0=0, r1=2, into=None):
+            into = xg(i)[:, r0:r1] if into is None else into
+            for r in range(r0, r1):
+                source[(i, r)] = into[:, r - r0, :]
+            nc.gpsimd.tensor_tensor(out=into, in0=cast[i][:, r0:r1], in1=scale_sb[:].unsqueeze(1).to_broadcast([P, r1 - r0, POINTS]), op=MULT)
 
-        last = {}
-
-        def do_prod_last(r, into):
-            last[r] = into
-            nc.gpsimd.tensor_tensor(out=into, in0=cast[PAIRS - 1][:, r, :], in1=scale_sb[:], op=MULT)
-
-        def do_turn(i, tiles=(0, 1), spare=False):
-            if spare:
-                x = ps_out.tile([P, 2, 2, P], F32, tag="o1", name="xt_t")
-            else:
-                x = ps_x.tile([P, 2, 2, P], F32, tag="x", name="xt_t")
+        def do_turn(i, tiles=(0, 1), pool=ps_x, tag="x"):
+            turned = pool.tile([P, 2, 2, P], F32, tag=tag, name="xt_t")
             for r in tiles:
-                xt[(i, r)] = x
-            for r in tiles:
-                pairs_of_k = (last[r] if i == PAIRS - 1 else prod(i)[:, r, :]).bitcast(F32)
+                xt[(i, r)] = turned
+                pairs_of_k = source[(i, r)].bitcast(F32)
                 for u in range(2):
-                    nc.tensor.transpose(x[:, r, u, :], pairs_of_k[:, u : 256 : 2], ident[:])
+                    nc.tensor.transpose(turned[:, r, u, :], pairs_of_k[:, u : 256 : 2], ident[:])
 
-        def do_group(i, r0=0, r1=2, engine=None):
-            (engine or nc.scalar.copy)(
-                out=xg(i)[:, r0:r1, :].bitcast(F32).rearrange("p r (q u) -> p r q u", u=2),
-                in_=xt[(i, r0)][:, r0:r1].rearrange("p r u q -> p r q u"),
+        def do_group(i):
+            nc.scalar.copy(
+                out=xg(i).bitcast(F32).rearrange("p r (q u) -> p r q u", u=2),
+                in_=xt[(i, 0)][:].rearrange("p r u q -> p r q u"),
             )
 
         codes, planes = {}, {}
@@ -209,7 +195,7 @@ def tile_perspectronencodernetwork_pa_w8_kernel(
             new_codes(c)
             nc.vector.quantize_mx(
                 out=codes[c][:].rearrange("p a w -> p (a w)").bitcast(FP8X4), scales=planes[c][:].rearrange("p a w -> p (a w)"),
-                in_=ring[c % 3][:].rearrange("p a r s -> p (a r s)"),
+                in_=ring[c % 2][:].rearrange("p a r s -> p (a r s)"),
             )
 
         def do_quant_x(i, r0=0, r1=2):
@@ -219,17 +205,41 @@ def tile_perspectronencodernetwork_pa_w8_kernel(
                 in_=xg(i)[:, r0:r1, :].rearrange("p r s -> p (r s)"),
             )
 
-        def do_group_v(b, n0, n1, engine=None):
+        def do_quant_h(i, r0=0, r1=2):
+            new_codes(i)
+            nc.vector.quantize_mx(
+                out=hq[i][:, 512 * r0 : 512 * r1].bitcast(FP8X4), scales=hs[i][:, P * r0 : P * r1],
+                in_=hg(i)[:, r0:r1].rearrange("p r q t -> p (r q t)"),
+            )
+
+        def grouped(b):
             if b not in vg:
-                vg[b] = work.tile([P, 4, P, 4], BF16, tag="vg", name="vg_t", align_bytes=64)
-            src = vraw[b // 2][:, b % 2].rearrange("p j (n m t) -> p n j m t", m=2, t=4)[:, n0:n1]
-            dst = vg[b][:].rearrange("p t (n m) j -> p n j m t", m=2)[:, n0:n1]
+                vg[b] = work.tile([P, 4, P, 4], BF16, tag="vg", name="vg_t", align_bytes=64, bufs=2)
+            return vg[b]
+
+        def do_group_v(b, n0, n1, engine=None):
+            src = vraw[b][:].rearrange("p j (n m t) -> p n j m t", m=2, t=4)[:, n0:n1]
+            dst = grouped(b)[:].rearrange("p t (n m) j -> p n j m t", m=2)[:, n0:n1]
             (engine or nc.scalar.copy)(out=dst, in_=src)
 
+        def do_weave_v(b, s0, s1, pool=ps_h, tag="h"):
+            vb[(b, s0)] = pool.tile([P, 2, STRIP, 4], BF16, tag=tag, name="vb_t")
+            for s in range(s0, s1):
+                nc.tensor.matmul(
+                    vb[(b, s0)][:, s - s0].rearrange("p f j -> p j f"), lhsT=ident_bf[:],
+                    rhs=vraw[b][:, :, STRIP * s : STRIP * (s + 1)], start=True, stop=True,
+                )
+
+        def do_keep_v(b, s0, s1):
+            m0, m1 = STRIP // 4 * s0, STRIP // 4 * s1
+            nc.scalar.copy(
+                out=grouped(b)[:, :, m0:m1, :].bitcast(F32),
+                in_=vb[(b, s0)][:, : s1 - s0].bitcast(F32).rearrange("p s (m t) u -> p t (s m) u", t=4),
+            )
 
         def do_quant_v(b):
-            vq[b] = work.tile([P, 4 * FEATS], U8, tag="vq", name="vq_t", align_bytes=64)
-            vs[b] = work.tile([P, FEATS], U8, tag="vs", name="vs_t", align_bytes=64)
+            vq[b] = work.tile([P, 4 * FEATS], U8, tag="vq", name="vq_t", align_bytes=64, bufs=2)
+            vs[b] = work.tile([P, FEATS], U8, tag="vs", name="vs_t", align_bytes=64, bufs=2)
             nc.vector.quantize_mx(out=vq[b][:].bitcast(FP8X4), scales=vs[b][:], in_=vg[b][:].rearrange("p t m j -> p (t m j)"))
 
         def do_mix(i, r):
@@ -249,14 +259,7 @@ def tile_perspectronencodernetwork_pa_w8_kernel(
         def do_relu(i, r):
             nc.scalar.activation(out=hg(i)[:, r], in_=hps[(i, r)][:].rearrange("p t q -> p q t"), func=RELU)
 
-        def do_quant_h(i, r0=0, r1=2):
-            new_codes(i)
-            nc.vector.quantize_mx(
-                out=hq[i][:, 512 * r0 : 512 * r1].bitcast(FP8X4), scales=hs[i][:, P * r0 : P * r1],
-                in_=hg(i)[:, r0:r1].rearrange("p r q t -> p (r q t)"),
-            )
-
-        free_banks = [1, 0, 3, 2]
+        free_banks = [4, 1, 2, 3, 0]
         place = {}
 
         def do_project(i, k):
@@ -274,97 +277,100 @@ def tile_perspectronencodernetwork_pa_w8_kernel(
                 start=True, stop=True,
             )
 
+        def result(i, k):
+            w = k // 2
+            if (i, w) not in res:
+                res[(i, w)] = stores.tile([P, 2, FEATS], F32, tag="y%d" % w, name="y_t")
+            return res[(i, w)][:, k % 2, :]
+
         def store(i, k):
             w, h = k // 2, 2 * (i % 2)
             done[(i, w)] = done.get((i, w), 0) + 1
             if done[(i, w)] == 2:
                 rows = outs[w][i // 2].rearrange("(p r) n -> p r n", r=4)
-                nc.sync.dma_start(out=rows[:, h : h + 2, :], in_=res[(i // 2, w)][:, h : h + 2, :])
+                nc.sync.dma_start(out=rows[:, h : h + 2, :], in_=res[(i, w)][:])
 
-        def shared_columns(i, k):
-            return slice(FEATS - SHARED.get((i, k), 0), FEATS)
-
-        def result(i, k):
-            b, w, r = i // 2, k // 2, 2 * (i % 2) + k % 2
-            if (b, w) not in res:
-                res[(b, w)] = stores.tile([P, 4, FEATS], F32, tag="y%d" % w, name="y_t")
-            return res[(b, w)][:, r, :]
-
-        def do_empty(i, k):
-            own = slice(0, shared_columns(i, k).start)
-            if own.stop:
-                nc.vector.tensor_tensor(out=result(i, k)[:, own], in0=bank[(i, k)][:, own], in1=bias_sb[:, k // 2, own], op=ADD)
+        def do_empty(i, k, width=FEATS):
+            cols = slice(0, width)
+            nc.vector.tensor_tensor(out=result(i, k)[:, cols], in0=bank[(i, k)][:, cols], in1=bias_sb[:, k // 2, cols], op=ADD)
             free_banks.append(place[(i, k)])
+            store(i, k)
 
-        def do_share(i, k):
-            if SHARED.get((i, k), 0):
-                cols = shared_columns(i, k)
-                y = result(i, k)[:, cols]
-                nc.scalar.copy(out=y, in_=bank[(i, k)][:, cols])
-                nc.gpsimd.tensor_tensor(out=y, in0=y, in1=bias_sb[:, k // 2, cols], op=ADD)
+        def do_copy_out(i, k, width=FEATS):
+            cols = slice(FEATS - width, FEATS)
+            nc.scalar.copy(out=result(i, k)[:, cols], in_=bank[(i, k)][:, cols])
+            if width == FEATS:
+                free_banks.append(place[(i, k)])
+
+        def do_add_bias(i, k, width=FEATS):
+            cols = slice(FEATS - width, FEATS)
+            y = result(i, k)[:, cols]
+            nc.gpsimd.tensor_tensor(out=y, in0=y, in1=bias_sb[:, k // 2, cols], op=ADD)
+            if width == FEATS:
+                store(i, k)
 
         warm_up(ps_h, "h", 2, ones[:])
         do_group_v(0, 16, 64, nc.vector.tensor_copy)
         do_group_v(0, 0, 16)
-        spread_biases(0, 2)
+        warm_up(ps_h, "h", 2, vraw[0][:, 0, :])
         do_cast(0, 0, 1)
         do_turn(0, (0,))
+        spread_scales("o0")
         do_cast(0, 1, 2)
-        do_turn(0, (1,))
-        spread_biases(2, 3)
-        warm_up(ps_h, "h", 1, bias_rows[:, :FEATS])
-        spread_scales()
+        do_turn(0, (1,), ps_out, "o4")
+        spread_biases(0, 2, "o2")
         do_cast(1)
-        do_turn(1, (0, 1), True)
+        do_turn(1, (0, 1), ps_out, "o1")
         do_quant_v(0)
         do_scale_out(0, 0)
         do_scale_out(0, 1)
-        do_cast(2)
-        warm_up(ps_h, "h", 1, bias_rows[:, :FEATS])
-        do_turn(2)
-        do_cast(3)
         keep_scales()
+        do_cast(2, 0, 1)
         do_quant_x(0, 0, 1)
         do_quant_x(0, 1, 2)
-        do_prod(3)
+        do_prod(2, 0, 1, ring[1][:, 1, 0:1])
         do_mix(0, 0)
         do_mix(0, 1)
-        do_group_v(1, 0, 8)
+        spread_biases(2, 3, "o3")
+        do_weave_v(1, 0, 1, ps_out, "o0")
         do_scale_out(1, 0)
         do_scale_out(1, 1)
-        do_scale_out(2, 0)
-        do_scale_out(2, 1)
-        keep_biases(2, 3, nc.vector.tensor_copy)
-        keep_biases(0, 2, nc.scalar.copy)
+        do_cast(2, 1, 2)
+        do_group_v(1, 16, 32)
+        keep_biases(0, 1, nc.vector.tensor_copy)
         do_relu(0, 0)
-        warm_up(ps_x, "x", 2, hg(0)[:, 0].rearrange("p q t -> p (q t)"))
         do_relu(0, 1)
-        do_cast(4)
-        do_quant_h(0)
+        do_cast(3)
+        do_quant_h(0, 0, 1)
         do_quant_x(1)
-        do_group_v(1, 48, 64, nc.vector.tensor_copy)
-        do_prod(4)
+        do_quant_h(0, 1, 2)
+        keep_biases(1, 2, nc.vector.tensor_copy)
+        do_prod(2, 1, 2, ring[0][:, 0, 0:1])
+        do_prod(3)
+        do_keep_v(1, 0, 1)
+        keep_biases(2, 3, nc.scalar.copy)
         do_project(0, 0)
-        do_project(0, 1)
         do_mix(1, 0)
-        do_project(0, 2)
+        do_project(0, 1)
         do_mix(1, 1)
+        do_project(0, 2)
         do_project(0, 3)
-        do_group_v(1, 8, 40)
-        do_empty(0, 0)
+        do_project(0, 4)
+        do_turn(2)
         do_relu(1, 0)
         do_relu(1, 1)
-        store(0, 0)
-        do_empty(0, 1)
-        store(0, 1)
-        do_project(0, 4)
-        do_empty(0, 2)
-        store(0, 2)
+        do_group_v(1, 32, 48)
+        do_group(2)
+        do_group_v(1, 48, 64)
+        do_cast(4)
+        do_empty(0, 0)
         do_project(0, 5)
+        do_empty(0, 1)
+        do_empty(0, 2)
         do_empty(0, 3)
-        store(0, 3)
-        do_group_v(1, 40, 48)
-        do_cast(5)
+        do_empty(0, 4)
+        do_empty(0, 5)
+        do_weave_v(2, 0, PE_STRIPS)
         do_turn(3)
 
         for c in range(1, PAIRS + 1):
@@ -372,57 +378,53 @@ def tile_perspectronencodernetwork_pa_w8_kernel(
                 do_quant_hx(c)
                 do_quant_v((c + 1) // 2)
             else:
-                if c < PAIRS:
-                    do_quant_h(c)
                 if c + 1 < PAIRS:
                     do_quant_x(c + 1)
-            if c + LEAD < PAIRS - 1:
+                if c < PAIRS:
+                    do_quant_h(c)
+            if c + LEAD < PAIRS:
                 do_prod(c + LEAD)
-            elif c == BUSY - 1:
-                do_prod_last(0, xg(c + 1)[:, 0, :])
-            elif c == BUSY:
-                do_prod_last(1, ring[c % 3][:, 0, 0, :])
-            do_share(c - 1, 5)
-            vb, vh = (c + 3) // 2, (c + 1) % 2
-            if vb < SETS:
-                do_group_v(vb, 32 * vh, 32 * (vh + 1) if c < BUSY else LAST_CUT)
-            first, second = (2, 0) if (c, 2) in SHARED else (0, 1)
-            third = 3 - first - second
+            b, half = (c + 3) // 2, (c + 1) % 2
+            if b < SETS and PE_STRIPS:
+                do_keep_v(b, 2 * half, 2 * half + PE_STRIPS)
+            if c + 2 < PAIRS:
+                do_group(c + 2)
+            if b < SETS and PE_STRIPS < 2:
+                do_group_v(b, 32 * half + 16 * PE_STRIPS, 32 * (half + 1))
+            share = 0 if c == 1 else SHARE if c < BUSY else FEATS
             if c < PAIRS:
-                do_project(c, first)
-                do_project(c, second)
-                do_share(c, 2)
+                if c == 1:
+                    do_project(c, 0)
+                do_project(c, 2)
+                if share:
+                    do_copy_out(c, 2, share)
+                    do_add_bias(c, 2, share)
+                if c > 1:
+                    do_project(c, 0)
+                do_project(c, 1)
             if c + 1 < PAIRS:
                 do_mix(c + 1, 0)
                 do_mix(c + 1, 1)
-            for k in (5, 4):
-                do_empty(c - 1, k)
-                store(c - 1, k)
-            if c < PAIRS:
-                do_project(c, third)
-                do_project(c, 3)
+            if c > 1:
+                do_empty(c - 1, 5)
+                do_empty(c - 1, 4)
+            if c == PAIRS:
+                break
+            do_project(c, 3)
             if c + 1 < PAIRS:
                 do_relu(c + 1, 0)
                 do_relu(c + 1, 1)
-            if c < BUSY:
-                do_group(c + 2)
-            if c == BUSY - 1:
-                do_turn(c + 3)
-                do_group(c + 3)
-            if c == BUSY:
-                do_group_v(vb, LAST_CUT, 64)
-                do_turn(c + 3)
-                do_group(c + 3)
             if c + LEAD + 1 < PAIRS:
                 do_cast(c + LEAD + 1)
-            if c < PAIRS:
-                for k in (0, 1):
-                    do_empty(c, k)
-                    store(c, k)
-                do_project(c, 4)
-                do_project(c, 5)
-                for k in (2, 3):
-                    do_empty(c, k)
-                    store(c, k)
-            if c < BUSY - 1:
-                do_turn(c + 3)
+            for k in ((1, 0) if c % 2 and c > 1 else (0, 1)):
+                do_empty(c, k)
+            do_project(c, 4)
+            do_project(c, 5)
+            do_empty(c, 3)
+            if share < FEATS:
+                do_empty(c, 2, FEATS - share)
+            b, half = (c + 4) // 2, c % 2
+            if b < SETS and PE_STRIPS:
+                do_weave_v(b, 2 * half, 2 * half + PE_STRIPS)
+            if c + LEAD < PAIRS:
+                do_turn(c + LEAD)

@@ -23,8 +23,8 @@ EARLY = 2
 LEAD = 3
 BUSY = PAIRS - LEAD
 STRIP = 128
-PE_STRIPS = 1
-SHARE = 256
+FIRST_SHARE = 128
+SHARE = 240
 
 
 def tile_perspectronencodernetwork_pa_w8_kernel(
@@ -176,10 +176,10 @@ def tile_perspectronencodernetwork_pa_w8_kernel(
                 for u in range(2):
                     nc.tensor.transpose(turned[:, r, u, :], pairs_of_k[:, u : 256 : 2], ident[:])
 
-        def do_group(i):
+        def do_group(i, r1=2):
             nc.scalar.copy(
-                out=xg(i).bitcast(F32).rearrange("p r (q u) -> p r q u", u=2),
-                in_=xt[(i, 0)][:].rearrange("p r u q -> p r q u"),
+                out=xg(i)[:, :r1].bitcast(F32).rearrange("p r (q u) -> p r q u", u=2),
+                in_=xt[(i, 0)][:, :r1].rearrange("p r u q -> p r q u"),
             )
 
         codes, planes = {}, {}
@@ -259,7 +259,7 @@ def tile_perspectronencodernetwork_pa_w8_kernel(
         def do_relu(i, r):
             nc.scalar.activation(out=hg(i)[:, r], in_=hps[(i, r)][:].rearrange("p t q -> p q t"), func=RELU)
 
-        free_banks = [4, 1, 2, 3, 0]
+        free_banks = [1, 2, 0, 3, 4]
         place = {}
 
         def do_project(i, k):
@@ -286,8 +286,8 @@ def tile_perspectronencodernetwork_pa_w8_kernel(
         def store(i, k):
             w, h = k // 2, 2 * (i % 2)
             done[(i, w)] = done.get((i, w), 0) + 1
+            rows = outs[w][i // 2].rearrange("(p r) n -> p r n", r=4)
             if done[(i, w)] == 2:
-                rows = outs[w][i // 2].rearrange("(p r) n -> p r n", r=4)
                 nc.sync.dma_start(out=rows[:, h : h + 2, :], in_=res[(i, w)][:])
 
         def do_empty(i, k, width=FEATS):
@@ -336,41 +336,41 @@ def tile_perspectronencodernetwork_pa_w8_kernel(
         do_scale_out(1, 0)
         do_scale_out(1, 1)
         do_cast(2, 1, 2)
-        do_group_v(1, 16, 32)
+        do_turn(2, (1,), ps_out, "o4")
+        do_group_v(1, 16, 48)
         keep_biases(0, 1, nc.vector.tensor_copy)
         do_relu(0, 0)
         do_relu(0, 1)
         do_cast(3)
         do_quant_h(0, 0, 1)
-        do_quant_x(1)
-        do_quant_h(0, 1, 2)
         keep_biases(1, 2, nc.vector.tensor_copy)
-        do_prod(2, 1, 2, ring[0][:, 0, 0:1])
-        do_prod(3)
+        do_quant_h(0, 1, 2)
+        do_quant_x(1)
+        do_prod(3, 0, 2, ring[0][:, 0])
         do_keep_v(1, 0, 1)
         keep_biases(2, 3, nc.scalar.copy)
+        do_group_v(1, 48, 64)
         do_project(0, 0)
-        do_mix(1, 0)
         do_project(0, 1)
+        do_mix(1, 0)
         do_mix(1, 1)
         do_project(0, 2)
         do_project(0, 3)
-        do_project(0, 4)
-        do_turn(2)
+        do_turn(2, (0,))
         do_relu(1, 0)
         do_relu(1, 1)
-        do_group_v(1, 32, 48)
-        do_group(2)
-        do_group_v(1, 48, 64)
+        do_copy_out(0, 2, FIRST_SHARE)
+        do_add_bias(0, 2, FIRST_SHARE)
+        do_group(2, 1)
         do_cast(4)
         do_empty(0, 0)
-        do_project(0, 5)
         do_empty(0, 1)
-        do_empty(0, 2)
+        do_scale_out(2, 1)
+        do_project(0, 4)
+        do_project(0, 5)
         do_empty(0, 3)
-        do_empty(0, 4)
-        do_empty(0, 5)
-        do_weave_v(2, 0, PE_STRIPS)
+        do_empty(0, 2, FEATS - FIRST_SHARE)
+        do_weave_v(2, 0, 1)
         do_turn(3)
 
         for c in range(1, PAIRS + 1):
@@ -378,36 +378,30 @@ def tile_perspectronencodernetwork_pa_w8_kernel(
                 do_quant_hx(c)
                 do_quant_v((c + 1) // 2)
             else:
-                if c + 1 < PAIRS:
-                    do_quant_x(c + 1)
                 if c < PAIRS:
                     do_quant_h(c)
+                if c + 1 < PAIRS:
+                    do_quant_x(c + 1)
             if c + LEAD < PAIRS:
-                do_prod(c + LEAD)
+                do_prod(c + LEAD, 0, 2, None if c % 2 else ring[c % 2][:, 0])
             b, half = (c + 3) // 2, (c + 1) % 2
-            if b < SETS and PE_STRIPS:
-                do_keep_v(b, 2 * half, 2 * half + PE_STRIPS)
+            if b < SETS:
+                do_group_v(b, 32 * half + 16, 32 * (half + 1))
+                do_keep_v(b, 2 * half, 2 * half + 1)
             if c + 2 < PAIRS:
                 do_group(c + 2)
-            if b < SETS and PE_STRIPS < 2:
-                do_group_v(b, 32 * half + 16 * PE_STRIPS, 32 * (half + 1))
-            share = 0 if c == 1 else SHARE if c < BUSY else FEATS
+            share = SHARE if c < BUSY else FEATS
             if c < PAIRS:
-                if c == 1:
-                    do_project(c, 0)
                 do_project(c, 2)
-                if share:
-                    do_copy_out(c, 2, share)
-                    do_add_bias(c, 2, share)
-                if c > 1:
-                    do_project(c, 0)
+                do_copy_out(c, 2, share)
+                do_add_bias(c, 2, share)
+                do_project(c, 0)
                 do_project(c, 1)
             if c + 1 < PAIRS:
                 do_mix(c + 1, 0)
                 do_mix(c + 1, 1)
-            if c > 1:
-                do_empty(c - 1, 5)
-                do_empty(c - 1, 4)
+            do_empty(c - 1, 5)
+            do_empty(c - 1, 4)
             if c == PAIRS:
                 break
             do_project(c, 3)
@@ -416,7 +410,7 @@ def tile_perspectronencodernetwork_pa_w8_kernel(
                 do_relu(c + 1, 1)
             if c + LEAD + 1 < PAIRS:
                 do_cast(c + LEAD + 1)
-            for k in ((1, 0) if c % 2 and c > 1 else (0, 1)):
+            for k in ((1, 0) if c % 2 and c < BUSY else (0, 1)):
                 do_empty(c, k)
             do_project(c, 4)
             do_project(c, 5)
@@ -424,7 +418,7 @@ def tile_perspectronencodernetwork_pa_w8_kernel(
             if share < FEATS:
                 do_empty(c, 2, FEATS - share)
             b, half = (c + 4) // 2, c % 2
-            if b < SETS and PE_STRIPS:
-                do_weave_v(b, 2 * half, 2 * half + PE_STRIPS)
+            if b < SETS:
+                do_weave_v(b, 2 * half, 2 * half + 1)
             if c + LEAD < PAIRS:
                 do_turn(c + LEAD)

@@ -23,8 +23,7 @@ EARLY = 2
 LEAD = 3
 BUSY = PAIRS - LEAD
 STRIP = 128
-FIRST_SHARE = 128
-SHARE = 240
+SHARE = 256
 
 
 def tile_perspectronencodernetwork_pa_w8_kernel(
@@ -96,11 +95,11 @@ def tile_perspectronencodernetwork_pa_w8_kernel(
         load_wscales(0)
         load_words(0)
         load_words(1)
+        load_codes(2, 3)
         load_wscales(1)
         load_words(2)
-        load_wscales(2)
-        load_codes(2, 3)
         load_v(2)
+        load_wscales(2)
         load_codes(3, 6)
         load_v(3)
         load_v(4)
@@ -309,7 +308,7 @@ def tile_perspectronencodernetwork_pa_w8_kernel(
             if width == FEATS:
                 store(i, k)
 
-        warm_up(ps_h, "h", 2, ones[:])
+        warm_up(ps_h, "h", 4, ones[:])
         do_group_v(0, 16, 64, nc.vector.tensor_copy)
         do_group_v(0, 0, 16)
         warm_up(ps_h, "h", 2, vraw[0][:, 0, :])
@@ -337,7 +336,7 @@ def tile_perspectronencodernetwork_pa_w8_kernel(
         do_scale_out(1, 1)
         do_cast(2, 1, 2)
         do_turn(2, (1,), ps_out, "o4")
-        do_group_v(1, 16, 48)
+        do_group_v(1, 16, 32)
         keep_biases(0, 1, nc.vector.tensor_copy)
         do_relu(0, 0)
         do_relu(0, 1)
@@ -349,7 +348,7 @@ def tile_perspectronencodernetwork_pa_w8_kernel(
         do_prod(3, 0, 2, ring[0][:, 0])
         do_keep_v(1, 0, 1)
         keep_biases(2, 3, nc.scalar.copy)
-        do_group_v(1, 48, 64)
+        do_group_v(1, 32, 48)
         do_project(0, 0)
         do_project(0, 1)
         do_mix(1, 0)
@@ -359,9 +358,8 @@ def tile_perspectronencodernetwork_pa_w8_kernel(
         do_turn(2, (0,))
         do_relu(1, 0)
         do_relu(1, 1)
-        do_copy_out(0, 2, FIRST_SHARE)
-        do_add_bias(0, 2, FIRST_SHARE)
         do_group(2, 1)
+        do_group_v(1, 48, 64)
         do_cast(4)
         do_empty(0, 0)
         do_empty(0, 1)
@@ -369,7 +367,7 @@ def tile_perspectronencodernetwork_pa_w8_kernel(
         do_project(0, 4)
         do_project(0, 5)
         do_empty(0, 3)
-        do_empty(0, 2, FEATS - FIRST_SHARE)
+        do_empty(0, 2)
         do_weave_v(2, 0, 1)
         do_turn(3)
 
@@ -413,7 +411,8 @@ def tile_perspectronencodernetwork_pa_w8_kernel(
             for k in ((1, 0) if c % 2 and c < BUSY else (0, 1)):
                 do_empty(c, k)
             do_project(c, 4)
-            do_project(c, 5)
+            if c != BUSY - 1:
+                do_project(c, 5)
             do_empty(c, 3)
             if share < FEATS:
                 do_empty(c, 2, FEATS - share)
@@ -422,3 +421,5 @@ def tile_perspectronencodernetwork_pa_w8_kernel(
                 do_weave_v(b, 2 * half, 2 * half + 1)
             if c + LEAD < PAIRS:
                 do_turn(c + LEAD)
+            if c == BUSY - 1:
+                do_project(c, 5)

@@ -23,6 +23,7 @@ EARLY = 2
 LEAD = 3
 BUSY = PAIRS - LEAD
 STRIP = 128
+SECOND_QUEUE = [(9, 0), (10, 0), (11, 0), (11, 2)]
 SHARE = 256
 
 
@@ -287,7 +288,8 @@ def tile_perspectronencodernetwork_pa_w8_kernel(
             done[(i, w)] = done.get((i, w), 0) + 1
             rows = outs[w][i // 2].rearrange("(p r) n -> p r n", r=4)
             if done[(i, w)] == 2:
-                nc.sync.dma_start(out=rows[:, h : h + 2, :], in_=res[(i, w)][:])
+                queue = nc.scalar if (i, w) in SECOND_QUEUE else nc.sync
+                queue.dma_start(out=rows[:, h : h + 2, :], in_=res[(i, w)][:])
 
         def do_empty(i, k, width=FEATS):
             cols = slice(0, width)

@@ -24,7 +24,7 @@ LEAD = 3
 BUSY = PAIRS - LEAD
 STRIP = 128
 SECOND_QUEUE = [(9, 0), (10, 0), (11, 0), (11, 2)]
-SHARE = 256
+SHARE = 224
 
 
 def tile_perspectronencodernetwork_pa_w8_kernel(

@@ -24,7 +24,7 @@ LEAD = 3
 BUSY = PAIRS - LEAD
 STRIP = 128
 SECOND_QUEUE = [(9, 0), (10, 0), (11, 0), (11, 2)]
-SHARE = 224
+SHARE = (224, 264)
 
 
 def tile_perspectronencodernetwork_pa_w8_kernel(
@@ -132,13 +132,13 @@ def tile_perspectronencodernetwork_pa_w8_kernel(
             for n in range(count):
                 nc.tensor.matmul(idle[:], lhsT=ones[:, :P], rhs=moving, start=True, stop=True)
 
-        ring = [keep.tile([P, 2, 2, POINTS], BF16, align_bytes=64, name="ring%d" % n) for n in range(2)]
+        ring = [keep.tile([P, 5, POINTS], BF16, align_bytes=64, name="ring%d" % n) for n in range(2)]
 
         def hg(i):
-            return ring[i % 2][:, 0].rearrange("p r (q t) -> p r q t", t=4)
+            return ring[i % 2][:, 1:3].rearrange("p r (q t) -> p r q t", t=4)
 
         def xg(i):
-            return ring[(i - 1) % 2][:, 1]
+            return ring[(i - 1) % 2][:, 3:5]
 
         cast, xt, xq, xs = {}, {}, {}, {}
         vg, vq, vs, vb = {}, {}, {}, {}
@@ -191,11 +191,11 @@ def tile_perspectronencodernetwork_pa_w8_kernel(
                 hq[c], hs[c] = codes[c][:, 0], planes[c][:, 0]
                 xq[c + 1], xs[c + 1] = codes[c][:, 1], planes[c][:, 1]
 
-        def do_quant_hx(c):
+        def do_quant_hx(c, r0=0):
             new_codes(c)
             nc.vector.quantize_mx(
-                out=codes[c][:].rearrange("p a w -> p (a w)").bitcast(FP8X4), scales=planes[c][:].rearrange("p a w -> p (a w)"),
-                in_=ring[c % 2][:].rearrange("p a r s -> p (a r s)"),
+                out=codes[c][:].rearrange("p a w -> p (a w)")[:, 512 * r0 :].bitcast(FP8X4), scales=planes[c][:].rearrange("p a w -> p (a w)")[:, P * r0 :],
+                in_=ring[c % 2][:, 1 + r0 :].rearrange("p r s -> p (r s)"),
             )
 
         def do_quant_x(i, r0=0, r1=2):
@@ -329,7 +329,7 @@ def tile_perspectronencodernetwork_pa_w8_kernel(
         do_cast(2, 0, 1)
         do_quant_x(0, 0, 1)
         do_quant_x(0, 1, 2)
-        do_prod(2, 0, 1, ring[1][:, 1, 0:1])
+        do_prod(2, 0, 1)
         do_mix(0, 0)
         do_mix(0, 1)
         spread_biases(2, 3, "o3")
@@ -347,7 +347,7 @@ def tile_perspectronencodernetwork_pa_w8_kernel(
         keep_biases(1, 2, nc.vector.tensor_copy)
         do_quant_h(0, 1, 2)
         do_quant_x(1)
-        do_prod(3, 0, 2, ring[0][:, 0])
+        do_prod(3, 0, 2, ring[0][:, 1:3])
         do_keep_v(1, 0, 1)
         keep_biases(2, 3, nc.scalar.copy)
         do_group_v(1, 32, 48)
@@ -377,20 +377,20 @@ def tile_perspectronencodernetwork_pa_w8_kernel(
             if c % 2 == 1 and c + 1 < PAIRS:
                 do_quant_hx(c)
                 do_quant_v((c + 1) // 2)
-            else:
-                if c < PAIRS:
-                    do_quant_h(c)
-                if c + 1 < PAIRS:
-                    do_quant_x(c + 1)
+            elif c + 1 < PAIRS:
+                do_quant_h(c, 0, 1)
+                do_quant_hx(c, 1)
+            elif c < PAIRS:
+                do_quant_h(c)
             if c + LEAD < PAIRS:
-                do_prod(c + LEAD, 0, 2, None if c % 2 else ring[c % 2][:, 0])
+                do_prod(c + LEAD, 0, 2, None if c % 2 else ring[0][:, 0:2])
             b, half = (c + 3) // 2, (c + 1) % 2
             if b < SETS:
                 do_group_v(b, 32 * half + 16, 32 * (half + 1))
                 do_keep_v(b, 2 * half, 2 * half + 1)
             if c + 2 < PAIRS:
                 do_group(c + 2)
-            share = SHARE if c < BUSY else FEATS
+            share = SHARE[c % 2] if c < BUSY else FEATS
             if c < PAIRS:
                 do_project(c, 2)
                 do_copy_out(c, 2, share)

@@ -24,7 +24,7 @@ LEAD = 3
 BUSY = PAIRS - LEAD
 STRIP = 128
 SECOND_QUEUE = [(9, 0), (10, 0), (11, 0), (11, 2)]
-SHARE = (224, 264)
+SHARE = 240
 
 
 def tile_perspectronencodernetwork_pa_w8_kernel(
@@ -390,7 +390,7 @@ def tile_perspectronencodernetwork_pa_w8_kernel(
                 do_keep_v(b, 2 * half, 2 * half + 1)
             if c + 2 < PAIRS:
                 do_group(c + 2)
-            share = SHARE[c % 2] if c < BUSY else FEATS
+            share = SHARE if c < BUSY else FEATS
             if c < PAIRS:
                 do_project(c, 2)
                 do_copy_out(c, 2, share)

@@ -88,11 +88,11 @@ def tile_perspectronencodernetwork_pa_w8_kernel(
         load_v(0)
         load_codes(0, 1)
         load_scale()
+        load_v(1)
         load_bias(0)
         load_bias(1)
         load_codes(1, 2)
         load_bias(2)
-        load_v(1)
         load_wscales(0)
         load_words(0)
         load_words(1)
@@ -222,6 +222,10 @@ def tile_perspectronencodernetwork_pa_w8_kernel(
             dst = grouped(b)[:].rearrange("p t (n m) j -> p n j m t", m=2)[:, n0:n1]
             (engine or nc.scalar.copy)(out=dst, in_=src)
 
+        def do_group_v_pool(b, n0, n1):
+            src = vraw[b][:].rearrange("p j (m t) -> p t m j", t=4)[:, :, 2 * n0 : 2 * n1]
+            nc.gpsimd.tensor_scalar(out=grouped(b)[:, :, 2 * n0 : 2 * n1], in0=src, scalar1=1.0, scalar2=0.0, op0=MULT, op1=ADD)
+
         def do_weave_v(b, s0, s1, pool=ps_h, tag="h"):
             vb[(b, s0)] = pool.tile([P, 2, STRIP, 4], BF16, tag=tag, name="vb_t")
             for s in range(s0, s1):
@@ -323,6 +327,7 @@ def tile_perspectronencodernetwork_pa_w8_kernel(
         do_cast(1)
         do_turn(1, (0, 1), ps_out, "o1")
         do_quant_v(0)
+        do_group_v_pool(1, 44, 64)
         do_scale_out(0, 0)
         do_scale_out(0, 1)
         keep_scales()
@@ -350,7 +355,7 @@ def tile_perspectronencodernetwork_pa_w8_kernel(
         do_prod(3, 0, 2, ring[0][:, 1:3])
         do_keep_v(1, 0, 1)
         keep_biases(2, 3, nc.scalar.copy)
-        do_group_v(1, 32, 48)
+        do_group_v(1, 32, 44)
         do_project(0, 0)
         do_project(0, 1)
         do_mix(1, 0)
@@ -361,7 +366,6 @@ def tile_perspectronencodernetwork_pa_w8_kernel(
         do_relu(1, 0)
         do_relu(1, 1)
         do_group(2, 1)
-        do_group_v(1, 48, 64)
         do_cast(4)
         do_empty(0, 0)
         do_empty(0, 1)

@@ -18,6 +18,7 @@ COPY = mybir.ActivationFunctionType.Copy
 RELU = mybir.ActivationFunctionType.Relu
 
 P = 128
+FIRST_SHARE = 128
 PAIRS = 2 * SETS
 EARLY = 2
 LEAD = 3
@@ -47,10 +48,10 @@ def tile_perspectronencodernetwork_pa_w8_kernel(
         ps_x = ctx.enter_context(tc.psum_pool(name="ps_x", bufs=1))
         ctx.enter_context(tc.manual_schedule())
 
-        bias_rows = keep.tile([P, 3 * FEATS], BF16, name="bias_rows")
-        nc.vector.memset(bias_rows[:].bitcast(F32), 0.0)
         ones = keep.tile([P, FEATS], BF16, name="ones")
         nc.vector.memset(ones[:], 1.0)
+        bias_rows = keep.tile([P, 3 * FEATS], BF16, name="bias_rows")
+        nc.vector.memset(bias_rows[:].bitcast(F32), 0.0)
         wscale_sb = keep.tile([P, 3 * FEATS], U8, align_bytes=64, name="wscale_sb")
         nc.vector.memset(wscale_sb[:].bitcast(I32), 0)
         ident = keep.tile([P, P], F32, name="ident")
@@ -263,7 +264,7 @@ def tile_perspectronencodernetwork_pa_w8_kernel(
         def do_relu(i, r):
             nc.scalar.activation(out=hg(i)[:, r], in_=hps[(i, r)][:].rearrange("p t q -> p q t"), func=RELU)
 
-        free_banks = [1, 2, 0, 3, 4]
+        free_banks = [1, 0, 2, 3, 4]
         place = {}
 
         def do_project(i, k):
@@ -335,37 +336,40 @@ def tile_perspectronencodernetwork_pa_w8_kernel(
         do_quant_x(0, 0, 1)
         do_quant_x(0, 1, 2)
         do_prod(2, 0, 1)
+        keep_biases(0, 1, nc.vector.tensor_copy)
         do_mix(0, 0)
         do_mix(0, 1)
         spread_biases(2, 3, "o3")
-        do_weave_v(1, 0, 1, ps_out, "o0")
         do_scale_out(1, 0)
         do_scale_out(1, 1)
         do_cast(2, 1, 2)
         do_turn(2, (1,), ps_out, "o4")
-        do_group_v(1, 16, 32)
-        keep_biases(0, 1, nc.vector.tensor_copy)
+        do_cast(3, 0, 1)
         do_relu(0, 0)
+        do_weave_v(1, 0, 1)
         do_relu(0, 1)
-        do_cast(3)
+        do_cast(3, 1, 2)
         do_quant_h(0, 0, 1)
-        keep_biases(1, 2, nc.vector.tensor_copy)
-        do_quant_h(0, 1, 2)
         do_quant_x(1)
-        do_prod(3, 0, 2, ring[0][:, 1:3])
+        do_quant_h(0, 1, 2)
+        do_prod(3)
+        keep_biases(1, 2, nc.vector.tensor_copy)
         do_keep_v(1, 0, 1)
         keep_biases(2, 3, nc.scalar.copy)
-        do_group_v(1, 32, 44)
+        do_group_v(1, 16, 32)
         do_project(0, 0)
         do_project(0, 1)
+        do_project(0, 2)
         do_mix(1, 0)
         do_mix(1, 1)
-        do_project(0, 2)
         do_project(0, 3)
         do_turn(2, (0,))
+        do_copy_out(0, 2, FIRST_SHARE)
+        do_add_bias(0, 2, FIRST_SHARE)
         do_relu(1, 0)
         do_relu(1, 1)
         do_group(2, 1)
+        do_group_v(1, 32, 44)
         do_cast(4)
         do_empty(0, 0)
         do_empty(0, 1)
@@ -373,7 +377,7 @@ def tile_perspectronencodernetwork_pa_w8_kernel(
         do_project(0, 4)
         do_project(0, 5)
         do_empty(0, 3)
-        do_empty(0, 2)
+        do_empty(0, 2, FEATS - FIRST_SHARE)
         do_weave_v(2, 0, 1)
         do_turn(3)
 

@@ -18,8 +18,11 @@ COPY = mybir.ActivationFunctionType.Copy
 RELU = mybir.ActivationFunctionType.Relu
 
 P = 128
+STAGED = []
+STAGE = 320
 FIRST_SHARE = 128
 PAIRS = 2 * SETS
+LAST = PAIRS - 1
 EARLY = 2
 LEAD = 3
 BUSY = PAIRS - LEAD
@@ -97,10 +100,10 @@ def tile_perspectronencodernetwork_pa_w8_kernel(
         load_wscales(0)
         load_words(0)
         load_words(1)
-        load_codes(2, 3)
         load_wscales(1)
-        load_words(2)
         load_v(2)
+        load_codes(2, 3)
+        load_words(2)
         load_wscales(2)
         load_codes(3, 6)
         load_v(3)
@@ -177,10 +180,10 @@ def tile_perspectronencodernetwork_pa_w8_kernel(
                 for u in range(2):
                     nc.tensor.transpose(turned[:, r, u, :], pairs_of_k[:, u : 256 : 2], ident[:])
 
-        def do_group(i, r1=2):
+        def do_group(i, r1=2, r0=0):
             nc.scalar.copy(
-                out=xg(i)[:, :r1].bitcast(F32).rearrange("p r (q u) -> p r q u", u=2),
-                in_=xt[(i, 0)][:, :r1].rearrange("p r u q -> p r q u"),
+                out=xg(i)[:, r0:r1].bitcast(F32).rearrange("p r (q u) -> p r q u", u=2),
+                in_=xt[(i, r0)][:, r0:r1].rearrange("p r u q -> p r q u"),
             )
 
         codes, planes = {}, {}
@@ -315,10 +318,10 @@ def tile_perspectronencodernetwork_pa_w8_kernel(
             if width == FEATS:
                 store(i, k)
 
-        warm_up(ps_h, "h", 4, ones[:])
+        warm_up(ps_h, "h", 3, ones[:])
         do_group_v(0, 16, 64, nc.vector.tensor_copy)
         do_group_v(0, 0, 16)
-        warm_up(ps_h, "h", 2, vraw[0][:, 0, :])
+        warm_up(ps_h, "h", 3, vraw[0][:, 0, :])
         do_cast(0, 0, 1)
         do_turn(0, (0,))
         spread_scales("o0")
@@ -374,11 +377,11 @@ def tile_perspectronencodernetwork_pa_w8_kernel(
         do_empty(0, 0)
         do_empty(0, 1)
         do_scale_out(2, 1)
-        do_project(0, 4)
-        do_project(0, 5)
         do_empty(0, 3)
         do_empty(0, 2, FEATS - FIRST_SHARE)
         do_weave_v(2, 0, 1)
+        do_project(0, 4)
+        do_project(0, 5)
         do_turn(3)
 
         for c in range(1, PAIRS + 1):
@@ -390,26 +393,41 @@ def tile_perspectronencodernetwork_pa_w8_kernel(
                 do_quant_hx(c, 1)
             elif c < PAIRS:
                 do_quant_h(c)
-            if c + LEAD < PAIRS:
+            if c < BUSY - 1:
                 do_prod(c + LEAD, 0, 2, None if c % 2 else ring[0][:, 0:2])
+            elif c == BUSY - 1:
+                do_prod(LAST, 0, 1, ring[0][:, 1:2])
+            elif c == BUSY:
+                do_prod(LAST, 1, 2, ring[1][:, 3:4])
             b, half = (c + 3) // 2, (c + 1) % 2
             if b < SETS:
                 do_group_v(b, 32 * half + 16, 32 * (half + 1))
                 do_keep_v(b, 2 * half, 2 * half + 1)
-            if c + 2 < PAIRS:
+            if c + 2 < LAST - 1:
                 do_group(c + 2)
-            share = SHARE if c < BUSY else FEATS
+            elif c + 2 == LAST:
+                do_group(LAST, 1)
+            share = SHARE if c < BUSY - 1 else FEATS
+            staged = c - 1 in STAGED
+            if staged:
+                do_copy_out(c - 1, 5, STAGE)
+                do_add_bias(c - 1, 5, STAGE)
             if c < PAIRS:
                 do_project(c, 2)
                 do_copy_out(c, 2, share)
                 do_add_bias(c, 2, share)
+                if c + 2 == LAST - 1:
+                    do_group(c + 2)
                 do_project(c, 0)
                 do_project(c, 1)
             if c + 1 < PAIRS:
                 do_mix(c + 1, 0)
                 do_mix(c + 1, 1)
-            do_empty(c - 1, 5)
+            if not staged:
+                do_empty(c - 1, 5)
             do_empty(c - 1, 4)
+            if staged and STAGE < FEATS:
+                do_empty(c - 1, 5, FEATS - STAGE)
             if c == PAIRS:
                 break
             do_project(c, 3)
@@ -418,18 +436,20 @@ def tile_perspectronencodernetwork_pa_w8_kernel(
                 do_relu(c + 1, 1)
             if c + LEAD + 1 < PAIRS:
                 do_cast(c + LEAD + 1)
+            if c == BUSY:
+                do_turn(LAST, (1,))
+                do_group(LAST, 2, 1)
             for k in ((1, 0) if c % 2 and c < BUSY else (0, 1)):
                 do_empty(c, k)
             do_project(c, 4)
-            if c != BUSY - 1:
-                do_project(c, 5)
+            do_project(c, 5)
             do_empty(c, 3)
             if share < FEATS:
                 do_empty(c, 2, FEATS - share)
             b, half = (c + 4) // 2, c % 2
             if b < SETS:
                 do_weave_v(b, 2 * half, 2 * half + 1)
-            if c + LEAD < PAIRS:
+            if c < BUSY - 1:
                 do_turn(c + LEAD)
-            if c == BUSY - 1:
-                do_project(c, 5)
+            elif c == BUSY - 1:
+                do_turn(LAST, (0,))

@@ -15,11 +15,11 @@ FP8X4 = mybir.dt.float8_e4m3fn_x4
 ADD = mybir.AluOpType.add
 MULT = mybir.AluOpType.mult
 COPY = mybir.ActivationFunctionType.Copy
+IDENTITY = mybir.ActivationFunctionType.Identity
 RELU = mybir.ActivationFunctionType.Relu
 
 P = 128
-STAGED = []
-STAGE = 320
+SLICED = [(2, 5), (4, 5), (6, 5), (8, 4), (8, 5)]
 FIRST_SHARE = 128
 PAIRS = 2 * SETS
 LAST = PAIRS - 1
@@ -27,8 +27,11 @@ EARLY = 2
 LEAD = 3
 BUSY = PAIRS - LEAD
 STRIP = 128
-SECOND_QUEUE = [(9, 0), (10, 0), (11, 0), (11, 2)]
-SHARE = 240
+SECOND_QUEUE = [(9, 1), (10, 0), (11, 0), (11, 2)]
+STAGE = 256
+SHARE_SLICED = 208
+SHARE8 = 448
+SHARE = 232
 
 
 def tile_perspectronencodernetwork_pa_w8_kernel(
@@ -111,7 +114,7 @@ def tile_perspectronencodernetwork_pa_w8_kernel(
         load_v(5)
 
         scale_sb = keep.tile([P, POINTS], F32, name="scale_sb")
-        bias_sb = keep.tile([P, 3, FEATS], BF16, name="bias_sb")
+        bias_sb = keep.tile([P, 4, FEATS], BF16, name="bias_sb")
         spread = {}
 
         def spread_scales(tag):
@@ -128,8 +131,12 @@ def tile_perspectronencodernetwork_pa_w8_kernel(
                 spread[w] = rows[:, w - w0 :, :]
                 nc.tensor.matmul(rows[:, w - w0, :], lhsT=ones[:, :P], rhs=bias_rows[:, FEATS * w : FEATS * (w + 1)], start=True, stop=True)
 
+            if w1 == 3:
+                nc.tensor.matmul(rows[:, 1, :2], lhsT=bias_rows[:, 3 * FEATS - P :], rhs=ones[:, :2], start=True, stop=True)
+
         def keep_biases(w0, w1, engine):
-            engine(out=bias_sb[:, w0:w1, :], in_=spread[w0][:, : w1 - w0, :])
+            width = FEATS * (w1 - w0) + (2 if w1 == 3 else 0)
+            engine(out=bias_sb[:, w0:].rearrange("p w n -> p (w n)")[:, :width], in_=spread[w0].rearrange("p w n -> p (w n)")[:, :width])
 
         def warm_up(pool, tag, count, moving):
             idle = pool.tile([P, FEATS], F32, tag=tag, name="idle")
@@ -276,14 +283,30 @@ def tile_perspectronencodernetwork_pa_w8_kernel(
             free_banks.remove(place[(i, k)])
             o = ps_out.tile([P, FEATS], F32, tag="o%d" % place[(i, k)], name="o_t")
             bank[(i, k)] = o
-            nc.tensor.matmul_mx(
-                out=o[:],
-                lhsT=hq[i][:, 512 * r : 512 * (r + 1)].bitcast(FP8X4),
-                lhsT_scale=hs[i][:, P * r : P * (r + 1)],
-                rhs=w_sb[:, w, :].bitcast(FP8X4),
-                rhs_scale=wscale_sb[:, FEATS * w : FEATS * (w + 1)],
-                start=True, stop=True,
-            )
+            h_codes, h_scales = hq[i][:, 512 * r : 512 * (r + 1)].bitcast(FP8X4), hs[i][:, P * r : P * (r + 1)]
+            for c0, c1 in [(0, 2 * P), (2 * P, 3 * P)] if (i, k) in SLICED else [(0, FEATS)]:
+                nc.tensor.matmul_mx(
+                    out=o[:, c0:c1], lhsT=h_codes, lhsT_scale=h_scales,
+                    rhs=w_sb[:, w, 4 * c0 : 4 * c1].bitcast(FP8X4), rhs_scale=wscale_sb[:, FEATS * w + c0 : FEATS * w + c1],
+                    start=True, stop=True,
+                )
+            if (i, k) in SLICED:
+                nc.tensor.matmul_mx(
+                    out=o[:, 3 * P :], lhsT=w_sb[:, w, 12 * P :].bitcast(FP8X4), lhsT_scale=wscale_sb[:, FEATS * w + 3 * P : FEATS * (w + 1)],
+                    rhs=h_codes, rhs_scale=h_scales, start=True, stop=True,
+                )
+
+        sliced = {}
+
+        def do_slice_bias(i, k):
+            sliced[(i, k)] = work.tile([P, P], F32, tag="sliced", name="sliced_t", bufs=2)
+            nc.scalar.activation(out=sliced[(i, k)][:], in_=bank[(i, k)][:, 3 * P :], func=IDENTITY, bias=bias_sb[:, 3, 0:1])
+
+        def do_slice_back(i, k):
+            nc.tensor.transpose(bank[(i, k)][:, 3 * P :], sliced[(i, k)][:], ident[:])
+
+        def do_slice_out(i, k):
+            nc.scalar.copy(out=result(i, k)[:, 3 * P :], in_=bank[(i, k)][:, 3 * P :])
 
         def result(i, k):
             w = k // 2
@@ -399,6 +422,9 @@ def tile_perspectronencodernetwork_pa_w8_kernel(
                 do_prod(LAST, 0, 1, ring[0][:, 1:2])
             elif c == BUSY:
                 do_prod(LAST, 1, 2, ring[1][:, 3:4])
+            for k in (4, 5):
+                if (c - 1, k) in SLICED:
+                    do_slice_out(c - 1, k)
             b, half = (c + 3) // 2, (c + 1) % 2
             if b < SETS:
                 do_group_v(b, 32 * half + 16, 32 * (half + 1))
@@ -407,9 +433,8 @@ def tile_perspectronencodernetwork_pa_w8_kernel(
                 do_group(c + 2)
             elif c + 2 == LAST:
                 do_group(LAST, 1)
-            share = SHARE if c < BUSY - 1 else FEATS
-            staged = c - 1 in STAGED
-            if staged:
+            share = (SHARE_SLICED if (c - 1, 5) in SLICED else SHARE) if c < BUSY - 1 else (SHARE8 if c == BUSY - 1 else FEATS)
+            if c == BUSY + 1:
                 do_copy_out(c - 1, 5, STAGE)
                 do_add_bias(c - 1, 5, STAGE)
             if c < PAIRS:
@@ -423,19 +448,21 @@ def tile_perspectronencodernetwork_pa_w8_kernel(
             if c + 1 < PAIRS:
                 do_mix(c + 1, 0)
                 do_mix(c + 1, 1)
-            if not staged:
-                do_empty(c - 1, 5)
-            do_empty(c - 1, 4)
-            if staged and STAGE < FEATS:
+            if c == BUSY + 1:
+                do_empty(c - 1, 4)
                 do_empty(c - 1, 5, FEATS - STAGE)
+            elif (c - 1, 5) in SLICED:
+                do_empty(c - 1, 4, FEATS - P if (c - 1, 4) in SLICED else FEATS)
+                do_empty(c - 1, 5, FEATS - P)
+            else:
+                do_empty(c - 1, 5)
+                do_empty(c - 1, 4)
             if c == PAIRS:
                 break
             do_project(c, 3)
             if c + 1 < PAIRS:
                 do_relu(c + 1, 0)
                 do_relu(c + 1, 1)
-            if c + LEAD + 1 < PAIRS:
-                do_cast(c + LEAD + 1)
             if c == BUSY:
                 do_turn(LAST, (1,))
                 do_group(LAST, 2, 1)
@@ -443,12 +470,20 @@ def tile_perspectronencodernetwork_pa_w8_kernel(
                 do_empty(c, k)
             do_project(c, 4)
             do_project(c, 5)
+            for k in (4, 5):
+                if (c, k) in SLICED:
+                    do_slice_bias(c, k)
+            if c + LEAD + 1 < PAIRS:
+                do_cast(c + LEAD + 1)
             do_empty(c, 3)
             if share < FEATS:
                 do_empty(c, 2, FEATS - share)
             b, half = (c + 4) // 2, c % 2
             if b < SETS:
                 do_weave_v(b, 2 * half, 2 * half + 1)
+            for k in (4, 5):
+                if (c, k) in SLICED:
+                    do_slice_back(c, k)
             if c < BUSY - 1:
                 do_turn(c + LEAD)
             elif c == BUSY - 1:

@@ -19,7 +19,7 @@ IDENTITY = mybir.ActivationFunctionType.Identity
 RELU = mybir.ActivationFunctionType.Relu
 
 P = 128
-SLICED = [(2, 5), (4, 5), (6, 5), (8, 4), (8, 5)]
+SLICED = [(2, 5), (4, 5), (6, 5), (8, 5)]
 FIRST_SHARE = 128
 PAIRS = 2 * SETS
 LAST = PAIRS - 1
@@ -28,7 +28,6 @@ LEAD = 3
 BUSY = PAIRS - LEAD
 STRIP = 128
 SECOND_QUEUE = [(9, 1), (10, 0), (11, 0), (11, 2)]
-STAGE = 256
 SHARE_SLICED = 208
 SHARE8 = 448
 SHARE = 232
@@ -408,7 +407,11 @@ def tile_perspectronencodernetwork_pa_w8_kernel(
         do_turn(3)
 
         for c in range(1, PAIRS + 1):
-            if c % 2 == 1 and c + 1 < PAIRS:
+            if c == BUSY:
+                do_quant_h(c, 0, 1)
+                do_quant_hx(c, 1)
+                do_quant_v((c + 1) // 2)
+            elif c % 2 == 1 and c + 1 < PAIRS:
                 do_quant_hx(c)
                 do_quant_v((c + 1) // 2)
             elif c + 1 < PAIRS:
@@ -434,9 +437,6 @@ def tile_perspectronencodernetwork_pa_w8_kernel(
             elif c + 2 == LAST:
                 do_group(LAST, 1)
             share = (SHARE_SLICED if (c - 1, 5) in SLICED else SHARE) if c < BUSY - 1 else (SHARE8 if c == BUSY - 1 else FEATS)
-            if c == BUSY + 1:
-                do_copy_out(c - 1, 5, STAGE)
-                do_add_bias(c - 1, 5, STAGE)
             if c < PAIRS:
                 do_project(c, 2)
                 do_copy_out(c, 2, share)
@@ -448,10 +448,7 @@ def tile_perspectronencodernetwork_pa_w8_kernel(
             if c + 1 < PAIRS:
                 do_mix(c + 1, 0)
                 do_mix(c + 1, 1)
-            if c == BUSY + 1:
-                do_empty(c - 1, 4)
-                do_empty(c - 1, 5, FEATS - STAGE)
-            elif (c - 1, 5) in SLICED:
+            if (c - 1, 5) in SLICED:
                 do_empty(c - 1, 4, FEATS - P if (c - 1, 4) in SLICED else FEATS)
                 do_empty(c - 1, 5, FEATS - P)
             else:

@@ -19,8 +19,9 @@ IDENTITY = mybir.ActivationFunctionType.Identity
 RELU = mybir.ActivationFunctionType.Relu
 
 P = 128
-SLICED = [(2, 5), (4, 5), (6, 5), (8, 5)]
+SLICED = [(c, k) for c in (2, 4, 6) for k in (4, 5)] + [(8, 5)]
 FIRST_SHARE = 128
+SECOND_SHARE = 192
 PAIRS = 2 * SETS
 LAST = PAIRS - 1
 EARLY = 2
@@ -28,7 +29,7 @@ LEAD = 3
 BUSY = PAIRS - LEAD
 STRIP = 128
 SECOND_QUEUE = [(9, 1), (10, 0), (11, 0), (11, 2)]
-SHARE_SLICED = 208
+SHARE_SLICED = 168
 SHARE8 = 448
 SHARE = 232
 
@@ -418,7 +419,8 @@ def tile_perspectronencodernetwork_pa_w8_kernel(
                 do_quant_h(c, 0, 1)
                 do_quant_hx(c, 1)
             elif c < PAIRS:
-                do_quant_h(c)
+                do_quant_h(c, 0, 1)
+                do_quant_h(c, 1, 2)
             if c < BUSY - 1:
                 do_prod(c + LEAD, 0, 2, None if c % 2 else ring[0][:, 0:2])
             elif c == BUSY - 1:
@@ -436,7 +438,7 @@ def tile_perspectronencodernetwork_pa_w8_kernel(
                 do_group(c + 2)
             elif c + 2 == LAST:
                 do_group(LAST, 1)
-            share = (SHARE_SLICED if (c - 1, 5) in SLICED else SHARE) if c < BUSY - 1 else (SHARE8 if c == BUSY - 1 else FEATS)
+            share = (SECOND_SHARE if c == 1 else SHARE_SLICED if (c - 1, 5) in SLICED else SHARE) if c < BUSY - 1 else (SHARE8 if c == BUSY - 1 else FEATS)
             if c < PAIRS:
                 do_project(c, 2)
                 do_copy_out(c, 2, share)

from contextlib import ExitStack

import concourse.mybir as mybir
from concourse.masks import make_identity

SETS, POINTS, FEATS = 6, 512, 512
FLOPS = 2 * SETS * POINTS * FEATS * (POINTS + 3 * FEATS)

F32 = mybir.dt.float32
BF16 = mybir.dt.bfloat16
U8 = mybir.dt.uint8
I32 = mybir.dt.int32
FP8 = mybir.dt.float8_e4m3fn
FP8X4 = mybir.dt.float8_e4m3fn_x4
ADD = mybir.AluOpType.add
MULT = mybir.AluOpType.mult
COPY = mybir.ActivationFunctionType.Copy
IDENTITY = mybir.ActivationFunctionType.Identity
RELU = mybir.ActivationFunctionType.Relu

P = 128
SLICED = [(c, k) for c in (2, 4, 6) for k in (4, 5)] + [(8, 5)]
FIRST_SHARE = 128
SECOND_SHARE = 192
PAIRS = 2 * SETS
LAST = PAIRS - 1
EARLY = 2
LEAD = 3
BUSY = PAIRS - LEAD
STRIP = 128
SECOND_QUEUE = [(9, 1), (10, 0), (11, 0), (11, 2)]
SHARE_SLICED = 168
SHARE8 = 448
SHARE = 232


def tile_perspectronencodernetwork_pa_w8_kernel(
    tc, attn1_bytes, attn1_scale, v1,
    wq_words, wq_scales, bq, wk_words, wk_scales, bk, wv_words, wv_scales, bv,
    out_0, out_1, out_2,
):
    nc = tc.nc
    outs = [out_0, out_1, out_2]
    words_in = [wq_words, wk_words, wv_words]
    wscales_in = [wq_scales, wk_scales, wv_scales]
    biases_in = [bq, bk, bv]

    with ExitStack() as ctx:
        keep = ctx.enter_context(tc.tile_pool(name="keep", bufs=1))
        work = ctx.enter_context(tc.tile_pool(name="work", bufs=3))
        stores = ctx.enter_context(tc.tile_pool(name="stores", bufs=PAIRS - 1))
        ps_out = ctx.enter_context(tc.psum_pool(name="ps_out", bufs=1))
        ps_h = ctx.enter_context(tc.psum_pool(name="ps_h", bufs=2))
        ps_x = ctx.enter_context(tc.psum_pool(name="ps_x", bufs=1))
        ctx.enter_context(tc.manual_schedule())

        ones = keep.tile([P, FEATS], BF16, name="ones")
        nc.vector.memset(ones[:], 1.0)
        bias_rows = keep.tile([P, 3 * FEATS], BF16, name="bias_rows")
        nc.vector.memset(bias_rows[:].bitcast(F32), 0.0)
        wscale_sb = keep.tile([P, 3 * FEATS], U8, align_bytes=64, name="wscale_sb")
        nc.vector.memset(wscale_sb[:].bitcast(I32), 0)
        ident = keep.tile([P, P], F32, name="ident")
        make_identity(nc, ident[:])
        ident_bf = keep.tile([P, P], BF16, name="ident_bf")
        nc.vector.tensor_copy(out=ident_bf[:], in_=ident[:])

        scale_col = keep.tile([P, 4], F32, name="scale_col")
        codes_in = keep.tile([P, SETS, 4, POINTS], U8, align_bytes=64, name="codes_in")
        vraw = [keep.tile([P, 4, FEATS], BF16, name="vraw%d" % b) for b in range(SETS)]
        w_sb = keep.tile([P, 3, 4 * FEATS], U8, align_bytes=64, name="w_sb")

        def load_codes(b0, b1):
            nc.sync.dma_start(out=codes_in[:, b0:b1], in_=attn1_bytes[b0:b1].rearrange("b (p r) s -> p b r s", r=4))

        def load_v(b):
            nc.sync.dma_start(out=vraw[b][:], in_=v1[b].rearrange("(p j) f -> p j f", j=4))

        def load_words(w):
            nc.sync.dma_start(out=w_sb[:, w, :], in_=words_in[w][0].rearrange("p n t -> p (n t)"))

        def load_wscales(w):
            for quad in range(4):
                nc.sync.dma_start(
                    out=wscale_sb[32 * quad : 32 * quad + 4, FEATS * w : FEATS * (w + 1)].bitcast(I32),
                    in_=wscales_in[w][0, 4 * quad : 4 * quad + 4, :].bitcast(I32),
                )

        def load_bias(w):
            nc.sync.dma_start(out=bias_rows[0:1, FEATS * w : FEATS * (w + 1)], in_=biases_in[w].rearrange("(o n) -> o n", o=1))

        def load_scale():
            nc.sync.dma_start(out=scale_col[:], in_=attn1_scale.rearrange("a b (p t) -> p (a b t)", t=4))

        load_v(0)
        load_codes(0, 1)
        load_scale()
        load_v(1)
        load_bias(0)
        load_bias(1)
        load_codes(1, 2)
        load_bias(2)
        load_wscales(0)
        load_words(0)
        load_words(1)
        load_wscales(1)
        load_v(2)
        load_codes(2, 3)
        load_words(2)
        load_wscales(2)
        load_codes(3, 6)
        load_v(3)
        load_v(4)
        load_v(5)

        scale_sb = keep.tile([P, POINTS], F32, name="scale_sb")
        bias_sb = keep.tile([P, 4, FEATS], BF16, name="bias_sb")
        spread = {}

        def spread_scales(tag):
            spread["scale"] = ps_out.tile([P, 4, P], F32, tag=tag, name="scale_ps")
            for t in range(4):
                nc.tensor.transpose(spread["scale"][:, t, :], scale_col[:, t : t + 1].to_broadcast([P, P]), ident[:])

        def keep_scales():
            nc.scalar.activation(out=scale_sb[:].rearrange("q (p t) -> q p t", t=4), in_=spread["scale"][:].rearrange("q t p -> q p t"), func=COPY)

        def spread_biases(w0, w1, tag):
            rows = ps_out.tile([P, 2, FEATS], BF16, tag=tag, name="bias_ps")
            for w in range(w0, w1):
                spread[w] = rows[:, w - w0 :, :]
                nc.tensor.matmul(rows[:, w - w0, :], lhsT=ones[:, :P], rhs=bias_rows[:, FEATS * w : FEATS * (w + 1)], start=True, stop=True)

            if w1 == 3:
                nc.tensor.matmul(rows[:, 1, :2], lhsT=bias_rows[:, 3 * FEATS - P :], rhs=ones[:, :2], start=True, stop=True)

        def keep_biases(w0, w1, engine):
            width = FEATS * (w1 - w0) + (2 if w1 == 3 else 0)
            engine(out=bias_sb[:, w0:].rearrange("p w n -> p (w n)")[:, :width], in_=spread[w0].rearrange("p w n -> p (w n)")[:, :width])

        def warm_up(pool, tag, count, moving):
            idle = pool.tile([P, FEATS], F32, tag=tag, name="idle")
            for n in range(count):
                nc.tensor.matmul(idle[:], lhsT=ones[:, :P], rhs=moving, start=True, stop=True)

        ring = [keep.tile([P, 5, POINTS], BF16, align_bytes=64, name="ring%d" % n) for n in range(2)]

        def hg(i):
            return ring[i % 2][:, 1:3].rearrange("p r (q t) -> p r q t", t=4)

        def xg(i):
            return ring[(i - 1) % 2][:, 3:5]

        cast, xt, xq, xs = {}, {}, {}, {}
        vg, vq, vs, vb = {}, {}, {}, {}
        hps, hq, hs = {}, {}, {}
        bank, res, done = {}, {}, {}
        source = {}

        def do_cast(i, r0=0, r1=2):
            if i not in cast:
                cast[i] = work.tile([P, 2, POINTS], BF16, tag="cast", name="cast_t")
            h = 2 * (i % 2)
            nc.scalar.copy(out=cast[i][:, r0:r1, :], in_=codes_in[:, i // 2, h + r0 : h + r1, :].bitcast(FP8))
            for r in range(r0, r1):
                source[(i, r)] = cast[i][:, r, :]

        def do_scale_out(i, r):
            nc.vector.tensor_tensor(
                out=xg(i)[:, r, :].rearrange("p (q u e) -> p q u e", u=2, e=2),
                in0=xt[(i, r)][:, r].bitcast(BF16).rearrange("p u (q e) -> p q u e", e=2),
                in1=scale_col[:].rearrange("p (u e) -> p u e", e=2).unsqueeze(1).to_broadcast([P, P, 2, 2]),
                op=MULT,
            )

        def do_prod(i, r0=0, r1=2, into=None):
            into = xg(i)[:, r0:r1] if into is None else into
            for r in range(r0, r1):
                source[(i, r)] = into[:, r - r0, :]
            nc.gpsimd.tensor_tensor(out=into, in0=cast[i][:, r0:r1], in1=scale_sb[:].unsqueeze(1).to_broadcast([P, r1 - r0, POINTS]), op=MULT)

        def do_turn(i, tiles=(0, 1), pool=ps_x, tag="x"):
            turned = pool.tile([P, 2, 2, P], F32, tag=tag, name="xt_t")
            for r in tiles:
                xt[(i, r)] = turned
                pairs_of_k = source[(i, r)].bitcast(F32)
                for u in range(2):
                    nc.tensor.transpose(turned[:, r, u, :], pairs_of_k[:, u : 256 : 2], ident[:])

        def do_group(i, r1=2, r0=0):
            nc.scalar.copy(
                out=xg(i)[:, r0:r1].bitcast(F32).rearrange("p r (q u) -> p r q u", u=2),
                in_=xt[(i, r0)][:, r0:r1].rearrange("p r u q -> p r q u"),
            )

        codes, planes = {}, {}

        def new_codes(c):
            if c not in codes:
                codes[c] = work.tile([P, 2, 4 * 2 * P], U8, tag="codes", name="codes_t", align_bytes=64)
                planes[c] = work.tile([P, 2, 2 * P], U8, tag="planes", name="planes_t", align_bytes=64)
                hq[c], hs[c] = codes[c][:, 0], planes[c][:, 0]
                xq[c + 1], xs[c + 1] = codes[c][:, 1], planes[c][:, 1]

        def do_quant_hx(c, r0=0):
            new_codes(c)
            nc.vector.quantize_mx(
                out=codes[c][:].rearrange("p a w -> p (a w)")[:, 512 * r0 :].bitcast(FP8X4), scales=planes[c][:].rearrange("p a w -> p (a w)")[:, P * r0 :],
                in_=ring[c % 2][:, 1 + r0 :].rearrange("p r s -> p (r s)"),
            )

        def do_quant_x(i, r0=0, r1=2):
            new_codes(i - 1)
            nc.vector.quantize_mx(
                out=xq[i][:, 512 * r0 : 512 * r1].bitcast(FP8X4), scales=xs[i][:, P * r0 : P * r1],
                in_=xg(i)[:, r0:r1, :].rearrange("p r s -> p (r s)"),
            )

        def do_quant_h(i, r0=0, r1=2):
            new_codes(i)
            nc.vector.quantize_mx(
                out=hq[i][:, 512 * r0 : 512 * r1].bitcast(FP8X4), scales=hs[i][:, P * r0 : P * r1],
                in_=hg(i)[:, r0:r1].rearrange("p r q t -> p (r q t)"),
            )

        def grouped(b):
            if b not in vg:
                vg[b] = work.tile([P, 4, P, 4], BF16, tag="vg", name="vg_t", align_bytes=64, bufs=2)
            return vg[b]

        def do_group_v(b, n0, n1, engine=None):
            src = vraw[b][:].rearrange("p j (n m t) -> p n j m t", m=2, t=4)[:, n0:n1]
            dst = grouped(b)[:].rearrange("p t (n m) j -> p n j m t", m=2)[:, n0:n1]
            (engine or nc.scalar.copy)(out=dst, in_=src)

        def do_group_v_pool(b, n0, n1):
            src = vraw[b][:].rearrange("p j (m t) -> p t m j", t=4)[:, :, 2 * n0 : 2 * n1]
            nc.gpsimd.tensor_scalar(out=grouped(b)[:, :, 2 * n0 : 2 * n1], in0=src, scalar1=1.0, scalar2=0.0, op0=MULT, op1=ADD)

        def do_weave_v(b, s0, s1, pool=ps_h, tag="h"):
            vb[(b, s0)] = pool.tile([P, 2, STRIP, 4], BF16, tag=tag, name="vb_t")
            for s in range(s0, s1):
                nc.tensor.matmul(
                    vb[(b, s0)][:, s - s0].rearrange("p f j -> p j f"), lhsT=ident_bf[:],
                    rhs=vraw[b][:, :, STRIP * s : STRIP * (s + 1)], start=True, stop=True,
                )

        def do_keep_v(b, s0, s1):
            m0, m1 = STRIP // 4 * s0, STRIP // 4 * s1
            nc.scalar.copy(
                out=grouped(b)[:, :, m0:m1, :].bitcast(F32),
                in_=vb[(b, s0)][:, : s1 - s0].bitcast(F32).rearrange("p s (m t) u -> p t (s m) u", t=4),
            )

        def do_quant_v(b):
            vq[b] = work.tile([P, 4 * FEATS], U8, tag="vq", name="vq_t", align_bytes=64, bufs=2)
            vs[b] = work.tile([P, FEATS], U8, tag="vs", name="vs_t", align_bytes=64, bufs=2)
            nc.vector.quantize_mx(out=vq[b][:].bitcast(FP8X4), scales=vs[b][:], in_=vg[b][:].rearrange("p t m j -> p (t m j)"))

        def do_mix(i, r):
            b = i // 2
            h = ps_h.tile([P, 4, P], F32, tag="h", name="h_t")
            hps[(i, r)] = h
            for t in range(4):
                nc.tensor.matmul_mx(
                    out=h[:, t, :],
                    lhsT=vq[b][:, 512 * t : 512 * (t + 1)].bitcast(FP8X4),
                    lhsT_scale=vs[b][:, P * t : P * (t + 1)],
                    rhs=xq[i][:, 512 * r : 512 * (r + 1)].bitcast(FP8X4),
                    rhs_scale=xs[i][:, P * r : P * (r + 1)],
                    start=True, stop=True,
                )

        def do_relu(i, r):
            nc.scalar.activation(out=hg(i)[:, r], in_=hps[(i, r)][:].rearrange("p t q -> p q t"), func=RELU)

        free_banks = [1, 0, 2, 3, 4]
        place = {}

        def do_project(i, k):
            w, r = k // 2, k % 2
            place[(i, k)] = free_banks[0]
            free_banks.remove(place[(i, k)])
            o = ps_out.tile([P, FEATS], F32, tag="o%d" % place[(i, k)], name="o_t")
            bank[(i, k)] = o
            h_codes, h_scales = hq[i][:, 512 * r : 512 * (r + 1)].bitcast(FP8X4), hs[i][:, P * r : P * (r + 1)]
            for c0, c1 in [(0, 2 * P), (2 * P, 3 * P)] if (i, k) in SLICED else [(0, FEATS)]:
                nc.tensor.matmul_mx(
                    out=o[:, c0:c1], lhsT=h_codes, lhsT_scale=h_scales,
                    rhs=w_sb[:, w, 4 * c0 : 4 * c1].bitcast(FP8X4), rhs_scale=wscale_sb[:, FEATS * w + c0 : FEATS * w + c1],
                    start=True, stop=True,
                )
            if (i, k) in SLICED:
                nc.tensor.matmul_mx(
                    out=o[:, 3 * P :], lhsT=w_sb[:, w, 12 * P :].bitcast(FP8X4), lhsT_scale=wscale_sb[:, FEATS * w + 3 * P : FEATS * (w + 1)],
                    rhs=h_codes, rhs_scale=h_scales, start=True, stop=True,
                )

        sliced = {}

        def do_slice_bias(i, k):
            sliced[(i, k)] = work.tile([P, P], F32, tag="sliced", name="sliced_t", bufs=2)
            nc.scalar.activation(out=sliced[(i, k)][:], in_=bank[(i, k)][:, 3 * P :], func=IDENTITY, bias=bias_sb[:, 3, 0:1])

        def do_slice_back(i, k):
            nc.tensor.transpose(bank[(i, k)][:, 3 * P :], sliced[(i, k)][:], ident[:])

        def do_slice_out(i, k):
            nc.scalar.copy(out=result(i, k)[:, 3 * P :], in_=bank[(i, k)][:, 3 * P :])

        def result(i, k):
            w = k // 2
            if (i, w) not in res:
                res[(i, w)] = stores.tile([P, 2, FEATS], F32, tag="y%d" % w, name="y_t")
            return res[(i, w)][:, k % 2, :]

        def store(i, k):
            w, h = k // 2, 2 * (i % 2)
            done[(i, w)] = done.get((i, w), 0) + 1
            rows = outs[w][i // 2].rearrange("(p r) n -> p r n", r=4)
            if done[(i, w)] == 2:
                queue = nc.scalar if (i, w) in SECOND_QUEUE else nc.sync
                queue.dma_start(out=rows[:, h : h + 2, :], in_=res[(i, w)][:])

        def do_empty(i, k, width=FEATS):
            cols = slice(0, width)
            nc.vector.tensor_tensor(out=result(i, k)[:, cols], in0=bank[(i, k)][:, cols], in1=bias_sb[:, k // 2, cols], op=ADD)
            free_banks.append(place[(i, k)])
            store(i, k)

        def do_copy_out(i, k, width=FEATS):
            cols = slice(FEATS - width, FEATS)
            nc.scalar.copy(out=result(i, k)[:, cols], in_=bank[(i, k)][:, cols])
            if width == FEATS:
                free_banks.append(place[(i, k)])

        def do_add_bias(i, k, width=FEATS):
            cols = slice(FEATS - width, FEATS)
            y = result(i, k)[:, cols]
            nc.gpsimd.tensor_tensor(out=y, in0=y, in1=bias_sb[:, k // 2, cols], op=ADD)
            if width == FEATS:
                store(i, k)

        warm_up(ps_h, "h", 3, ones[:])
        do_group_v(0, 16, 64, nc.vector.tensor_copy)
        do_group_v(0, 0, 16)
        warm_up(ps_h, "h", 3, vraw[0][:, 0, :])
        do_cast(0, 0, 1)
        do_turn(0, (0,))
        spread_scales("o0")
        do_cast(0, 1, 2)
        do_turn(0, (1,), ps_out, "o4")
        spread_biases(0, 2, "o2")
        do_cast(1)
        do_turn(1, (0, 1), ps_out, "o1")
        do_quant_v(0)
        do_group_v_pool(1, 44, 64)
        do_scale_out(0, 0)
        do_scale_out(0, 1)
        keep_scales()
        do_cast(2, 0, 1)
        do_quant_x(0, 0, 1)
        do_quant_x(0, 1, 2)
        do_prod(2, 0, 1)
        keep_biases(0, 1, nc.vector.tensor_copy)
        do_mix(0, 0)
        do_mix(0, 1)
        spread_biases(2, 3, "o3")
        do_scale_out(1, 0)
        do_scale_out(1, 1)
        do_cast(2, 1, 2)
        do_turn(2, (1,), ps_out, "o4")
        do_cast(3, 0, 1)
        do_relu(0, 0)
        do_weave_v(1, 0, 1)
        do_relu(0, 1)
        do_cast(3, 1, 2)
        do_quant_h(0, 0, 1)
        do_quant_x(1)
        do_quant_h(0, 1, 2)
        do_prod(3)
        keep_biases(1, 2, nc.vector.tensor_copy)
        do_keep_v(1, 0, 1)
        keep_biases(2, 3, nc.scalar.copy)
        do_group_v(1, 16, 32)
        do_project(0, 0)
        do_project(0, 1)
        do_project(0, 2)
        do_mix(1, 0)
        do_mix(1, 1)
        do_project(0, 3)
        do_turn(2, (0,))
        do_copy_out(0, 2, FIRST_SHARE)
        do_add_bias(0, 2, FIRST_SHARE)
        do_relu(1, 0)
        do_relu(1, 1)
        do_group(2, 1)
        do_group_v(1, 32, 44)
        do_cast(4)
        do_empty(0, 0)
        do_empty(0, 1)
        do_scale_out(2, 1)
        do_empty(0, 3)
        do_empty(0, 2, FEATS - FIRST_SHARE)
        do_weave_v(2, 0, 1)
        do_project(0, 4)
        do_project(0, 5)
        do_turn(3)

        for c in range(1, PAIRS + 1):
            if c == BUSY:
                do_quant_h(c, 0, 1)
                do_quant_hx(c, 1)
                do_quant_v((c + 1) // 2)
            elif c % 2 == 1 and c + 1 < PAIRS:
                do_quant_hx(c)
                do_quant_v((c + 1) // 2)
            elif c + 1 < PAIRS:
                do_quant_h(c, 0, 1)
                do_quant_hx(c, 1)
            elif c < PAIRS:
                do_quant_h(c, 0, 1)
                do_quant_h(c, 1, 2)
            if c < BUSY - 1:
                do_prod(c + LEAD, 0, 2, None if c % 2 else ring[0][:, 0:2])
            elif c == BUSY - 1:
                do_prod(LAST, 0, 1, ring[0][:, 1:2])
            elif c == BUSY:
                do_prod(LAST, 1, 2, ring[1][:, 3:4])
            for k in (4, 5):
                if (c - 1, k) in SLICED:
                    do_slice_out(c - 1, k)
            b, half = (c + 3) // 2, (c + 1) % 2
            if b < SETS:
                do_group_v(b, 32 * half + 16, 32 * (half + 1))
                do_keep_v(b, 2 * half, 2 * half + 1)
            if c + 2 < LAST - 1:
                do_group(c + 2)
            elif c + 2 == LAST:
                do_group(LAST, 1)
            share = (SECOND_SHARE if c == 1 else SHARE_SLICED if (c - 1, 5) in SLICED else SHARE) if c < BUSY - 1 else (SHARE8 if c == BUSY - 1 else FEATS)
            if c < PAIRS:
                do_project(c, 2)
                do_copy_out(c, 2, share)
                do_add_bias(c, 2, share)
                if c + 2 == LAST - 1:
                    do_group(c + 2)
                do_project(c, 0)
                do_project(c, 1)
            if c + 1 < PAIRS:
                do_mix(c + 1, 0)
                do_mix(c + 1, 1)
            if (c - 1, 5) in SLICED:
                do_empty(c - 1, 4, FEATS - P if (c - 1, 4) in SLICED else FEATS)
                do_empty(c - 1, 5, FEATS - P)
            else:
                do_empty(c - 1, 5)
                do_empty(c - 1, 4)
            if c == PAIRS:
                break
            do_project(c, 3)
            if c + 1 < PAIRS:
                do_relu(c + 1, 0)
                do_relu(c + 1, 1)
            if c == BUSY:
                do_turn(LAST, (1,))
                do_group(LAST, 2, 1)
            for k in ((1, 0) if c % 2 and c < BUSY else (0, 1)):
                do_empty(c, k)
            do_project(c, 4)
            do_project(c, 5)
            for k in (4, 5):
                if (c, k) in SLICED:
                    do_slice_bias(c, k)
            if c + LEAD + 1 < PAIRS:
                do_cast(c + LEAD + 1)
            do_empty(c, 3)
            if share < FEATS:
                do_empty(c, 2, FEATS - share)
            b, half = (c + 4) // 2, c % 2
            if b < SETS:
                do_weave_v(b, 2 * half, 2 * half + 1)
            for k in (4, 5):
                if (c, k) in SLICED:
                    do_slice_back(c, k)
            if c < BUSY - 1:
                do_turn(c + LEAD)
            elif c == BUSY - 1:
                do_turn(LAST, (0,))
